import numpy as np
import ml_dtypes


def mxq(x, axis, fmt="e4m3"):
    dtype, down = {"e4m3": (ml_dtypes.float8_e4m3fn, 7), "e5m2": (ml_dtypes.float8_e5m2, 14)}[fmt]
    v = np.moveaxis(np.asarray(x, np.float32).astype(ml_dtypes.bfloat16).astype(np.float64), axis, -1)
    blocks = v.reshape(v.shape[:-1] + (-1, 32))
    amax = np.abs(blocks).max(-1, keepdims=True)
    byte = np.maximum(np.where(amax > 0, np.frexp(amax)[1] - 1 + 127, 0) - down, 1)
    scale = np.exp2(byte - 127.0)
    codes = (blocks / scale).astype(np.float32).astype(dtype).astype(np.float64)
    return np.moveaxis((codes * scale).reshape(v.shape), -1, axis)


WIDE = False


def mx_kscale(k):
    if not WIDE:
        return np.ones(k)
    levels = np.array([10, -10, 5, -5, 0])
    a = np.random.permutation(np.resize(levels, k // 512 * 4)).reshape(k // 512, 4)
    idx = np.arange(k)
    return np.exp2(a[idx // 512, idx % 128 // 32])


BF16 = ml_dtypes.bfloat16


def bf(x):
    return np.asarray(x, np.float32).astype(BF16)


def f64(x):
    return np.asarray(x).astype(np.float64)


B, C, H, W = 128, 1024, 3, 3
C3, CH, P = 3 * C, C // 2, H * W


def sigmoid(v):
    return 1.0 / (1.0 + np.exp(-v))


def setup_inputs():
    s, t = mx_kscale(C3), mx_kscale(CH)
    n = np.random.standard_normal
    return {
        "fv": bf(n((B, C3, H, W)) * s[None, :, None, None]),
        "ft": bf(n((B, C))),
        "Wa": bf(n((CH, C3)) / np.sqrt(C3) / s[None, :] * t[:, None]),
        "ba": bf(n(CH) * 0.3 * t),
        "Wb": bf(n((C, CH)) * 2.0 / np.sqrt(CH) / t[None, :]),
        "bb": bf(n(C) * 0.5),
        "Wfc2": bf(n((C, C)) / np.sqrt(C)),
        "bfc2": bf(n(C) * 0.3),
    }


def reference(fv, ft, Wa, ba, Wb, bb, Wfc2, bfc2):
    h = np.maximum((mxq(f64(Wa), 1, "e4m3") @ mxq(f64(fv).reshape(B, C3, P), 1, "e4m3")) + f64(ba)[None, :, None], 0.0)
    fv2 = (mxq(f64(Wb), 1, "e4m3") @ mxq(h, 1, "e4m3")) + f64(bb)[None, :, None]
    gate = sigmoid(fv2.mean(axis=2))
    ft2 = f64(ft) @ f64(Wfc2).T + f64(bfc2)
    return ft2 + ft2 * gate

@@ -1,0 +1,359 @@
+from contextlib import ExitStack
+
+import concourse.mybir as mybir
+from concourse.masks import make_identity
+
+F32 = mybir.dt.float32
+BF16 = mybir.dt.bfloat16
+U32 = mybir.dt.uint32
+U8 = mybir.dt.uint8
+FP8X4 = mybir.dt.float8_e4m3fn_x4
+ACT = mybir.ActivationFunctionType
+ALU = mybir.AluOpType
+
+P = 128
+B, C, PIX = 128, 1024, 9
+C3, CH = 3 * C, C // 2
+NG = C3 // 512
+COLS = PIX * B
+FLOPS = 2 * (CH * C3 * COLS + C * CH * COLS + B * C * C)
+
+MANUAL = True
+
+
+def tile_joint_module_pb_kernel(tc, fv, ft, Wa, ba, Wb, bb, Wfc2, bfc2, out):
+    nc = tc.nc
+    with ExitStack() as ctx:
+        const = ctx.enter_context(tc.tile_pool(name="const", bufs=1))
+        keep = ctx.enter_context(tc.tile_pool(name="keep", bufs=1))
+        fvraw_pool = ctx.enter_context(tc.tile_pool(name="fvraw", bufs=4))
+        wraw_pool = ctx.enter_context(tc.tile_pool(name="wraw", bufs=6))
+        tw_pool = ctx.enter_context(tc.tile_pool(name="tw", bufs=2))
+        grp_pool = ctx.enter_context(tc.tile_pool(name="grp", bufs=2))
+        wag_pool = ctx.enter_context(tc.tile_pool(name="wag", bufs=2))
+        psum = ctx.enter_context(tc.psum_pool(name="ps", bufs=1))
+        if MANUAL:
+            ctx.enter_context(tc.manual_schedule())
+
+        ident = const.tile([P, P], F32, name="ident")
+        make_identity(nc, ident[:])
+        ba_raw = const.tile([P, 4], BF16, name="ba_raw")
+        ba_f = const.tile([P, 4], F32, name="ba_f")
+        nc.scalar.dma_start(
+            out=ba_raw[:].rearrange("p (s e) -> p s e", s=2),
+            in_=ba.rearrange("(s p e) -> p s e", s=2, e=2),
+        )
+        warm_in = const.tile([P, 1], F32, name="warm_in")
+        warm_out = const.tile([P, 1], F32, name="warm_out")
+        nc.vector.memset(warm_in[:], 0.0)
+        nc.scalar.activation(out=warm_out[:], in_=warm_in[:], func=ACT.Sigmoid)
+        nc.vector.tensor_copy(out=ba_f[:], in_=ba_raw[:])
+
+        fvc = keep.tile([P, NG, COLS], U32, name="fvc", align_bytes=64)
+        fvs = keep.tile([P, NG, COLS], U8, name="fvs", align_bytes=64)
+        wac = keep.tile([P, 2, NG, 256], U32, name="wac", align_bytes=64)
+        was = keep.tile([P, 2, NG, 256], U8, name="was", align_bytes=64)
+        wbg = keep.tile([P, C, 2], F32, name="wbg", align_bytes=64)
+        wbc = keep.tile([P, C], U32, name="wbc", align_bytes=64)
+        wbs = keep.tile([P, C], U8, name="wbs", align_bytes=64)
+        wfT = keep.tile([P, 4, C], F32, name="wfT")
+        ftT = keep.tile([P, 4, P], F32, name="ftT")
+        ft2 = keep.tile([P, C], F32, name="ft2")
+        hp = keep.tile([P, 4, COLS], BF16, name="hp")
+        hg = keep.tile([P, COLS, 4], BF16, name="hg", align_bytes=64)
+        hc = keep.tile([P, COLS], U32, name="hc", align_bytes=64)
+        hs = keep.tile([P, COLS], U8, name="hs", align_bytes=64)
+        z = keep.tile([P, C], F32, name="z")
+        ft_raw = const.tile([P, C], BF16, name="ft_raw")
+        bfc_bc = const.tile([P, C], BF16, name="bfc_bc")
+        bb_bc = const.tile([P, C], BF16, name="bb_bc")
+
+        fv_flat = fv.rearrange("b c h w -> b (c h w)")
+        wa_view = Wa.rearrange("(s p e) c -> s p e c", s=2, e=2)
+        wf_view = Wfc2.rearrange("(t p) c -> p t c", p=P)
+        wb_view = Wb.rearrange("(t p) m -> p t m", p=P)
+        fv_raw = []
+        wa_raw = []
+        for g in range(NG):
+            r = fvraw_pool.tile([P, 4608], BF16, name="fvr", tag="fvr")
+            nc.sync.dma_start(out=r[:], in_=fv_flat[:, g * 4608:(g + 1) * 4608])
+            fv_raw.append(r)
+            sm, gp = g % 2, g // 2
+            r = wraw_pool.tile([P, 2, 1024], BF16, name="war", tag="wr")
+            nc.sync.dma_start(out=r[:], in_=wa_view[sm][:, :, gp * 1024:(gp + 1) * 1024])
+            wa_raw.append(r)
+        nc.sync.dma_start(out=ft_raw[:], in_=ft)
+        wf_raw = []
+        for i in range(4):
+            r = wraw_pool.tile([P, 2, 1024], BF16, name="wfr", tag="wr")
+            nc.sync.dma_start(out=r[:], in_=wf_view[:, 2 * i:2 * i + 2, :])
+            wf_raw.append(r)
+        wb_raw = []
+        for i in range(2):
+            r = wraw_pool.tile([P, 4, 512], BF16, name="wbr", tag="wr")
+            nc.sync.dma_start(out=r[:], in_=wb_view[:, 4 * i:4 * i + 4, :])
+            wb_raw.append(r)
+        nc.sync.dma_start(out=bfc_bc[:], in_=bfc2.partition_broadcast(P))
+        nc.sync.dma_start(out=bb_bc[:], in_=bb.partition_broadcast(P))
+
+        used = []
+
+        def tbank(nrot):
+            tag = "tr%d" % (len(used) % nrot)
+            used.append(tag)
+            return psum.tile([P, 512], F32, name=tag, tag=tag)
+
+        def conv1_pass(acc, g, j, c0, n, start, stop):
+            sm, em = divmod(j, 2)
+            nc.tensor.matmul_mx(
+                out=acc,
+                lhsT=wac[:, sm, g, em * P:(em + 1) * P].bitcast(FP8X4),
+                lhsT_scale=was[:, sm, g, em * P:(em + 1) * P],
+                rhs=fvc[:, g, c0:c0 + n].bitcast(FP8X4),
+                rhs_scale=fvs[:, g, c0:c0 + n],
+                start=start,
+                stop=stop,
+            )
+
+        tws = {}
+        grps = {}
+
+        def tf_bank(g, w0, nw):
+            pb = tbank(4)
+            fw = fv_raw[g][:].bitcast(F32)
+            for s in range(2):
+                for wl in range(nw):
+                    st = s * 1152 + w0 + wl
+                    slot = s * nw + wl
+                    nc.tensor.transpose(pb[:, slot * P:(slot + 1) * P], fw[:, st:st + 1144:9], ident[:])
+            nc.scalar.copy(
+                out=tws[g][:, :, w0 * P:(w0 + nw) * P],
+                in_=pb[:, 0:2 * nw * P].rearrange("p (s r) -> p s r", s=2),
+            )
+
+        def regroup_quantise(g):
+            tb = tws[g][:].bitcast(BF16)
+            ev = tb[:, :, 0:2050].rearrange("p s (e r) -> p s e r", e=2)
+            od = tb[:, :, 1:2559].rearrange("p s (e r) -> p s e r", e=2)
+            l8 = tb[:, :, 254:2304].rearrange("p s (e r) -> p s e r", e=2)
+            gt = grps[g]
+            gf = gt[:].rearrange("p x b t -> p (x b t)")
+
+            def cp(src, a0, a1, x0):
+                nc.vector.tensor_copy(
+                    out=gt[:, x0 + 2 * a0:x0 + 2 * a1:2].rearrange("p a b (s e) -> p a b s e", s=2),
+                    in_=src[:, :, :, a0 * 256:a1 * 256:2].rearrange("p s e (a b) -> p a b s e", a=a1 - a0),
+                )
+
+            def qz(c0, n):
+                nc.vector.quantize_mx(
+                    out=fvc[:, g, c0:c0 + n].bitcast(FP8X4),
+                    scales=fvs[:, g, c0:c0 + n],
+                    in_=gf[:, 4 * c0:4 * (c0 + n)],
+                )
+
+            cp(ev, 0, 2, 0)
+            cp(od, 0, 2, 1)
+            cp(ev, 2, 4, 0)
+            qz(0, 512)
+            cp(od, 2, 4, 1)
+            nc.vector.tensor_copy(
+                out=gt[:, 8].rearrange("p b (s e) -> p b s e", s=2),
+                in_=l8[:, :, :, 770:1025:2].rearrange("p s e b -> p b s e"),
+            )
+            qz(512, 512)
+            qz(1024, 128)
+
+        def wa_unit(i):
+            sm, gp = i % 2, i // 2
+            ww = wa_raw[i][:].bitcast(F32)
+            wag = wag_pool.tile([P, 2, 2, P, 2], F32, name="wag", align_bytes=64)
+            for g2 in range(2):
+                pb = tbank(4)
+                for em in range(2):
+                    for s in range(2):
+                        slot = em * 2 + s
+                        c0 = 256 * g2 + P * s
+                        nc.tensor.transpose(pb[:, slot * P:(slot + 1) * P], ww[:, em, c0:c0 + P], ident[:])
+                nc.scalar.copy(out=wag[:, g2], in_=pb[:].rearrange("p (e s q) -> p e q s", e=2, s=2))
+            return wag
+
+        def wa_quantise(i, wag):
+            sm, gp = i % 2, i // 2
+            nc.vector.quantize_mx(
+                out=wac[:, sm, 2 * gp:2 * gp + 2, :].rearrange("p g w -> p (g w)").bitcast(FP8X4),
+                scales=was[:, sm, 2 * gp:2 * gp + 2, :].rearrange("p g w -> p (g w)"),
+                in_=wag[:].rearrange("p g e q s -> p (g e q s)").bitcast(BF16),
+            )
+
+        acc0 = []
+        m0 = [(g, j) for g in range(NG) for j in range(4)]
+
+        def m0_pair(k):
+            for g, j in m0[2 * k:2 * k + 2]:
+                if g == 0:
+                    acc0.append(psum.tile([P, 512], F32, name="acc%d" % j, tag="acc%d" % j))
+                conv1_pass(acc0[j][:], g, j, 0, 512, g == 0, g == NG - 1)
+
+        for g in range(NG):
+            tws[g] = tw_pool.tile([P, 2, 1280], F32, name="tw")
+            grps[g] = grp_pool.tile([P, PIX, P, 4], BF16, name="grp", align_bytes=64)
+            tf_bank(g, 0, 2)
+            tf_bank(g, 4, 2)
+            tf_bank(g, 6, 2)
+            if g >= 2:
+                m0_pair(2 * (g - 2))
+            tf_bank(g, 2, 2)
+            tf_bank(g, 8, 1)
+            wag = wa_unit(g)
+            if g >= 2:
+                m0_pair(2 * (g - 2) + 1)
+            regroup_quantise(g)
+            wa_quantise(g, wag)
+
+        m0_pair(8)
+        m0_pair(9)
+        pb = tbank(3)
+        fw = ft_raw[:].bitcast(F32)
+        for k in range(4):
+            nc.tensor.transpose(pb[:, k * P:(k + 1) * P], fw[:, k * P:(k + 1) * P], ident[:])
+        nc.scalar.copy(out=ftT[:].rearrange("p k b -> p (k b)"), in_=pb[:])
+        ft_e = ftT[:].bitcast(BF16).rearrange("p k (b e) -> p k b e", e=2)
+        wf_e = wfT[:].bitcast(BF16).rearrange("p k (o e) -> p k o e", e=2)
+
+        def wf_unit(i):
+            ww = wf_raw[i][:].bitcast(F32)
+            for h in range(2):
+                pb = tbank(3)
+                for kl in range(2):
+                    for tl in range(2):
+                        slot = kl * 2 + tl
+                        k = 2 * h + kl
+                        nc.tensor.transpose(pb[:, slot * P:(slot + 1) * P], ww[:, tl, k * P:(k + 1) * P], ident[:])
+                nc.scalar.copy(
+                    out=wfT[:, 2 * h:2 * h + 2, i * 256:(i + 1) * 256],
+                    in_=pb[:].rearrange("p (k o) -> p k o", k=2),
+                )
+
+        def fc(half):
+            acc = psum.tile([P, 512], F32, name="fc", tag="tr3")
+            cols = slice(half * 512, (half + 1) * 512)
+            for idx in range(8):
+                k, e = divmod(idx, 2)
+                nc.tensor.matmul(
+                    out=acc[:], lhsT=ft_e[:, k, :, e], rhs=wf_e[:, k, cols, e], start=idx == 0, stop=idx == 7
+                )
+            nc.vector.tensor_tensor(out=ft2[:, cols], in0=acc[:], in1=bfc_bc[:, cols], op=ALU.add)
+
+        def wb_unit(i):
+            ww = wb_raw[i][:].bitcast(F32)
+            for h in range(2):
+                pb = tbank(3)
+                for tl in range(2):
+                    for sm in range(2):
+                        slot = tl * 2 + sm
+                        nc.tensor.transpose(
+                            pb[:, slot * P:(slot + 1) * P], ww[:, 2 * h + tl, sm * P:(sm + 1) * P], ident[:]
+                        )
+                o0 = (4 * i + 2 * h) * P
+                nc.scalar.copy(
+                    out=wbg[:, o0:o0 + 256, :].rearrange("p (t o) s -> p t o s", t=2),
+                    in_=pb[:].rearrange("p (t s o) -> p t o s", t=2, s=2),
+                )
+            nc.vector.quantize_mx(
+                out=wbc[:, i * 512:(i + 1) * 512].bitcast(FP8X4),
+                scales=wbs[:, i * 512:(i + 1) * 512],
+                in_=wbg[:, i * 512:(i + 1) * 512, :].rearrange("p o s -> p (o s)").bitcast(BF16),
+            )
+
+        wf_unit(0)
+        wf_unit(1)
+        wf_unit(2)
+        fc(0)
+        wf_unit(3)
+        wb_unit(0)
+        fc(1)
+        wb_unit(1)
+
+        acc1 = [psum.tile([P, 512], F32, name="c1_%d" % j, tag="tr%d" % j) for j in range(4)]
+        for g in range(NG - 1):
+            for j in range(4):
+                conv1_pass(acc1[j][:], g, j, 512, 512, g == 0, False)
+        m0_pair(10)
+        m0_pair(11)
+
+        def h_out(eng, bank, j, c0, n):
+            if eng == "s":
+                nc.scalar.activation(
+                    out=hp[:, j, c0:c0 + n], in_=bank, func=ACT.Relu, bias=ba_f[:, j:j + 1], scale=1.0
+                )
+            else:
+                nc.vector.tensor_scalar(
+                    out=hp[:, j, c0:c0 + n], in0=bank, scalar1=ba_f[:, j:j + 1], scalar2=0.0,
+                    op0=ALU.add, op1=ALU.max,
+                )
+
+        def h_regroup(c0, n):
+            nc.vector.tensor_copy(
+                out=hg[:, c0:c0 + n, :].rearrange("p (c i) t -> p c t i", i=4),
+                in_=hp[:, :, c0:c0 + n].rearrange("p t (c i) -> p c t i", i=4),
+            )
+
+        def h_quantise(c0, n):
+            nc.vector.quantize_mx(
+                out=hc[:, c0:c0 + n].bitcast(FP8X4),
+                scales=hs[:, c0:c0 + n],
+                in_=hg[:, c0:c0 + n, :].rearrange("p c t -> p (c t)"),
+            )
+
+        h_out("s", acc0[0][:], 0, 0, 512)
+        h_out("v", acc0[2][:], 2, 0, 512)
+        h_out("s", acc0[1][:], 1, 0, 512)
+        h_out("v", acc0[3][:], 3, 0, 512)
+        for j in range(4):
+            conv1_pass(acc1[j][:], NG - 1, j, 512, 512, False, True)
+        h_regroup(0, 256)
+        h_regroup(256, 256)
+        h_quantise(0, 256)
+        h_quantise(256, 256)
+        h_out("s", acc1[0][:], 0, 512, 512)
+        h_out("s", acc1[1][:], 1, 512, 512)
+        h_out("v", acc1[3][:], 3, 512, 512)
+        h_out("s", acc1[2][:], 2, 512, 512)
+
+        acc2 = psum.tile([P, 512], F32, name="c2", tag="acc0")
+        for j in range(4):
+            for g in range(NG):
+                conv1_pass(acc2[:, j * P:(j + 1) * P], g, j, 1024, P, g == 0, g == NG - 1)
+        h_regroup(512, 256)
+        h_regroup(768, 256)
+        h_quantise(512, 256)
+        h_quantise(768, 256)
+        for j in range(4):
+            h_out("s", acc2[:, j * P:(j + 1) * P], j, 1024, P)
+        h_regroup(1024, P)
+        h_quantise(1024, P)
+
+        gacc = [psum.tile([P, 512], F32, name="g%d" % i, tag="acc%d" % (i + 1)) for i in range(2)]
+        for x in range(PIX):
+            for half in range(2):
+                nc.tensor.matmul_mx(
+                    out=gacc[half][:],
+                    lhsT=hc[:, x * P:(x + 1) * P].bitcast(FP8X4),
+                    lhsT_scale=hs[:, x * P:(x + 1) * P],
+                    rhs=wbc[:, half * 512:(half + 1) * 512].bitcast(FP8X4),
+                    rhs_scale=wbs[:, half * 512:(half + 1) * 512],
+                    start=x == 0,
+                    stop=x == PIX - 1,
+                )
+
+        for half in range(2):
+            cols = slice(half * 512, (half + 1) * 512)
+            nc.vector.scalar_tensor_tensor(
+                out=z[:, cols], in0=gacc[half][:], scalar=1.0 / PIX, in1=bb_bc[:, cols], op0=ALU.mult, op1=ALU.add
+            )
+            nc.scalar.activation(out=z[:, cols], in_=z[:, cols], func=ACT.Sigmoid)
+            nc.vector.scalar_tensor_tensor(
+                out=z[:, cols], in0=z[:, cols], scalar=1.0, in1=ft2[:, cols], op0=ALU.add, op1=ALU.mult
+            )
+            nc.sync.dma_start(out=out[:, cols], in_=z[:, cols])

@@ -14,11 +14,12 @@ ALU = mybir.AluOpType
 P = 128
 B, C, PIX = 128, 1024, 9
 C3, CH = 3 * C, C // 2
-NG = C3 // 512
+NK = C3 // 512
 COLS = PIX * B
 FLOPS = 2 * (CH * C3 * COLS + C * CH * COLS + B * C * C)
 
 MANUAL = True
+XQUEUE2 = "sync"
 
 
 def tile_joint_module_pb_kernel(tc, fv, ft, Wa, ba, Wb, bb, Wfc2, bfc2, out):
@@ -26,14 +27,18 @@ def tile_joint_module_pb_kernel(tc, fv, ft, Wa, ba, Wb, bb, Wfc2, bfc2, out):
     with ExitStack() as ctx:
         const = ctx.enter_context(tc.tile_pool(name="const", bufs=1))
         keep = ctx.enter_context(tc.tile_pool(name="keep", bufs=1))
-        fvraw_pool = ctx.enter_context(tc.tile_pool(name="fvraw", bufs=4))
-        wraw_pool = ctx.enter_context(tc.tile_pool(name="wraw", bufs=6))
-        tw_pool = ctx.enter_context(tc.tile_pool(name="tw", bufs=2))
-        grp_pool = ctx.enter_context(tc.tile_pool(name="grp", bufs=2))
+        xh_pool = ctx.enter_context(tc.tile_pool(name="xh", bufs=2))
+        slab_pool = ctx.enter_context(tc.tile_pool(name="slab", bufs=6))
+        tw_pool = ctx.enter_context(tc.tile_pool(name="tw", bufs=1))
+        w8_pool = ctx.enter_context(tc.tile_pool(name="w8", bufs=4))
+        wraw_pool = ctx.enter_context(tc.tile_pool(name="wraw", bufs=4))
         wag_pool = ctx.enter_context(tc.tile_pool(name="wag", bufs=2))
         psum = ctx.enter_context(tc.psum_pool(name="ps", bufs=1))
         if MANUAL:
             ctx.enter_context(tc.manual_schedule())
+
+        def slab(shape, name):
+            return slab_pool.tile(shape, BF16, name=name, tag="slab", align_bytes=64)
 
         ident = const.tile([P, P], F32, name="ident")
         make_identity(nc, ident[:])
@@ -49,21 +54,16 @@ def tile_joint_module_pb_kernel(tc, fv, ft, Wa, ba, Wb, bb, Wfc2, bfc2, out):
         nc.scalar.activation(out=warm_out[:], in_=warm_in[:], func=ACT.Sigmoid)
         nc.vector.tensor_copy(out=ba_f[:], in_=ba_raw[:])
 
-        fvc = keep.tile([P, NG, COLS], U32, name="fvc", align_bytes=64)
-        fvs = keep.tile([P, NG, COLS], U8, name="fvs", align_bytes=64)
-        wac = keep.tile([P, 2, NG, 256], U32, name="wac", align_bytes=64)
-        was = keep.tile([P, 2, NG, 256], U8, name="was", align_bytes=64)
-        wbg = keep.tile([P, C, 2], F32, name="wbg", align_bytes=64)
+        fvc = keep.tile([P, NK, COLS], U32, name="fvc", align_bytes=64)
+        fvs = keep.tile([P, NK, COLS], U8, name="fvs", align_bytes=64)
+        wac = keep.tile([P, 2, NK, 256], U32, name="wac", align_bytes=64)
+        was = keep.tile([P, 2, NK, 256], U8, name="was", align_bytes=64)
         wbc = keep.tile([P, C], U32, name="wbc", align_bytes=64)
         wbs = keep.tile([P, C], U8, name="wbs", align_bytes=64)
-        wfT = keep.tile([P, 4, C], F32, name="wfT")
         ftT = keep.tile([P, 4, P], F32, name="ftT")
         ft2 = keep.tile([P, C], F32, name="ft2")
-        hp = keep.tile([P, 4, COLS], BF16, name="hp")
-        hg = keep.tile([P, COLS, 4], BF16, name="hg", align_bytes=64)
         hc = keep.tile([P, COLS], U32, name="hc", align_bytes=64)
         hs = keep.tile([P, COLS], U8, name="hs", align_bytes=64)
-        z = keep.tile([P, C], F32, name="z")
         ft_raw = const.tile([P, C], BF16, name="ft_raw")
         bfc_bc = const.tile([P, C], BF16, name="bfc_bc")
         bb_bc = const.tile([P, C], BF16, name="bb_bc")
@@ -72,16 +72,37 @@ def tile_joint_module_pb_kernel(tc, fv, ft, Wa, ba, Wb, bb, Wfc2, bfc2, out):
         wa_view = Wa.rearrange("(s p e) c -> s p e c", s=2, e=2)
         wf_view = Wfc2.rearrange("(t p) c -> p t c", p=P)
         wb_view = Wb.rearrange("(t p) m -> p t m", p=P)
-        fv_raw = []
-        wa_raw = []
-        for g in range(NG):
-            r = fvraw_pool.tile([P, 4608], BF16, name="fvr", tag="fvr")
-            nc.sync.dma_start(out=r[:], in_=fv_flat[:, g * 4608:(g + 1) * 4608])
-            fv_raw.append(r)
-            sm, gp = g % 2, g // 2
-            r = wraw_pool.tile([P, 2, 1024], BF16, name="war", tag="wr")
-            nc.sync.dma_start(out=r[:], in_=wa_view[sm][:, :, gp * 1024:(gp + 1) * 1024])
-            wa_raw.append(r)
+        fv_raw = {}
+        wab_raw = []
+        for k in (4, 5):
+            fv_raw[k] = slab([P, 4608], "fvr")
+            nc.sync.dma_start(out=fv_raw[k][:], in_=fv_flat[:, k * 4608:(k + 1) * 4608])
+            if k == 4:
+                for sm in range(2):
+                    r = wraw_pool.tile([P, 2, 1024], BF16, name="war", tag="wr")
+                    nc.sync.dma_start(out=r[:], in_=wa_view[sm][:, :, 2048:3072])
+                    wab_raw.append(r)
+        wa1_raw = []
+        for sm in range(2):
+            r = w8_pool.tile([P, 2, 2048], BF16, name="wa1r", tag="w8", align_bytes=64)
+            nc.sync.dma_start(out=r[:], in_=wa_view[sm][:, :, 0:2048])
+            wa1_raw.append(r)
+        xh = []
+        for bh in range(2):
+            xt = xh_pool.tile([P, 64, 144], BF16, name="xh")
+            src = fv_flat[bh * 64:(bh + 1) * 64, 0:18432].rearrange(
+                "b (g c h e) -> c h g b e", g=16, c=4, h=2
+            )
+            for cls in range(4):
+                for half in range(2):
+                    q0 = 32 * cls + half
+                    eng = nc.sync
+                    if cls >= 2 and XQUEUE2 == "gpsimd":
+                        eng = nc.gpsimd
+                    if cls >= 2 and XQUEUE2 == "scalar":
+                        eng = nc.scalar
+                    eng.dma_start(out=xt[q0:q0 + 31:2, :, :], in_=src[cls, half])
+            xh.append(xt)
         nc.sync.dma_start(out=ft_raw[:], in_=ft)
         wf_raw = []
         for i in range(4):
@@ -98,157 +119,222 @@ def tile_joint_module_pb_kernel(tc, fv, ft, Wa, ba, Wb, bb, Wfc2, bfc2, out):
 
         used = []
 
-        def tbank(nrot):
-            tag = "tr%d" % (len(used) % nrot)
+        def tbank(prefix, nrot):
+            tag = "%s%d" % (prefix, len(used) % nrot)
             used.append(tag)
             return psum.tile([P, 512], F32, name=tag, tag=tag)
 
-        def conv1_pass(acc, g, j, c0, n, start, stop):
+        def conv1_pass(acc, k, j, c0, n, start, stop):
             sm, em = divmod(j, 2)
             nc.tensor.matmul_mx(
                 out=acc,
-                lhsT=wac[:, sm, g, em * P:(em + 1) * P].bitcast(FP8X4),
-                lhsT_scale=was[:, sm, g, em * P:(em + 1) * P],
-                rhs=fvc[:, g, c0:c0 + n].bitcast(FP8X4),
-                rhs_scale=fvs[:, g, c0:c0 + n],
+                lhsT=wac[:, sm, k, em * P:(em + 1) * P].bitcast(FP8X4),
+                lhsT_scale=was[:, sm, k, em * P:(em + 1) * P],
+                rhs=fvc[:, k, c0:c0 + n].bitcast(FP8X4),
+                rhs_scale=fvs[:, k, c0:c0 + n],
                 start=start,
                 stop=stop,
             )
 
-        tws = {}
-        grps = {}
-
-        def tf_bank(g, w0, nw):
-            pb = tbank(4)
-            fw = fv_raw[g][:].bitcast(F32)
-            for s in range(2):
-                for wl in range(nw):
-                    st = s * 1152 + w0 + wl
-                    slot = s * nw + wl
-                    nc.tensor.transpose(pb[:, slot * P:(slot + 1) * P], fw[:, st:st + 1144:9], ident[:])
-            nc.scalar.copy(
-                out=tws[g][:, :, w0 * P:(w0 + nw) * P],
-                in_=pb[:, 0:2 * nw * P].rearrange("p (s r) -> p s r", s=2),
+        def fv_quantise(k, gt, c0, n):
+            nc.vector.quantize_mx(
+                out=fvc[:, k, c0:c0 + n].bitcast(FP8X4),
+                scales=fvs[:, k, c0:c0 + n],
+                in_=gt[:, 4 * c0:4 * (c0 + n)],
             )
 
-        def regroup_quantise(g):
-            tb = tws[g][:].bitcast(BF16)
+        def tf_chunk(k, tw):
+            fw = fv_raw[k][:].bitcast(F32)
+            for w0, nw in ((0, 2), (4, 2), (6, 2), (2, 2), (8, 1)):
+                pb = tbank("tr", 4)
+                for s in range(2):
+                    for wl in range(nw):
+                        st = s * 1152 + w0 + wl
+                        slot = s * nw + wl
+                        nc.tensor.transpose(pb[:, slot * P:(slot + 1) * P], fw[:, st:st + 1144:9], ident[:])
+                nc.scalar.copy(
+                    out=tw[:, :, w0 * P:(w0 + nw) * P],
+                    in_=pb[:, 0:2 * nw * P].rearrange("p (s r) -> p s r", s=2),
+                )
+
+        def tf_regroup(tw, gt):
+            tb = tw[:].bitcast(BF16)
             ev = tb[:, :, 0:2050].rearrange("p s (e r) -> p s e r", e=2)
             od = tb[:, :, 1:2559].rearrange("p s (e r) -> p s e r", e=2)
             l8 = tb[:, :, 254:2304].rearrange("p s (e r) -> p s e r", e=2)
-            gt = grps[g]
-            gf = gt[:].rearrange("p x b t -> p (x b t)")
-
-            def cp(src, a0, a1, x0):
+            g3 = gt[:].rearrange("p (b x t) -> p b x t", x=PIX, t=4)
+            for src, x0 in ((ev, 0), (od, 1)):
                 nc.vector.tensor_copy(
-                    out=gt[:, x0 + 2 * a0:x0 + 2 * a1:2].rearrange("p a b (s e) -> p a b s e", s=2),
-                    in_=src[:, :, :, a0 * 256:a1 * 256:2].rearrange("p s e (a b) -> p a b s e", a=a1 - a0),
+                    out=g3[:, :, x0:x0 + 8:2, :].rearrange("p b a (s e) -> p a b s e", s=2),
+                    in_=src[:, :, :, 0:1024:2].rearrange("p s e (a b) -> p a b s e", a=4),
                 )
-
-            def qz(c0, n):
-                nc.vector.quantize_mx(
-                    out=fvc[:, g, c0:c0 + n].bitcast(FP8X4),
-                    scales=fvs[:, g, c0:c0 + n],
-                    in_=gf[:, 4 * c0:4 * (c0 + n)],
-                )
-
-            cp(ev, 0, 2, 0)
-            cp(od, 0, 2, 1)
-            cp(ev, 2, 4, 0)
-            qz(0, 512)
-            cp(od, 2, 4, 1)
             nc.vector.tensor_copy(
-                out=gt[:, 8].rearrange("p b (s e) -> p b s e", s=2),
+                out=g3[:, :, 8, :].rearrange("p b (s e) -> p b s e", s=2),
                 in_=l8[:, :, :, 770:1025:2].rearrange("p s e b -> p b s e"),
             )
-            qz(512, 512)
-            qz(1024, 128)
 
-        def wa_unit(i):
-            sm, gp = i % 2, i // 2
-            ww = wa_raw[i][:].bitcast(F32)
-            wag = wag_pool.tile([P, 2, 2, P, 2], F32, name="wag", align_bytes=64)
+        def wa_unit(sm, gp, ww):
+            wag = wag_pool.tile([P, 2, 2, P, 2], F32, name="wag", tag="wag", align_bytes=64)
             for g2 in range(2):
-                pb = tbank(4)
+                pb = tbank("tr", 4)
                 for em in range(2):
                     for s in range(2):
                         slot = em * 2 + s
-                        c0 = 256 * g2 + P * s
-                        nc.tensor.transpose(pb[:, slot * P:(slot + 1) * P], ww[:, em, c0:c0 + P], ident[:])
+                        if gp == 2:
+                            c0 = 256 * g2 + P * s
+                            stat = ww[:, em, c0:c0 + P]
+                        else:
+                            c0 = 2 * (2 * gp + g2) + s
+                            stat = ww[:, em, c0:c0 + 1017:8]
+                        nc.tensor.transpose(pb[:, slot * P:(slot + 1) * P], stat, ident[:])
                 nc.scalar.copy(out=wag[:, g2], in_=pb[:].rearrange("p (e s q) -> p e q s", e=2, s=2))
             return wag
 
-        def wa_quantise(i, wag):
-            sm, gp = i % 2, i // 2
+        def wa_quantise(sm, gp, wag):
             nc.vector.quantize_mx(
                 out=wac[:, sm, 2 * gp:2 * gp + 2, :].rearrange("p g w -> p (g w)").bitcast(FP8X4),
                 scales=was[:, sm, 2 * gp:2 * gp + 2, :].rearrange("p g w -> p (g w)"),
                 in_=wag[:].rearrange("p g e q s -> p (g e q s)").bitcast(BF16),
             )
 
-        acc0 = []
-        m0 = [(g, j) for g in range(NG) for j in range(4)]
+        tw4 = tw_pool.tile([P, 2, 1280], F32, name="tw")
+        g4 = slab([P, 4608], "grp")
+        tf_chunk(4, tw4)
+        wq0 = wa_unit(0, 2, wab_raw[0][:].bitcast(F32))
+        wq1 = wa_unit(1, 2, wab_raw[1][:].bitcast(F32))
+        tf_regroup(tw4, g4)
+        wa_quantise(0, 2, wq0)
+        fv_quantise(4, g4, 0, 512)
+        fv_quantise(4, g4, 512, 512)
+        fv_quantise(4, g4, 1024, P)
+        wa_quantise(1, 2, wq1)
 
-        def m0_pair(k):
-            for g, j in m0[2 * k:2 * k + 2]:
-                if g == 0:
-                    acc0.append(psum.tile([P, 512], F32, name="acc%d" % j, tag="acc%d" % j))
-                conv1_pass(acc0[j][:], g, j, 0, 512, g == 0, g == NG - 1)
+        tw5 = tw_pool.tile([P, 2, 1280], F32, name="tw")
+        g5 = slab([P, 4608], "grp")
+        tf_chunk(5, tw5)
+        wp = []
+        for sm in range(2):
+            t = w8_pool.tile([P, 2, 1024], F32, name="wp", tag="w8", align_bytes=64)
+            rw = wa1_raw[sm][:].bitcast(F32)
+            for em in range(2):
+                nc.scalar.copy(
+                    out=t[:, em, :].rearrange("p (c g r) -> p c g r", c=4, g=16),
+                    in_=rw[:, em, :].rearrange("p (g c r) -> p c g r", g=16, c=4),
+                )
+            wp.append(t)
+        tf_regroup(tw5, g5)
+        wq0 = wa_unit(0, 0, wp[0][:])
+        wa_quantise(0, 0, wq0)
+        fv_quantise(5, g5, 0, 512)
+        fv_quantise(5, g5, 512, 512)
+        fv_quantise(5, g5, 1024, P)
+        for sm, gp in ((1, 0), (0, 1), (1, 1)):
+            wq0 = wa_unit(sm, gp, wp[sm][:])
+            wa_quantise(sm, gp, wq0)
 
-        for g in range(NG):
-            tws[g] = tw_pool.tile([P, 2, 1280], F32, name="tw")
-            grps[g] = grp_pool.tile([P, PIX, P, 4], BF16, name="grp", align_bytes=64)
-            tf_bank(g, 0, 2)
-            tf_bank(g, 4, 2)
-            tf_bank(g, 6, 2)
-            if g >= 2:
-                m0_pair(2 * (g - 2))
-            tf_bank(g, 2, 2)
-            tf_bank(g, 8, 1)
-            wag = wa_unit(g)
-            if g >= 2:
-                m0_pair(2 * (g - 2) + 1)
-            regroup_quantise(g)
-            wa_quantise(g, wag)
+        acc0 = [psum.tile([P, 512], F32, name="acc%d" % j, tag="acc%d" % j) for j in range(4)]
+        acc1 = [psum.tile([P, 512], F32, name="c1_%d" % j, tag="tr%d" % j) for j in range(4)]
+        for k in (4, 5):
+            for j in range(4):
+                conv1_pass(acc0[j][:], k, j, 0, 512, k == 4, False)
+        for k in (4, 5):
+            for j in range(4):
+                conv1_pass(acc1[j][:], k, j, 512, 512, k == 4, False)
 
-        m0_pair(8)
-        m0_pair(9)
-        pb = tbank(3)
-        fw = ft_raw[:].bitcast(F32)
+        ga = [slab([P, 4608], "grp") for g in range(4)]
+
+        def a_regroup(g, bh):
+            nc.vector.tensor_copy(
+                out=ga[g][:, bh * 2304:(bh + 1) * 2304].rearrange("p (b x j) -> p b x j", x=PIX, j=4),
+                in_=xh[bh][:, :, 36 * g:36 * g + 36].rearrange("p b (j x) -> p b x j", j=4),
+            )
+
+        a_regroup(0, 0)
+        a_regroup(1, 0)
+        fv_quantise(0, ga[0], 0, 512)
+        a_regroup(2, 0)
+        fv_quantise(1, ga[1], 0, 512)
+        a_regroup(3, 0)
+        fv_quantise(2, ga[2], 0, 512)
+        fv_quantise(3, ga[3], 0, 512)
         for k in range(4):
-            nc.tensor.transpose(pb[:, k * P:(k + 1) * P], fw[:, k * P:(k + 1) * P], ident[:])
-        nc.scalar.copy(out=ftT[:].rearrange("p k b -> p (k b)"), in_=pb[:])
-        ft_e = ftT[:].bitcast(BF16).rearrange("p k (b e) -> p k b e", e=2)
-        wf_e = wfT[:].bitcast(BF16).rearrange("p k (o e) -> p k o e", e=2)
+            for j in range(4):
+                conv1_pass(acc0[j][:], k, j, 0, 512, False, k == 3)
+
+        hp = slab([P, 4, PIX, P], "hp")
+        hg = slab([P, COLS, 4], "hg")
+
+        def h_piece(eng, dst, src, j):
+            if eng == "s":
+                nc.scalar.activation(out=dst, in_=src, func=ACT.Relu, bias=ba_f[:, j:j + 1], scale=1.0)
+            else:
+                nc.vector.tensor_scalar(
+                    out=dst, in0=src, scalar1=ba_f[:, j:j + 1], scalar2=0.0, op0=ALU.add, op1=ALU.max
+                )
+
+        def h_out(eng, bank, j, n0, n):
+            head = (PIX - n0 % PIX) % PIX
+            nb = (n - head) // PIX
+            b0 = (n0 + head) // PIX
+            tail = n - head - PIX * nb
+            h_piece(
+                eng,
+                hp[:, j, :, b0:b0 + nb],
+                bank[:, head:head + PIX * nb].rearrange("p (b x) -> p x b", x=PIX),
+                j,
+            )
+            if head:
+                h_piece(eng, hp[:, j, PIX - head:PIX, b0 - 1], bank[:, 0:head], j)
+            if tail:
+                h_piece(eng, hp[:, j, 0:tail, b0 + nb], bank[:, n - tail:n], j)
+
+        for j in range(4):
+            h_out("s", acc0[j][:], j, 0, 512)
+
+        wfT = [w8_pool.tile([P, 2, C], F32, name="wfT", tag="w8", align_bytes=64) for h in range(2)]
+        wbg = w8_pool.tile([P, C, 2], F32, name="wbg", tag="w8", align_bytes=64)
+
+        def ft_unit():
+            pb = tbank("acc", 3)
+            fw = ft_raw[:].bitcast(F32)
+            for k in range(4):
+                nc.tensor.transpose(pb[:, k * P:(k + 1) * P], fw[:, k * P:(k + 1) * P], ident[:])
+            nc.scalar.copy(out=ftT[:].rearrange("p k b -> p (k b)"), in_=pb[:])
 
         def wf_unit(i):
             ww = wf_raw[i][:].bitcast(F32)
             for h in range(2):
-                pb = tbank(3)
+                pb = tbank("acc", 3)
                 for kl in range(2):
                     for tl in range(2):
                         slot = kl * 2 + tl
                         k = 2 * h + kl
                         nc.tensor.transpose(pb[:, slot * P:(slot + 1) * P], ww[:, tl, k * P:(k + 1) * P], ident[:])
                 nc.scalar.copy(
-                    out=wfT[:, 2 * h:2 * h + 2, i * 256:(i + 1) * 256],
+                    out=wfT[h][:, :, i * 256:(i + 1) * 256],
                     in_=pb[:].rearrange("p (k o) -> p k o", k=2),
                 )
 
-        def fc(half):
-            acc = psum.tile([P, 512], F32, name="fc", tag="tr3")
+        def fc(half, tag):
+            acc = psum.tile([P, 512], F32, name="fc", tag=tag)
             cols = slice(half * 512, (half + 1) * 512)
+            ft_e = ftT[:].bitcast(BF16).rearrange("p k (b e) -> p k b e", e=2)
             for idx in range(8):
                 k, e = divmod(idx, 2)
+                wf_e = wfT[k // 2][:].bitcast(BF16).rearrange("p k (o e) -> p k o e", e=2)
                 nc.tensor.matmul(
-                    out=acc[:], lhsT=ft_e[:, k, :, e], rhs=wf_e[:, k, cols, e], start=idx == 0, stop=idx == 7
+                    out=acc[:], lhsT=ft_e[:, k, :, e], rhs=wf_e[:, k % 2, cols, e], start=idx == 0, stop=idx == 7
                 )
+            return acc
+
+        def fc_add(half, acc):
+            cols = slice(half * 512, (half + 1) * 512)
             nc.vector.tensor_tensor(out=ft2[:, cols], in0=acc[:], in1=bfc_bc[:, cols], op=ALU.add)
 
         def wb_unit(i):
             ww = wb_raw[i][:].bitcast(F32)
             for h in range(2):
-                pb = tbank(3)
+                pb = tbank("acc", 3)
                 for tl in range(2):
                     for sm in range(2):
                         slot = tl * 2 + sm
@@ -260,43 +346,66 @@ def tile_joint_module_pb_kernel(tc, fv, ft, Wa, ba, Wb, bb, Wfc2, bfc2, out):
                     out=wbg[:, o0:o0 + 256, :].rearrange("p (t o) s -> p t o s", t=2),
                     in_=pb[:].rearrange("p (t s o) -> p t o s", t=2, s=2),
                 )
+
+        def wb_quantise(i):
             nc.vector.quantize_mx(
                 out=wbc[:, i * 512:(i + 1) * 512].bitcast(FP8X4),
                 scales=wbs[:, i * 512:(i + 1) * 512],
                 in_=wbg[:, i * 512:(i + 1) * 512, :].rearrange("p o s -> p (o s)").bitcast(BF16),
             )
 
+        def c1_passes(k):
+            for j in range(4):
+                conv1_pass(acc1[j][:], k, j, 512, 512, False, k == 3)
+
+        def a_quantise_rest(g):
+            fv_quantise(g, ga[g], 512, 512)
+            fv_quantise(g, ga[g], 1024, P)
+
+        a_regroup(0, 1)
+        a_regroup(1, 1)
+        a_quantise_rest(0)
+        ft_unit()
         wf_unit(0)
+        c1_passes(0)
+        a_regroup(2, 1)
+        a_quantise_rest(1)
         wf_unit(1)
         wf_unit(2)
-        fc(0)
+        c1_passes(1)
+        a_regroup(3, 1)
+        a_quantise_rest(2)
         wf_unit(3)
         wb_unit(0)
-        fc(1)
+        c1_passes(2)
+        wb_quantise(0)
+        a_quantise_rest(3)
         wb_unit(1)
+        c1_passes(3)
+        wb_quantise(1)
 
-        acc1 = [psum.tile([P, 512], F32, name="c1_%d" % j, tag="tr%d" % j) for j in range(4)]
-        for g in range(NG - 1):
-            for j in range(4):
-                conv1_pass(acc1[j][:], g, j, 512, 512, g == 0, False)
-        m0_pair(10)
-        m0_pair(11)
+        h_out("s", acc1[0][:], 0, 512, 512)
+        h_out("v", acc1[2][:], 2, 512, 512)
+        h_out("s", acc1[1][:], 1, 512, 512)
+        h_out("v", acc1[3][:], 3, 512, 512)
 
-        def h_out(eng, bank, j, c0, n):
-            if eng == "s":
-                nc.scalar.activation(
-                    out=hp[:, j, c0:c0 + n], in_=bank, func=ACT.Relu, bias=ba_f[:, j:j + 1], scale=1.0
-                )
-            else:
-                nc.vector.tensor_scalar(
-                    out=hp[:, j, c0:c0 + n], in0=bank, scalar1=ba_f[:, j:j + 1], scalar2=0.0,
-                    op0=ALU.add, op1=ALU.max,
-                )
+        acc2 = psum.tile([P, 512], F32, name="c2", tag="acc0")
+        order = (4, 5, 0, 1, 2, 3)
+        for j in range(4):
+            for k in order:
+                conv1_pass(acc2[:, j * P:(j + 1) * P], k, j, 1024, P, k == 4, k == 3)
+        h_out("s", acc2[:, 0:P], 0, 1024, P)
+        h_out("v", acc2[:, 2 * P:3 * P], 2, 1024, P)
+        h_out("s", acc2[:, P:2 * P], 1, 1024, P)
+        h_out("v", acc2[:, 3 * P:4 * P], 3, 1024, P)
+        fc0 = fc(0, "acc3")
+
+        hpf = hp[:].rearrange("p t x b -> p t (x b)")
 
         def h_regroup(c0, n):
             nc.vector.tensor_copy(
                 out=hg[:, c0:c0 + n, :].rearrange("p (c i) t -> p c t i", i=4),
-                in_=hp[:, :, c0:c0 + n].rearrange("p t (c i) -> p c t i", i=4),
+                in_=hpf[:, :, c0:c0 + n].rearrange("p t (c i) -> p c t i", i=4),
             )
 
         def h_quantise(c0, n):
@@ -306,35 +415,19 @@ def tile_joint_module_pb_kernel(tc, fv, ft, Wa, ba, Wb, bb, Wfc2, bfc2, out):
                 in_=hg[:, c0:c0 + n, :].rearrange("p c t -> p (c t)"),
             )
 
-        h_out("s", acc0[0][:], 0, 0, 512)
-        h_out("v", acc0[2][:], 2, 0, 512)
-        h_out("s", acc0[1][:], 1, 0, 512)
-        h_out("v", acc0[3][:], 3, 0, 512)
-        for j in range(4):
-            conv1_pass(acc1[j][:], NG - 1, j, 512, 512, False, True)
         h_regroup(0, 256)
         h_regroup(256, 256)
         h_quantise(0, 256)
-        h_quantise(256, 256)
-        h_out("s", acc1[0][:], 0, 512, 512)
-        h_out("s", acc1[1][:], 1, 512, 512)
-        h_out("v", acc1[3][:], 3, 512, 512)
-        h_out("s", acc1[2][:], 2, 512, 512)
-
-        acc2 = psum.tile([P, 512], F32, name="c2", tag="acc0")
-        for j in range(4):
-            for g in range(NG):
-                conv1_pass(acc2[:, j * P:(j + 1) * P], g, j, 1024, P, g == 0, g == NG - 1)
         h_regroup(512, 256)
+        h_quantise(256, 256)
         h_regroup(768, 256)
         h_quantise(512, 256)
-        h_quantise(768, 256)
-        for j in range(4):
-            h_out("s", acc2[:, j * P:(j + 1) * P], j, 1024, P)
         h_regroup(1024, P)
+        h_quantise(768, 256)
         h_quantise(1024, P)
+        fc_add(0, fc0)
 
-        gacc = [psum.tile([P, 512], F32, name="g%d" % i, tag="acc%d" % (i + 1)) for i in range(2)]
+        gacc = [psum.tile([P, 512], F32, name="g%d" % i, tag="tr%d" % i) for i in range(2)]
         for x in range(PIX):
             for half in range(2):
                 nc.tensor.matmul_mx(
@@ -346,13 +439,19 @@ def tile_joint_module_pb_kernel(tc, fv, ft, Wa, ba, Wb, bb, Wfc2, bfc2, out):
                     start=x == 0,
                     stop=x == PIX - 1,
                 )
+        fc1 = fc(1, "acc1")
 
+        z = wag_pool.tile([P, C], F32, name="z", tag="wag", align_bytes=64)
         for half in range(2):
             cols = slice(half * 512, (half + 1) * 512)
             nc.vector.scalar_tensor_tensor(
                 out=z[:, cols], in0=gacc[half][:], scalar=1.0 / PIX, in1=bb_bc[:, cols], op0=ALU.mult, op1=ALU.add
             )
             nc.scalar.activation(out=z[:, cols], in_=z[:, cols], func=ACT.Sigmoid)
+        for half in range(2):
+            cols = slice(half * 512, (half + 1) * 512)
+            if half == 1:
+                fc_add(1, fc1)
             nc.vector.scalar_tensor_tensor(
                 out=z[:, cols], in0=z[:, cols], scalar=1.0, in1=ft2[:, cols], op0=ALU.add, op1=ALU.mult
             )

@@ -19,7 +19,6 @@ COLS = PIX * B
 FLOPS = 2 * (CH * C3 * COLS + C * CH * COLS + B * C * C)
 
 MANUAL = True
-XQUEUE2 = "sync"
 
 
 def tile_joint_module_pb_kernel(tc, fv, ft, Wa, ba, Wb, bb, Wfc2, bfc2, out):
@@ -87,35 +86,34 @@ def tile_joint_module_pb_kernel(tc, fv, ft, Wa, ba, Wb, bb, Wfc2, bfc2, out):
             r = w8_pool.tile([P, 2, 2048], BF16, name="wa1r", tag="w8", align_bytes=64)
             nc.sync.dma_start(out=r[:], in_=wa_view[sm][:, :, 0:2048])
             wa1_raw.append(r)
-        xh = []
-        for bh in range(2):
-            xt = xh_pool.tile([P, 64, 144], BF16, name="xh")
+        xh = [xh_pool.tile([P, 64, 144], BF16, name="xh") for bh in range(2)]
+
+        def x_load(eng, bh, classes):
             src = fv_flat[bh * 64:(bh + 1) * 64, 0:18432].rearrange(
                 "b (g c h e) -> c h g b e", g=16, c=4, h=2
             )
-            for cls in range(4):
+            for cls in classes:
                 for half in range(2):
                     q0 = 32 * cls + half
-                    eng = nc.sync
-                    if cls >= 2 and XQUEUE2 == "gpsimd":
-                        eng = nc.gpsimd
-                    if cls >= 2 and XQUEUE2 == "scalar":
-                        eng = nc.scalar
-                    eng.dma_start(out=xt[q0:q0 + 31:2, :, :], in_=src[cls, half])
-            xh.append(xt)
-        nc.sync.dma_start(out=ft_raw[:], in_=ft)
+                    eng.dma_start(out=xh[bh][q0:q0 + 31:2, :, :], in_=src[cls, half])
+
         wf_raw = []
-        for i in range(4):
-            r = wraw_pool.tile([P, 2, 1024], BF16, name="wfr", tag="wr")
-            nc.sync.dma_start(out=r[:], in_=wf_view[:, 2 * i:2 * i + 2, :])
-            wf_raw.append(r)
         wb_raw = []
-        for i in range(2):
-            r = wraw_pool.tile([P, 4, 512], BF16, name="wbr", tag="wr")
-            nc.sync.dma_start(out=r[:], in_=wb_view[:, 4 * i:4 * i + 4, :])
-            wb_raw.append(r)
-        nc.sync.dma_start(out=bfc_bc[:], in_=bfc2.partition_broadcast(P))
-        nc.sync.dma_start(out=bb_bc[:], in_=bb.partition_broadcast(P))
+
+        def late_loads():
+            nc.sync.dma_start(out=ft_raw[:], in_=ft)
+            for i in range(4):
+                r = wraw_pool.tile([P, 2, 1024], BF16, name="wfr", tag="wr")
+                nc.sync.dma_start(out=r[:], in_=wf_view[:, 2 * i:2 * i + 2, :])
+                wf_raw.append(r)
+            for i in range(2):
+                r = wraw_pool.tile([P, 4, 512], BF16, name="wbr", tag="wr")
+                nc.sync.dma_start(out=r[:], in_=wb_view[:, 4 * i:4 * i + 4, :])
+                wb_raw.append(r)
+            nc.sync.dma_start(out=bfc_bc[:], in_=bfc2.partition_broadcast(P))
+            nc.sync.dma_start(out=bb_bc[:], in_=bb.partition_broadcast(P))
+
+        x_load(nc.sync, 0, (0, 1))
 
         used = []
 
@@ -202,6 +200,8 @@ def tile_joint_module_pb_kernel(tc, fv, ft, Wa, ba, Wb, bb, Wfc2, bfc2, out):
         tf_chunk(4, tw4)
         wq0 = wa_unit(0, 2, wab_raw[0][:].bitcast(F32))
         wq1 = wa_unit(1, 2, wab_raw[1][:].bitcast(F32))
+        x_load(nc.scalar, 0, (2, 3))
+        x_load(nc.sync, 1, (0, 1))
         tf_regroup(tw4, g4)
         wa_quantise(0, 2, wq0)
         fv_quantise(4, g4, 0, 512)
@@ -231,6 +231,8 @@ def tile_joint_module_pb_kernel(tc, fv, ft, Wa, ba, Wb, bb, Wfc2, bfc2, out):
         for sm, gp in ((1, 0), (0, 1), (1, 1)):
             wq0 = wa_unit(sm, gp, wp[sm][:])
             wa_quantise(sm, gp, wq0)
+        x_load(nc.scalar, 1, (2, 3))
+        late_loads()
 
         acc0 = [psum.tile([P, 512], F32, name="acc%d" % j, tag="acc%d" % j) for j in range(4)]
         acc1 = [psum.tile([P, 512], F32, name="c1_%d" % j, tag="tr%d" % j) for j in range(4)]

@@ -14,7 +14,7 @@ ALU = mybir.AluOpType
 P = 128
 B, C, PIX = 128, 1024, 9
 C3, CH = 3 * C, C // 2
-NK = C3 // 512
+NG = C3 // 512
 COLS = PIX * B
 FLOPS = 2 * (CH * C3 * COLS + C * CH * COLS + B * C * C)
 
@@ -26,18 +26,14 @@ def tile_joint_module_pb_kernel(tc, fv, ft, Wa, ba, Wb, bb, Wfc2, bfc2, out):
     with ExitStack() as ctx:
         const = ctx.enter_context(tc.tile_pool(name="const", bufs=1))
         keep = ctx.enter_context(tc.tile_pool(name="keep", bufs=1))
-        xh_pool = ctx.enter_context(tc.tile_pool(name="xh", bufs=2))
-        slab_pool = ctx.enter_context(tc.tile_pool(name="slab", bufs=6))
-        tw_pool = ctx.enter_context(tc.tile_pool(name="tw", bufs=1))
-        w8_pool = ctx.enter_context(tc.tile_pool(name="w8", bufs=4))
-        wraw_pool = ctx.enter_context(tc.tile_pool(name="wraw", bufs=4))
+        fvraw_pool = ctx.enter_context(tc.tile_pool(name="fvraw", bufs=4))
+        wraw_pool = ctx.enter_context(tc.tile_pool(name="wraw", bufs=6))
+        odd_pool = ctx.enter_context(tc.tile_pool(name="odd", bufs=3))
+        grp_pool = ctx.enter_context(tc.tile_pool(name="grp", bufs=2))
         wag_pool = ctx.enter_context(tc.tile_pool(name="wag", bufs=2))
         psum = ctx.enter_context(tc.psum_pool(name="ps", bufs=1))
         if MANUAL:
             ctx.enter_context(tc.manual_schedule())
-
-        def slab(shape, name):
-            return slab_pool.tile(shape, BF16, name=name, tag="slab", align_bytes=64)
 
         ident = const.tile([P, P], F32, name="ident")
         make_identity(nc, ident[:])
@@ -53,16 +49,21 @@ def tile_joint_module_pb_kernel(tc, fv, ft, Wa, ba, Wb, bb, Wfc2, bfc2, out):
         nc.scalar.activation(out=warm_out[:], in_=warm_in[:], func=ACT.Sigmoid)
         nc.vector.tensor_copy(out=ba_f[:], in_=ba_raw[:])
 
-        fvc = keep.tile([P, NK, COLS], U32, name="fvc", align_bytes=64)
-        fvs = keep.tile([P, NK, COLS], U8, name="fvs", align_bytes=64)
-        wac = keep.tile([P, 2, NK, 256], U32, name="wac", align_bytes=64)
-        was = keep.tile([P, 2, NK, 256], U8, name="was", align_bytes=64)
+        fvc = keep.tile([P, NG, COLS], U32, name="fvc", align_bytes=64)
+        fvs = keep.tile([P, NG, COLS], U8, name="fvs", align_bytes=64)
+        wac = keep.tile([P, 2, NG, 256], U32, name="wac", align_bytes=64)
+        was = keep.tile([P, 2, NG, 256], U8, name="was", align_bytes=64)
+        wbg = keep.tile([P, C, 2], F32, name="wbg", align_bytes=64)
         wbc = keep.tile([P, C], U32, name="wbc", align_bytes=64)
         wbs = keep.tile([P, C], U8, name="wbs", align_bytes=64)
+        wfT = keep.tile([P, 4, C], F32, name="wfT")
         ftT = keep.tile([P, 4, P], F32, name="ftT")
         ft2 = keep.tile([P, C], F32, name="ft2")
+        hp = keep.tile([P, 4, COLS], BF16, name="hp")
+        hg = keep.tile([P, COLS, 4], BF16, name="hg", align_bytes=64)
         hc = keep.tile([P, COLS], U32, name="hc", align_bytes=64)
         hs = keep.tile([P, COLS], U8, name="hs", align_bytes=64)
+        z = keep.tile([P, C], F32, name="z")
         ft_raw = const.tile([P, C], BF16, name="ft_raw")
         bfc_bc = const.tile([P, C], BF16, name="bfc_bc")
         bb_bc = const.tile([P, C], BF16, name="bb_bc")
@@ -71,272 +72,185 @@ def tile_joint_module_pb_kernel(tc, fv, ft, Wa, ba, Wb, bb, Wfc2, bfc2, out):
         wa_view = Wa.rearrange("(s p e) c -> s p e c", s=2, e=2)
         wf_view = Wfc2.rearrange("(t p) c -> p t c", p=P)
         wb_view = Wb.rearrange("(t p) m -> p t m", p=P)
-        fv_raw = {}
-        wab_raw = []
-        for k in (4, 5):
-            fv_raw[k] = slab([P, 4608], "fvr")
-            nc.sync.dma_start(out=fv_raw[k][:], in_=fv_flat[:, k * 4608:(k + 1) * 4608])
-            if k == 4:
-                for sm in range(2):
-                    r = wraw_pool.tile([P, 2, 1024], BF16, name="war", tag="wr")
-                    nc.sync.dma_start(out=r[:], in_=wa_view[sm][:, :, 2048:3072])
-                    wab_raw.append(r)
-        wa1_raw = []
-        for sm in range(2):
-            r = w8_pool.tile([P, 2, 2048], BF16, name="wa1r", tag="w8", align_bytes=64)
-            nc.sync.dma_start(out=r[:], in_=wa_view[sm][:, :, 0:2048])
-            wa1_raw.append(r)
-        xh = [xh_pool.tile([P, 64, 144], BF16, name="xh") for bh in range(2)]
-
-        def x_load(eng, bh, classes):
-            src = fv_flat[bh * 64:(bh + 1) * 64, 0:18432].rearrange(
-                "b (g c h e) -> c h g b e", g=16, c=4, h=2
-            )
-            for cls in classes:
-                for half in range(2):
-                    q0 = 32 * cls + half
-                    eng.dma_start(out=xh[bh][q0:q0 + 31:2, :, :], in_=src[cls, half])
-
+        fv_raw = []
+        wa_raw = []
+        for g in range(NG):
+            r = fvraw_pool.tile([P, 4608], BF16, name="fvr", tag="fvr")
+            nc.sync.dma_start(out=r[:], in_=fv_flat[:, g * 4608:(g + 1) * 4608])
+            fv_raw.append(r)
+            sm, gp = g % 2, g // 2
+            r = wraw_pool.tile([P, 2, 1024], BF16, name="war", tag="wr")
+            nc.sync.dma_start(out=r[:], in_=wa_view[sm][:, :, gp * 1024:(gp + 1) * 1024])
+            wa_raw.append(r)
+        nc.sync.dma_start(out=ft_raw[:], in_=ft)
         wf_raw = []
+        for i in range(4):
+            r = wraw_pool.tile([P, 2, 1024], BF16, name="wfr", tag="wr")
+            nc.sync.dma_start(out=r[:], in_=wf_view[:, 2 * i:2 * i + 2, :])
+            wf_raw.append(r)
         wb_raw = []
-
-        def late_loads():
-            nc.sync.dma_start(out=ft_raw[:], in_=ft)
-            for i in range(4):
-                r = wraw_pool.tile([P, 2, 1024], BF16, name="wfr", tag="wr")
-                nc.sync.dma_start(out=r[:], in_=wf_view[:, 2 * i:2 * i + 2, :])
-                wf_raw.append(r)
-            for i in range(2):
-                r = wraw_pool.tile([P, 4, 512], BF16, name="wbr", tag="wr")
-                nc.sync.dma_start(out=r[:], in_=wb_view[:, 4 * i:4 * i + 4, :])
-                wb_raw.append(r)
-            nc.sync.dma_start(out=bfc_bc[:], in_=bfc2.partition_broadcast(P))
-            nc.sync.dma_start(out=bb_bc[:], in_=bb.partition_broadcast(P))
-
-        x_load(nc.sync, 0, (0, 1))
+        for i in range(2):
+            r = wraw_pool.tile([P, 4, 512], BF16, name="wbr", tag="wr")
+            nc.sync.dma_start(out=r[:], in_=wb_view[:, 4 * i:4 * i + 4, :])
+            wb_raw.append(r)
+        nc.sync.dma_start(out=bfc_bc[:], in_=bfc2.partition_broadcast(P))
+        nc.sync.dma_start(out=bb_bc[:], in_=bb.partition_broadcast(P))
 
         used = []
 
-        def tbank(prefix, nrot):
-            tag = "%s%d" % (prefix, len(used) % nrot)
+        def tbank(nrot):
+            tag = "tr%d" % (len(used) % nrot)
             used.append(tag)
             return psum.tile([P, 512], F32, name=tag, tag=tag)
 
-        def conv1_pass(acc, k, j, c0, n, start, stop):
+        def conv1_pass(acc, g, j, c0, n, start, stop):
             sm, em = divmod(j, 2)
             nc.tensor.matmul_mx(
                 out=acc,
-                lhsT=wac[:, sm, k, em * P:(em + 1) * P].bitcast(FP8X4),
-                lhsT_scale=was[:, sm, k, em * P:(em + 1) * P],
-                rhs=fvc[:, k, c0:c0 + n].bitcast(FP8X4),
-                rhs_scale=fvs[:, k, c0:c0 + n],
+                lhsT=wac[:, sm, g, em * P:(em + 1) * P].bitcast(FP8X4),
+                lhsT_scale=was[:, sm, g, em * P:(em + 1) * P],
+                rhs=fvc[:, g, c0:c0 + n].bitcast(FP8X4),
+                rhs_scale=fvs[:, g, c0:c0 + n],
                 start=start,
                 stop=stop,
             )
 
-        def fv_quantise(k, gt, c0, n):
-            nc.vector.quantize_mx(
-                out=fvc[:, k, c0:c0 + n].bitcast(FP8X4),
-                scales=fvs[:, k, c0:c0 + n],
-                in_=gt[:, 4 * c0:4 * (c0 + n)],
+        grps = {}
+        oddc = {}
+        last = {}
+
+        def shift_odd(g):
+            rv = fv_raw[g][:].rearrange("p (v r) -> p v r", r=18)
+            oddc[g] = odd_pool.tile([P, 256, 8], BF16, name="oddc")
+            last[g] = odd_pool.tile([P, 256, 2], BF16, name="last")
+            nc.gpsimd.tensor_scalar(
+                out=oddc[g][:], in0=rv[:, :, 9:17], scalar1=1.0, scalar2=0.0, op0=ALU.mult, op1=ALU.add
+            )
+            nc.gpsimd.tensor_scalar(
+                out=last[g][:], in0=rv[:, :, 8:18:9], scalar1=1.0, scalar2=0.0, op0=ALU.mult, op1=ALU.add
             )
 
-        def tf_chunk(k, tw):
-            fw = fv_raw[k][:].bitcast(F32)
-            for w0, nw in ((0, 2), (4, 2), (6, 2), (2, 2), (8, 1)):
-                pb = tbank("tr", 4)
-                for s in range(2):
-                    for wl in range(nw):
-                        st = s * 1152 + w0 + wl
-                        slot = s * nw + wl
-                        nc.tensor.transpose(pb[:, slot * P:(slot + 1) * P], fw[:, st:st + 1144:9], ident[:])
-                nc.scalar.copy(
-                    out=tw[:, :, w0 * P:(w0 + nw) * P],
-                    in_=pb[:, 0:2 * nw * P].rearrange("p (s r) -> p s r", s=2),
-                )
+        def tf_bank(g, a):
+            pb = tbank(4)
+            fw = fv_raw[g][:].bitcast(F32)
+            ow = oddc[g][:].rearrange("p v r -> p (v r)").bitcast(F32)
+            for s in range(2):
+                st = s * 1152 + a
+                nc.tensor.transpose(pb[:, 2 * s * P:(2 * s + 1) * P], fw[:, st:st + 1144:9], ident[:])
+                st = s * 512 + a
+                nc.tensor.transpose(pb[:, (2 * s + 1) * P:(2 * s + 2) * P], ow[:, st:st + 509:4], ident[:])
+            src = pb[:].bitcast(BF16).rearrange("p (t b h) -> p h b t", t=4, h=2)
+            if a % 2 == 0:
+                nc.scalar.copy(out=grps[g][:, 2 * a:2 * a + 2], in_=src)
+            else:
+                nc.vector.tensor_copy(out=grps[g][:, 2 * a:2 * a + 2], in_=src)
 
-        def tf_regroup(tw, gt):
-            tb = tw[:].bitcast(BF16)
-            ev = tb[:, :, 0:2050].rearrange("p s (e r) -> p s e r", e=2)
-            od = tb[:, :, 1:2559].rearrange("p s (e r) -> p s e r", e=2)
-            l8 = tb[:, :, 254:2304].rearrange("p s (e r) -> p s e r", e=2)
-            g3 = gt[:].rearrange("p (b x t) -> p b x t", x=PIX, t=4)
-            for src, x0 in ((ev, 0), (od, 1)):
-                nc.vector.tensor_copy(
-                    out=g3[:, :, x0:x0 + 8:2, :].rearrange("p b a (s e) -> p a b s e", s=2),
-                    in_=src[:, :, :, 0:1024:2].rearrange("p s e (a b) -> p a b s e", a=4),
-                )
-            nc.vector.tensor_copy(
-                out=g3[:, :, 8, :].rearrange("p b (s e) -> p b s e", s=2),
-                in_=l8[:, :, :, 770:1025:2].rearrange("p s e b -> p b s e"),
+        def tf_last(g):
+            pb = tbank(4)
+            lw = last[g][:].rearrange("p v r -> p (v r)").bitcast(F32)
+            for s in range(2):
+                nc.tensor.transpose(pb[:, s * P:(s + 1) * P], lw[:, s * P:(s + 1) * P], ident[:])
+            nc.scalar.copy(
+                out=grps[g][:, 8].bitcast(F32), in_=pb[:, 0:2 * P].rearrange("p (s b) -> p b s", s=2)
             )
 
-        def wa_unit(sm, gp, ww):
-            wag = wag_pool.tile([P, 2, 2, P, 2], F32, name="wag", tag="wag", align_bytes=64)
+        def fv_quantise(g):
+            gf = grps[g][:].rearrange("p x b t -> p (x b t)")
+            for c0, n in ((0, 512), (512, 512), (1024, 128)):
+                nc.vector.quantize_mx(
+                    out=fvc[:, g, c0:c0 + n].bitcast(FP8X4),
+                    scales=fvs[:, g, c0:c0 + n],
+                    in_=gf[:, 4 * c0:4 * (c0 + n)],
+                )
+
+        def wa_unit(i):
+            sm, gp = i % 2, i // 2
+            ww = wa_raw[i][:].bitcast(F32)
+            wag = wag_pool.tile([P, 2, 2, P, 2], F32, name="wag", align_bytes=64)
             for g2 in range(2):
-                pb = tbank("tr", 4)
+                pb = tbank(4)
                 for em in range(2):
                     for s in range(2):
                         slot = em * 2 + s
-                        if gp == 2:
-                            c0 = 256 * g2 + P * s
-                            stat = ww[:, em, c0:c0 + P]
-                        else:
-                            c0 = 2 * (2 * gp + g2) + s
-                            stat = ww[:, em, c0:c0 + 1017:8]
-                        nc.tensor.transpose(pb[:, slot * P:(slot + 1) * P], stat, ident[:])
+                        c0 = 256 * g2 + P * s
+                        nc.tensor.transpose(pb[:, slot * P:(slot + 1) * P], ww[:, em, c0:c0 + P], ident[:])
                 nc.scalar.copy(out=wag[:, g2], in_=pb[:].rearrange("p (e s q) -> p e q s", e=2, s=2))
             return wag
 
-        def wa_quantise(sm, gp, wag):
+        def wa_quantise(i, wag):
+            sm, gp = i % 2, i // 2
             nc.vector.quantize_mx(
                 out=wac[:, sm, 2 * gp:2 * gp + 2, :].rearrange("p g w -> p (g w)").bitcast(FP8X4),
                 scales=was[:, sm, 2 * gp:2 * gp + 2, :].rearrange("p g w -> p (g w)"),
                 in_=wag[:].rearrange("p g e q s -> p (g e q s)").bitcast(BF16),
             )
 
-        tw4 = tw_pool.tile([P, 2, 1280], F32, name="tw")
-        g4 = slab([P, 4608], "grp")
-        tf_chunk(4, tw4)
-        wq0 = wa_unit(0, 2, wab_raw[0][:].bitcast(F32))
-        wq1 = wa_unit(1, 2, wab_raw[1][:].bitcast(F32))
-        x_load(nc.scalar, 0, (2, 3))
-        x_load(nc.sync, 1, (0, 1))
-        tf_regroup(tw4, g4)
-        wa_quantise(0, 2, wq0)
-        fv_quantise(4, g4, 0, 512)
-        fv_quantise(4, g4, 512, 512)
-        fv_quantise(4, g4, 1024, P)
-        wa_quantise(1, 2, wq1)
+        acc0 = []
+        m0 = [(g, j) for g in range(NG) for j in range(4)]
 
-        tw5 = tw_pool.tile([P, 2, 1280], F32, name="tw")
-        g5 = slab([P, 4608], "grp")
-        tf_chunk(5, tw5)
-        wp = []
-        for sm in range(2):
-            t = w8_pool.tile([P, 2, 1024], F32, name="wp", tag="w8", align_bytes=64)
-            rw = wa1_raw[sm][:].bitcast(F32)
-            for em in range(2):
-                nc.scalar.copy(
-                    out=t[:, em, :].rearrange("p (c g r) -> p c g r", c=4, g=16),
-                    in_=rw[:, em, :].rearrange("p (g c r) -> p c g r", g=16, c=4),
-                )
-            wp.append(t)
-        tf_regroup(tw5, g5)
-        wq0 = wa_unit(0, 0, wp[0][:])
-        wa_quantise(0, 0, wq0)
-        fv_quantise(5, g5, 0, 512)
-        fv_quantise(5, g5, 512, 512)
-        fv_quantise(5, g5, 1024, P)
-        for sm, gp in ((1, 0), (0, 1), (1, 1)):
-            wq0 = wa_unit(sm, gp, wp[sm][:])
-            wa_quantise(sm, gp, wq0)
-        x_load(nc.scalar, 1, (2, 3))
-        late_loads()
+        def m0_pair(k):
+            for g, j in m0[2 * k:2 * k + 2]:
+                if g == 0:
+                    acc0.append(psum.tile([P, 512], F32, name="acc%d" % j, tag="acc%d" % j))
+                conv1_pass(acc0[j][:], g, j, 0, 512, g == 0, g == NG - 1)
 
-        acc0 = [psum.tile([P, 512], F32, name="acc%d" % j, tag="acc%d" % j) for j in range(4)]
-        acc1 = [psum.tile([P, 512], F32, name="c1_%d" % j, tag="tr%d" % j) for j in range(4)]
-        for k in (4, 5):
-            for j in range(4):
-                conv1_pass(acc0[j][:], k, j, 0, 512, k == 4, False)
-        for k in (4, 5):
-            for j in range(4):
-                conv1_pass(acc1[j][:], k, j, 512, 512, k == 4, False)
+        for g in range(3):
+            shift_odd(g)
+        for g in range(NG):
+            grps[g] = grp_pool.tile([P, PIX, P, 4], BF16, name="grp", align_bytes=64)
+            tf_bank(g, 0)
+            tf_bank(g, 1)
+            tf_bank(g, 2)
+            if g >= 2:
+                m0_pair(2 * (g - 2))
+            tf_bank(g, 3)
+            tf_last(g)
+            wag = wa_unit(g)
+            if g >= 2:
+                m0_pair(2 * (g - 2) + 1)
+            if g + 3 < NG:
+                shift_odd(g + 3)
+            fv_quantise(g)
+            wa_quantise(g, wag)
 
-        ga = [slab([P, 4608], "grp") for g in range(4)]
-
-        def a_regroup(g, bh):
-            nc.vector.tensor_copy(
-                out=ga[g][:, bh * 2304:(bh + 1) * 2304].rearrange("p (b x j) -> p b x j", x=PIX, j=4),
-                in_=xh[bh][:, :, 36 * g:36 * g + 36].rearrange("p b (j x) -> p b x j", j=4),
-            )
-
-        a_regroup(0, 0)
-        a_regroup(1, 0)
-        fv_quantise(0, ga[0], 0, 512)
-        a_regroup(2, 0)
-        fv_quantise(1, ga[1], 0, 512)
-        a_regroup(3, 0)
-        fv_quantise(2, ga[2], 0, 512)
-        fv_quantise(3, ga[3], 0, 512)
+        m0_pair(8)
+        m0_pair(9)
+        pb = tbank(3)
+        fw = ft_raw[:].bitcast(F32)
         for k in range(4):
-            for j in range(4):
-                conv1_pass(acc0[j][:], k, j, 0, 512, False, k == 3)
-
-        hp = slab([P, 4, PIX, P], "hp")
-        hg = slab([P, COLS, 4], "hg")
-
-        def h_piece(eng, dst, src, j):
-            if eng == "s":
-                nc.scalar.activation(out=dst, in_=src, func=ACT.Relu, bias=ba_f[:, j:j + 1], scale=1.0)
-            else:
-                nc.vector.tensor_scalar(
-                    out=dst, in0=src, scalar1=ba_f[:, j:j + 1], scalar2=0.0, op0=ALU.add, op1=ALU.max
-                )
-
-        def h_out(eng, bank, j, n0, n):
-            head = (PIX - n0 % PIX) % PIX
-            nb = (n - head) // PIX
-            b0 = (n0 + head) // PIX
-            tail = n - head - PIX * nb
-            h_piece(
-                eng,
-                hp[:, j, :, b0:b0 + nb],
-                bank[:, head:head + PIX * nb].rearrange("p (b x) -> p x b", x=PIX),
-                j,
-            )
-            if head:
-                h_piece(eng, hp[:, j, PIX - head:PIX, b0 - 1], bank[:, 0:head], j)
-            if tail:
-                h_piece(eng, hp[:, j, 0:tail, b0 + nb], bank[:, n - tail:n], j)
-
-        for j in range(4):
-            h_out("s", acc0[j][:], j, 0, 512)
-
-        wfT = [w8_pool.tile([P, 2, C], F32, name="wfT", tag="w8", align_bytes=64) for h in range(2)]
-        wbg = w8_pool.tile([P, C, 2], F32, name="wbg", tag="w8", align_bytes=64)
-
-        def ft_unit():
-            pb = tbank("acc", 3)
-            fw = ft_raw[:].bitcast(F32)
-            for k in range(4):
-                nc.tensor.transpose(pb[:, k * P:(k + 1) * P], fw[:, k * P:(k + 1) * P], ident[:])
-            nc.scalar.copy(out=ftT[:].rearrange("p k b -> p (k b)"), in_=pb[:])
+            nc.tensor.transpose(pb[:, k * P:(k + 1) * P], fw[:, k * P:(k + 1) * P], ident[:])
+        nc.scalar.copy(out=ftT[:].rearrange("p k b -> p (k b)"), in_=pb[:])
+        ft_e = ftT[:].bitcast(BF16).rearrange("p k (b e) -> p k b e", e=2)
+        wf_e = wfT[:].bitcast(BF16).rearrange("p k (o e) -> p k o e", e=2)
 
         def wf_unit(i):
             ww = wf_raw[i][:].bitcast(F32)
             for h in range(2):
-                pb = tbank("acc", 3)
+                pb = tbank(3)
                 for kl in range(2):
                     for tl in range(2):
                         slot = kl * 2 + tl
                         k = 2 * h + kl
                         nc.tensor.transpose(pb[:, slot * P:(slot + 1) * P], ww[:, tl, k * P:(k + 1) * P], ident[:])
                 nc.scalar.copy(
-                    out=wfT[h][:, :, i * 256:(i + 1) * 256],
+                    out=wfT[:, 2 * h:2 * h + 2, i * 256:(i + 1) * 256],
                     in_=pb[:].rearrange("p (k o) -> p k o", k=2),
                 )
 
-        def fc(half, tag):
-            acc = psum.tile([P, 512], F32, name="fc", tag=tag)
+        def fc(half):
+            acc = psum.tile([P, 512], F32, name="fc", tag="tr3")
             cols = slice(half * 512, (half + 1) * 512)
-            ft_e = ftT[:].bitcast(BF16).rearrange("p k (b e) -> p k b e", e=2)
             for idx in range(8):
                 k, e = divmod(idx, 2)
-                wf_e = wfT[k // 2][:].bitcast(BF16).rearrange("p k (o e) -> p k o e", e=2)
                 nc.tensor.matmul(
-                    out=acc[:], lhsT=ft_e[:, k, :, e], rhs=wf_e[:, k % 2, cols, e], start=idx == 0, stop=idx == 7
+                    out=acc[:], lhsT=ft_e[:, k, :, e], rhs=wf_e[:, k, cols, e], start=idx == 0, stop=idx == 7
                 )
-            return acc
-
-        def fc_add(half, acc):
-            cols = slice(half * 512, (half + 1) * 512)
             nc.vector.tensor_tensor(out=ft2[:, cols], in0=acc[:], in1=bfc_bc[:, cols], op=ALU.add)
 
         def wb_unit(i):
             ww = wb_raw[i][:].bitcast(F32)
             for h in range(2):
-                pb = tbank("acc", 3)
+                pb = tbank(3)
                 for tl in range(2):
                     for sm in range(2):
                         slot = tl * 2 + sm
@@ -348,66 +262,43 @@ def tile_joint_module_pb_kernel(tc, fv, ft, Wa, ba, Wb, bb, Wfc2, bfc2, out):
                     out=wbg[:, o0:o0 + 256, :].rearrange("p (t o) s -> p t o s", t=2),
                     in_=pb[:].rearrange("p (t s o) -> p t o s", t=2, s=2),
                 )
-
-        def wb_quantise(i):
             nc.vector.quantize_mx(
                 out=wbc[:, i * 512:(i + 1) * 512].bitcast(FP8X4),
                 scales=wbs[:, i * 512:(i + 1) * 512],
                 in_=wbg[:, i * 512:(i + 1) * 512, :].rearrange("p o s -> p (o s)").bitcast(BF16),
             )
 
-        def c1_passes(k):
-            for j in range(4):
-                conv1_pass(acc1[j][:], k, j, 512, 512, False, k == 3)
-
-        def a_quantise_rest(g):
-            fv_quantise(g, ga[g], 512, 512)
-            fv_quantise(g, ga[g], 1024, P)
-
-        a_regroup(0, 1)
-        a_regroup(1, 1)
-        a_quantise_rest(0)
-        ft_unit()
         wf_unit(0)
-        c1_passes(0)
-        a_regroup(2, 1)
-        a_quantise_rest(1)
         wf_unit(1)
         wf_unit(2)
-        c1_passes(1)
-        a_regroup(3, 1)
-        a_quantise_rest(2)
+        fc(0)
         wf_unit(3)
         wb_unit(0)
-        c1_passes(2)
-        wb_quantise(0)
-        a_quantise_rest(3)
+        fc(1)
         wb_unit(1)
-        c1_passes(3)
-        wb_quantise(1)
 
-        h_out("s", acc1[0][:], 0, 512, 512)
-        h_out("v", acc1[2][:], 2, 512, 512)
-        h_out("s", acc1[1][:], 1, 512, 512)
-        h_out("v", acc1[3][:], 3, 512, 512)
+        acc1 = [psum.tile([P, 512], F32, name="c1_%d" % j, tag="tr%d" % j) for j in range(4)]
+        for g in range(NG - 1):
+            for j in range(4):
+                conv1_pass(acc1[j][:], g, j, 512, 512, g == 0, False)
+        m0_pair(10)
+        m0_pair(11)
 
-        acc2 = psum.tile([P, 512], F32, name="c2", tag="acc0")
-        order = (4, 5, 0, 1, 2, 3)
-        for j in range(4):
-            for k in order:
-                conv1_pass(acc2[:, j * P:(j + 1) * P], k, j, 1024, P, k == 4, k == 3)
-        h_out("s", acc2[:, 0:P], 0, 1024, P)
-        h_out("v", acc2[:, 2 * P:3 * P], 2, 1024, P)
-        h_out("s", acc2[:, P:2 * P], 1, 1024, P)
-        h_out("v", acc2[:, 3 * P:4 * P], 3, 1024, P)
-        fc0 = fc(0, "acc3")
-
-        hpf = hp[:].rearrange("p t x b -> p t (x b)")
+        def h_out(eng, bank, j, c0, n):
+            if eng == "s":
+                nc.scalar.activation(
+                    out=hp[:, j, c0:c0 + n], in_=bank, func=ACT.Relu, bias=ba_f[:, j:j + 1], scale=1.0
+                )
+            else:
+                nc.vector.tensor_scalar(
+                    out=hp[:, j, c0:c0 + n], in0=bank, scalar1=ba_f[:, j:j + 1], scalar2=0.0,
+                    op0=ALU.add, op1=ALU.max,
+                )
 
         def h_regroup(c0, n):
             nc.vector.tensor_copy(
                 out=hg[:, c0:c0 + n, :].rearrange("p (c i) t -> p c t i", i=4),
-                in_=hpf[:, :, c0:c0 + n].rearrange("p t (c i) -> p c t i", i=4),
+                in_=hp[:, :, c0:c0 + n].rearrange("p t (c i) -> p c t i", i=4),
             )
 
         def h_quantise(c0, n):
@@ -417,19 +308,35 @@ def tile_joint_module_pb_kernel(tc, fv, ft, Wa, ba, Wb, bb, Wfc2, bfc2, out):
                 in_=hg[:, c0:c0 + n, :].rearrange("p c t -> p (c t)"),
             )
 
+        h_out("s", acc0[0][:], 0, 0, 512)
+        h_out("v", acc0[2][:], 2, 0, 512)
+        h_out("s", acc0[1][:], 1, 0, 512)
+        h_out("v", acc0[3][:], 3, 0, 512)
+        for j in range(4):
+            conv1_pass(acc1[j][:], NG - 1, j, 512, 512, False, True)
         h_regroup(0, 256)
         h_regroup(256, 256)
         h_quantise(0, 256)
-        h_regroup(512, 256)
         h_quantise(256, 256)
+        h_out("s", acc1[0][:], 0, 512, 512)
+        h_out("s", acc1[1][:], 1, 512, 512)
+        h_out("v", acc1[3][:], 3, 512, 512)
+        h_out("s", acc1[2][:], 2, 512, 512)
+
+        acc2 = psum.tile([P, 512], F32, name="c2", tag="acc0")
+        for j in range(4):
+            for g in range(NG):
+                conv1_pass(acc2[:, j * P:(j + 1) * P], g, j, 1024, P, g == 0, g == NG - 1)
+        h_regroup(512, 256)
         h_regroup(768, 256)
         h_quantise(512, 256)
-        h_regroup(1024, P)
         h_quantise(768, 256)
+        for j in range(4):
+            h_out("s", acc2[:, j * P:(j + 1) * P], j, 1024, P)
+        h_regroup(1024, P)
         h_quantise(1024, P)
-        fc_add(0, fc0)
 
-        gacc = [psum.tile([P, 512], F32, name="g%d" % i, tag="tr%d" % i) for i in range(2)]
+        gacc = [psum.tile([P, 512], F32, name="g%d" % i, tag="acc%d" % (i + 1)) for i in range(2)]
         for x in range(PIX):
             for half in range(2):
                 nc.tensor.matmul_mx(
@@ -441,19 +348,13 @@ def tile_joint_module_pb_kernel(tc, fv, ft, Wa, ba, Wb, bb, Wfc2, bfc2, out):
                     start=x == 0,
                     stop=x == PIX - 1,
                 )
-        fc1 = fc(1, "acc1")
 
-        z = wag_pool.tile([P, C], F32, name="z", tag="wag", align_bytes=64)
         for half in range(2):
             cols = slice(half * 512, (half + 1) * 512)
             nc.vector.scalar_tensor_tensor(
                 out=z[:, cols], in0=gacc[half][:], scalar=1.0 / PIX, in1=bb_bc[:, cols], op0=ALU.mult, op1=ALU.add
             )
             nc.scalar.activation(out=z[:, cols], in_=z[:, cols], func=ACT.Sigmoid)
-        for half in range(2):
-            cols = slice(half * 512, (half + 1) * 512)
-            if half == 1:
-                fc_add(1, fc1)
             nc.vector.scalar_tensor_tensor(
                 out=z[:, cols], in0=z[:, cols], scalar=1.0, in1=ft2[:, cols], op0=ALU.add, op1=ALU.mult
             )

@@ -123,12 +123,8 @@ def tile_joint_module_pb_kernel(tc, fv, ft, Wa, ba, Wb, bb, Wfc2, bfc2, out):
             rv = fv_raw[g][:].rearrange("p (v r) -> p v r", r=18)
             oddc[g] = odd_pool.tile([P, 256, 8], BF16, name="oddc")
             last[g] = odd_pool.tile([P, 256, 2], BF16, name="last")
-            nc.gpsimd.tensor_scalar(
-                out=oddc[g][:], in0=rv[:, :, 9:17], scalar1=1.0, scalar2=0.0, op0=ALU.mult, op1=ALU.add
-            )
-            nc.gpsimd.tensor_scalar(
-                out=last[g][:], in0=rv[:, :, 8:18:9], scalar1=1.0, scalar2=0.0, op0=ALU.mult, op1=ALU.add
-            )
+            nc.vector.tensor_copy(out=oddc[g][:], in_=rv[:, :, 9:17])
+            nc.vector.tensor_copy(out=last[g][:], in_=rv[:, :, 8:18:9])
 
         def tf_bank(g, a):
             pb = tbank(4)
@@ -140,7 +136,7 @@ def tile_joint_module_pb_kernel(tc, fv, ft, Wa, ba, Wb, bb, Wfc2, bfc2, out):
                 st = s * 512 + a
                 nc.tensor.transpose(pb[:, (2 * s + 1) * P:(2 * s + 2) * P], ow[:, st:st + 509:4], ident[:])
             src = pb[:].bitcast(BF16).rearrange("p (t b h) -> p h b t", t=4, h=2)
-            if a % 2 == 0:
+            if a < 3:
                 nc.scalar.copy(out=grps[g][:, 2 * a:2 * a + 2], in_=src)
             else:
                 nc.vector.tensor_copy(out=grps[g][:, 2 * a:2 * a + 2], in_=src)
@@ -194,8 +190,7 @@ def tile_joint_module_pb_kernel(tc, fv, ft, Wa, ba, Wb, bb, Wfc2, bfc2, out):
                     acc0.append(psum.tile([P, 512], F32, name="acc%d" % j, tag="acc%d" % j))
                 conv1_pass(acc0[j][:], g, j, 0, 512, g == 0, g == NG - 1)
 
-        for g in range(3):
-            shift_odd(g)
+        shift_odd(0)
         for g in range(NG):
             grps[g] = grp_pool.tile([P, PIX, P, 4], BF16, name="grp", align_bytes=64)
             tf_bank(g, 0)
@@ -208,8 +203,8 @@ def tile_joint_module_pb_kernel(tc, fv, ft, Wa, ba, Wb, bb, Wfc2, bfc2, out):
             wag = wa_unit(g)
             if g >= 2:
                 m0_pair(2 * (g - 2) + 1)
-            if g + 3 < NG:
-                shift_odd(g + 3)
+            if g + 1 < NG:
+                shift_odd(g + 1)
             fv_quantise(g)
             wa_quantise(g, wag)
 

@@ -72,22 +72,23 @@ def tile_joint_module_pb_kernel(tc, fv, ft, Wa, ba, Wb, bb, Wfc2, bfc2, out):
         wa_view = Wa.rearrange("(s p e) c -> s p e c", s=2, e=2)
         wf_view = Wfc2.rearrange("(t p) c -> p t c", p=P)
         wb_view = Wb.rearrange("(t p) m -> p t m", p=P)
-        fv_raw = []
-        wa_raw = []
-        for g in range(NG):
-            r = fvraw_pool.tile([P, 4608], BF16, name="fvr", tag="fvr")
-            nc.sync.dma_start(out=r[:], in_=fv_flat[:, g * 4608:(g + 1) * 4608])
-            fv_raw.append(r)
-            sm, gp = g % 2, g // 2
-            r = wraw_pool.tile([P, 2, 1024], BF16, name="war", tag="wr")
-            nc.sync.dma_start(out=r[:], in_=wa_view[sm][:, :, gp * 1024:(gp + 1) * 1024])
-            wa_raw.append(r)
         nc.sync.dma_start(out=ft_raw[:], in_=ft)
         wf_raw = []
         for i in range(4):
             r = wraw_pool.tile([P, 2, 1024], BF16, name="wfr", tag="wr")
             nc.sync.dma_start(out=r[:], in_=wf_view[:, 2 * i:2 * i + 2, :])
             wf_raw.append(r)
+        fv_raw = []
+        wa_raw = []
+        for gp in range(NG // 2):
+            for sm in range(2):
+                r = wraw_pool.tile([P, 2, 1024], BF16, name="war", tag="wr")
+                nc.sync.dma_start(out=r[:], in_=wa_view[sm][:, :, gp * 1024:(gp + 1) * 1024])
+                wa_raw.append(r)
+            for g in (2 * gp, 2 * gp + 1):
+                r = fvraw_pool.tile([P, 4608], BF16, name="fvr", tag="fvr")
+                nc.sync.dma_start(out=r[:], in_=fv_flat[:, g * 4608:(g + 1) * 4608])
+                fv_raw.append(r)
         wb_raw = []
         for i in range(2):
             r = wraw_pool.tile([P, 4, 512], BF16, name="wbr", tag="wr")
@@ -190,27 +191,7 @@ def tile_joint_module_pb_kernel(tc, fv, ft, Wa, ba, Wb, bb, Wfc2, bfc2, out):
                     acc0.append(psum.tile([P, 512], F32, name="acc%d" % j, tag="acc%d" % j))
                 conv1_pass(acc0[j][:], g, j, 0, 512, g == 0, g == NG - 1)
 
-        shift_odd(0)
-        for g in range(NG):
-            grps[g] = grp_pool.tile([P, PIX, P, 4], BF16, name="grp", align_bytes=64)
-            tf_bank(g, 0)
-            tf_bank(g, 1)
-            tf_bank(g, 2)
-            if g >= 2:
-                m0_pair(2 * (g - 2))
-            tf_bank(g, 3)
-            tf_last(g)
-            wag = wa_unit(g)
-            if g >= 2:
-                m0_pair(2 * (g - 2) + 1)
-            if g + 1 < NG:
-                shift_odd(g + 1)
-            fv_quantise(g)
-            wa_quantise(g, wag)
-
-        m0_pair(8)
-        m0_pair(9)
-        pb = tbank(3)
+        pb = tbank(4)
         fw = ft_raw[:].bitcast(F32)
         for k in range(4):
             nc.tensor.transpose(pb[:, k * P:(k + 1) * P], fw[:, k * P:(k + 1) * P], ident[:])
@@ -221,31 +202,64 @@ def tile_joint_module_pb_kernel(tc, fv, ft, Wa, ba, Wb, bb, Wfc2, bfc2, out):
         def wf_unit(i):
             ww = wf_raw[i][:].bitcast(F32)
             for h in range(2):
-                pb = tbank(3)
+                pb = tbank(4)
                 for kl in range(2):
                     for tl in range(2):
                         slot = kl * 2 + tl
                         k = 2 * h + kl
                         nc.tensor.transpose(pb[:, slot * P:(slot + 1) * P], ww[:, tl, k * P:(k + 1) * P], ident[:])
-                nc.scalar.copy(
-                    out=wfT[:, 2 * h:2 * h + 2, i * 256:(i + 1) * 256],
-                    in_=pb[:].rearrange("p (k o) -> p k o", k=2),
-                )
+                dst = wfT[:, 2 * h:2 * h + 2, i * 256:(i + 1) * 256]
+                src = pb[:].rearrange("p (k o) -> p k o", k=2)
+                if h == 0:
+                    nc.scalar.copy(out=dst, in_=src)
+                else:
+                    nc.vector.tensor_copy(out=dst, in_=src)
 
-        def fc(half):
-            acc = psum.tile([P, 512], F32, name="fc", tag="tr3")
-            cols = slice(half * 512, (half + 1) * 512)
+        def fc(i):
+            acc = psum.tile([P, 512], F32, name="fc", tag="acc%d" % i)
+            cols = slice(i * 256, (i + 1) * 256)
             for idx in range(8):
                 k, e = divmod(idx, 2)
                 nc.tensor.matmul(
-                    out=acc[:], lhsT=ft_e[:, k, :, e], rhs=wf_e[:, k, cols, e], start=idx == 0, stop=idx == 7
+                    out=acc[:, 0:256], lhsT=ft_e[:, k, :, e], rhs=wf_e[:, k, cols, e], start=idx == 0, stop=idx == 7
                 )
-            nc.vector.tensor_tensor(out=ft2[:, cols], in0=acc[:], in1=bfc_bc[:, cols], op=ALU.add)
+            nc.vector.tensor_copy(out=ft2[:, cols], in_=acc[:, 0:256])
+
+        wf_unit(0)
+        for i in range(1, 4):
+            wf_unit(i)
+            fc(i - 1)
+        wags = {}
+        wags[0] = wa_unit(0)
+        fc(3)
+        wags[1] = wa_unit(1)
+        wa_quantise(0, wags[0])
+        wa_quantise(1, wags[1])
+
+        shift_odd(0)
+        for g in range(NG):
+            grps[g] = grp_pool.tile([P, PIX, P, 4], BF16, name="grp", align_bytes=64)
+            tf_bank(g, 0)
+            tf_bank(g, 1)
+            if g >= 1:
+                m0_pair(2 * (g - 1))
+            tf_bank(g, 2)
+            tf_bank(g, 3)
+            tf_last(g)
+            if 2 <= g + 1 < NG:
+                wags[g + 1] = wa_unit(g + 1)
+            if g >= 1:
+                m0_pair(2 * (g - 1) + 1)
+            if g + 1 < NG:
+                shift_odd(g + 1)
+            fv_quantise(g)
+            if g + 1 in wags:
+                wa_quantise(g + 1, wags[g + 1])
 
         def wb_unit(i):
             ww = wb_raw[i][:].bitcast(F32)
             for h in range(2):
-                pb = tbank(3)
+                pb = tbank(4)
                 for tl in range(2):
                     for sm in range(2):
                         slot = tl * 2 + sm
@@ -263,13 +277,7 @@ def tile_joint_module_pb_kernel(tc, fv, ft, Wa, ba, Wb, bb, Wfc2, bfc2, out):
                 in_=wbg[:, i * 512:(i + 1) * 512, :].rearrange("p o s -> p (o s)").bitcast(BF16),
             )
 
-        wf_unit(0)
-        wf_unit(1)
-        wf_unit(2)
-        fc(0)
-        wf_unit(3)
         wb_unit(0)
-        fc(1)
         wb_unit(1)
 
         acc1 = [psum.tile([P, 512], F32, name="c1_%d" % j, tag="tr%d" % j) for j in range(4)]
@@ -332,25 +340,36 @@ def tile_joint_module_pb_kernel(tc, fv, ft, Wa, ba, Wb, bb, Wfc2, bfc2, out):
         h_quantise(1024, P)
 
         gacc = [psum.tile([P, 512], F32, name="g%d" % i, tag="acc%d" % (i + 1)) for i in range(2)]
-        for x in range(PIX):
-            for half in range(2):
-                nc.tensor.matmul_mx(
-                    out=gacc[half][:],
-                    lhsT=hc[:, x * P:(x + 1) * P].bitcast(FP8X4),
-                    lhsT_scale=hs[:, x * P:(x + 1) * P],
-                    rhs=wbc[:, half * 512:(half + 1) * 512].bitcast(FP8X4),
-                    rhs_scale=wbs[:, half * 512:(half + 1) * 512],
-                    start=x == 0,
-                    stop=x == PIX - 1,
-                )
+        order = [(half, x) for half in range(2) for x in range(4)]
+        order += [(half, x) for half in range(2) for x in range(4, PIX)]
+        for half, x in order:
+            nc.tensor.matmul_mx(
+                out=gacc[half][:],
+                lhsT=hc[:, x * P:(x + 1) * P].bitcast(FP8X4),
+                lhsT_scale=hs[:, x * P:(x + 1) * P],
+                rhs=wbc[:, half * 512:(half + 1) * 512].bitcast(FP8X4),
+                rhs_scale=wbs[:, half * 512:(half + 1) * 512],
+                start=x == 0,
+                stop=x == PIX - 1,
+            )
+        nc.vector.tensor_tensor(out=ft2[:], in0=ft2[:], in1=bfc_bc[:], op=ALU.add)
 
-        for half in range(2):
-            cols = slice(half * 512, (half + 1) * 512)
+        def gate_in(half, c0, n):
             nc.vector.scalar_tensor_tensor(
-                out=z[:, cols], in0=gacc[half][:], scalar=1.0 / PIX, in1=bb_bc[:, cols], op0=ALU.mult, op1=ALU.add
+                out=z[:, c0:c0 + n], in0=gacc[half][:, c0 - half * 512:c0 - half * 512 + n], scalar=1.0 / PIX,
+                in1=bb_bc[:, c0:c0 + n], op0=ALU.mult, op1=ALU.add,
             )
-            nc.scalar.activation(out=z[:, cols], in_=z[:, cols], func=ACT.Sigmoid)
+            nc.scalar.activation(out=z[:, c0:c0 + n], in_=z[:, c0:c0 + n], func=ACT.Sigmoid)
+
+        def gate_out(c0, n):
             nc.vector.scalar_tensor_tensor(
-                out=z[:, cols], in0=z[:, cols], scalar=1.0, in1=ft2[:, cols], op0=ALU.add, op1=ALU.mult
+                out=z[:, c0:c0 + n], in0=z[:, c0:c0 + n], scalar=1.0, in1=ft2[:, c0:c0 + n], op0=ALU.add, op1=ALU.mult
             )
-            nc.sync.dma_start(out=out[:, cols], in_=z[:, cols])
+            nc.sync.dma_start(out=out[:, c0:c0 + n], in_=z[:, c0:c0 + n])
+
+        gate_in(0, 0, 512)
+        gate_out(0, 512)
+        gate_in(1, 512, 256)
+        gate_in(1, 768, 256)
+        gate_out(512, 256)
+        gate_out(768, 256)

@@ -72,28 +72,43 @@ def tile_joint_module_pb_kernel(tc, fv, ft, Wa, ba, Wb, bb, Wfc2, bfc2, out):
         wa_view = Wa.rearrange("(s p e) c -> s p e c", s=2, e=2)
         wf_view = Wfc2.rearrange("(t p) c -> p t c", p=P)
         wb_view = Wb.rearrange("(t p) m -> p t m", p=P)
+        fv_raw = {}
+        wa_raw = {}
+        wf_raw = {}
+        wb_raw = {}
+
+        def load_fv(g, parts=1):
+            fv_raw[g] = fvraw_pool.tile([P, 4608], BF16, name="fvr", tag="fvr")
+            n = 4608 // parts
+            for i in range(parts):
+                nc.sync.dma_start(
+                    out=fv_raw[g][:, i * n:(i + 1) * n], in_=fv_flat[:, g * 4608 + i * n:g * 4608 + (i + 1) * n]
+                )
+
+        def load_wa(i):
+            sm, gp = i % 2, i // 2
+            wa_raw[i] = wraw_pool.tile([P, 2, 1024], BF16, name="war", tag="wr")
+            nc.sync.dma_start(out=wa_raw[i][:], in_=wa_view[sm][:, :, gp * 1024:(gp + 1) * 1024])
+
+        def load_wf(i):
+            wf_raw[i] = wraw_pool.tile([P, 2, 1024], BF16, name="wfr", tag="wr")
+            nc.sync.dma_start(out=wf_raw[i][:], in_=wf_view[:, 2 * i:2 * i + 2, :])
+
+        def load_wb(i):
+            wb_raw[i] = wraw_pool.tile([P, 4, 512], BF16, name="wbr", tag="wr")
+            nc.sync.dma_start(out=wb_raw[i][:], in_=wb_view[:, 4 * i:4 * i + 4, :])
+
+        load_fv(0, parts=2)
+        load_wa(0)
+        load_wa(1)
+        load_fv(1)
         nc.sync.dma_start(out=ft_raw[:], in_=ft)
-        wf_raw = []
-        for i in range(4):
-            r = wraw_pool.tile([P, 2, 1024], BF16, name="wfr", tag="wr")
-            nc.sync.dma_start(out=r[:], in_=wf_view[:, 2 * i:2 * i + 2, :])
-            wf_raw.append(r)
-        fv_raw = []
-        wa_raw = []
-        for gp in range(NG // 2):
-            for sm in range(2):
-                r = wraw_pool.tile([P, 2, 1024], BF16, name="war", tag="wr")
-                nc.sync.dma_start(out=r[:], in_=wa_view[sm][:, :, gp * 1024:(gp + 1) * 1024])
-                wa_raw.append(r)
-            for g in (2 * gp, 2 * gp + 1):
-                r = fvraw_pool.tile([P, 4608], BF16, name="fvr", tag="fvr")
-                nc.sync.dma_start(out=r[:], in_=fv_flat[:, g * 4608:(g + 1) * 4608])
-                fv_raw.append(r)
-        wb_raw = []
-        for i in range(2):
-            r = wraw_pool.tile([P, 4, 512], BF16, name="wbr", tag="wr")
-            nc.sync.dma_start(out=r[:], in_=wb_view[:, 4 * i:4 * i + 4, :])
-            wb_raw.append(r)
+        for g in range(2, NG):
+            load_wf(g - 2)
+            load_wa(g)
+            load_fv(g)
+        load_wb(0)
+        load_wb(1)
         nc.sync.dma_start(out=bfc_bc[:], in_=bfc2.partition_broadcast(P))
         nc.sync.dma_start(out=bb_bc[:], in_=bb.partition_broadcast(P))
 
@@ -120,12 +135,15 @@ def tile_joint_module_pb_kernel(tc, fv, ft, Wa, ba, Wb, bb, Wfc2, bfc2, out):
         oddc = {}
         last = {}
 
-        def shift_odd(g):
+        def shift_odd(g, parts=1):
             rv = fv_raw[g][:].rearrange("p (v r) -> p v r", r=18)
             oddc[g] = odd_pool.tile([P, 256, 8], BF16, name="oddc")
             last[g] = odd_pool.tile([P, 256, 2], BF16, name="last")
-            nc.vector.tensor_copy(out=oddc[g][:], in_=rv[:, :, 9:17])
-            nc.vector.tensor_copy(out=last[g][:], in_=rv[:, :, 8:18:9])
+            n = 256 // parts
+            for i in range(parts):
+                v = slice(i * n, (i + 1) * n)
+                nc.vector.tensor_copy(out=oddc[g][:, v], in_=rv[:, v, 9:17])
+                nc.vector.tensor_copy(out=last[g][:, v], in_=rv[:, v, 8:18:9])
 
         def tf_bank(g, a):
             pb = tbank(4)
@@ -137,7 +155,7 @@ def tile_joint_module_pb_kernel(tc, fv, ft, Wa, ba, Wb, bb, Wfc2, bfc2, out):
                 st = s * 512 + a
                 nc.tensor.transpose(pb[:, (2 * s + 1) * P:(2 * s + 2) * P], ow[:, st:st + 509:4], ident[:])
             src = pb[:].bitcast(BF16).rearrange("p (t b h) -> p h b t", t=4, h=2)
-            if a < 3:
+            if a != 1:
                 nc.scalar.copy(out=grps[g][:, 2 * a:2 * a + 2], in_=src)
             else:
                 nc.vector.tensor_copy(out=grps[g][:, 2 * a:2 * a + 2], in_=src)
@@ -191,13 +209,15 @@ def tile_joint_module_pb_kernel(tc, fv, ft, Wa, ba, Wb, bb, Wfc2, bfc2, out):
                     acc0.append(psum.tile([P, 512], F32, name="acc%d" % j, tag="acc%d" % j))
                 conv1_pass(acc0[j][:], g, j, 0, 512, g == 0, g == NG - 1)
 
-        pb = tbank(4)
-        fw = ft_raw[:].bitcast(F32)
-        for k in range(4):
-            nc.tensor.transpose(pb[:, k * P:(k + 1) * P], fw[:, k * P:(k + 1) * P], ident[:])
-        nc.scalar.copy(out=ftT[:].rearrange("p k b -> p (k b)"), in_=pb[:])
         ft_e = ftT[:].bitcast(BF16).rearrange("p k (b e) -> p k b e", e=2)
         wf_e = wfT[:].bitcast(BF16).rearrange("p k (o e) -> p k o e", e=2)
+
+        def ft_unit():
+            pb = tbank(4)
+            fw = ft_raw[:].bitcast(F32)
+            for k in range(4):
+                nc.tensor.transpose(pb[:, k * P:(k + 1) * P], fw[:, k * P:(k + 1) * P], ident[:])
+            nc.scalar.copy(out=ftT[:].rearrange("p k b -> p (k b)"), in_=pb[:])
 
         def wf_unit(i):
             ww = wf_raw[i][:].bitcast(F32)
@@ -216,7 +236,7 @@ def tile_joint_module_pb_kernel(tc, fv, ft, Wa, ba, Wb, bb, Wfc2, bfc2, out):
                     nc.vector.tensor_copy(out=dst, in_=src)
 
         def fc(i):
-            acc = psum.tile([P, 512], F32, name="fc", tag="acc%d" % i)
+            acc = tbank(4)
             cols = slice(i * 256, (i + 1) * 256)
             for idx in range(8):
                 k, e = divmod(idx, 2)
@@ -224,37 +244,6 @@ def tile_joint_module_pb_kernel(tc, fv, ft, Wa, ba, Wb, bb, Wfc2, bfc2, out):
                     out=acc[:, 0:256], lhsT=ft_e[:, k, :, e], rhs=wf_e[:, k, cols, e], start=idx == 0, stop=idx == 7
                 )
             nc.vector.tensor_copy(out=ft2[:, cols], in_=acc[:, 0:256])
-
-        wf_unit(0)
-        for i in range(1, 4):
-            wf_unit(i)
-            fc(i - 1)
-        wags = {}
-        wags[0] = wa_unit(0)
-        fc(3)
-        wags[1] = wa_unit(1)
-        wa_quantise(0, wags[0])
-        wa_quantise(1, wags[1])
-
-        shift_odd(0)
-        for g in range(NG):
-            grps[g] = grp_pool.tile([P, PIX, P, 4], BF16, name="grp", align_bytes=64)
-            tf_bank(g, 0)
-            tf_bank(g, 1)
-            if g >= 1:
-                m0_pair(2 * (g - 1))
-            tf_bank(g, 2)
-            tf_bank(g, 3)
-            tf_last(g)
-            if 2 <= g + 1 < NG:
-                wags[g + 1] = wa_unit(g + 1)
-            if g >= 1:
-                m0_pair(2 * (g - 1) + 1)
-            if g + 1 < NG:
-                shift_odd(g + 1)
-            fv_quantise(g)
-            if g + 1 in wags:
-                wa_quantise(g + 1, wags[g + 1])
 
         def wb_unit(i):
             ww = wb_raw[i][:].bitcast(F32)
@@ -267,18 +256,53 @@ def tile_joint_module_pb_kernel(tc, fv, ft, Wa, ba, Wb, bb, Wfc2, bfc2, out):
                             pb[:, slot * P:(slot + 1) * P], ww[:, 2 * h + tl, sm * P:(sm + 1) * P], ident[:]
                         )
                 o0 = (4 * i + 2 * h) * P
-                nc.scalar.copy(
-                    out=wbg[:, o0:o0 + 256, :].rearrange("p (t o) s -> p t o s", t=2),
-                    in_=pb[:].rearrange("p (t s o) -> p t o s", t=2, s=2),
-                )
+                dst = wbg[:, o0:o0 + 256, :].rearrange("p (t o) s -> p t o s", t=2)
+                src = pb[:].rearrange("p (t s o) -> p t o s", t=2, s=2)
+                if h == 0:
+                    nc.scalar.copy(out=dst, in_=src)
+                else:
+                    nc.vector.tensor_copy(out=dst, in_=src)
+
+        def wb_quantise(i):
             nc.vector.quantize_mx(
                 out=wbc[:, i * 512:(i + 1) * 512].bitcast(FP8X4),
                 scales=wbs[:, i * 512:(i + 1) * 512],
                 in_=wbg[:, i * 512:(i + 1) * 512, :].rearrange("p o s -> p (o s)").bitcast(BF16),
             )
 
-        wb_unit(0)
-        wb_unit(1)
+        wags = {}
+
+        shift_odd(0, parts=2)
+        for g in range(NG):
+            grps[g] = grp_pool.tile([P, PIX, P, 4], BF16, name="grp", align_bytes=64)
+            tf_bank(g, 0)
+            tf_bank(g, 1)
+            if g >= 2:
+                fc(g - 2)
+            tf_bank(g, 2)
+            tf_bank(g, 3)
+            tf_last(g)
+            if g >= 1:
+                m0_pair(2 * (g - 1))
+            made = [0, 1] if g == 0 else [g + 1] if g + 1 < NG else []
+            for i in made:
+                wags[i] = wa_unit(i)
+            if g == 1:
+                ft_unit()
+            if 1 <= g < 5:
+                wf_unit(g - 1)
+            if g == 5:
+                wb_unit(0)
+                wb_unit(1)
+            if g >= 1:
+                m0_pair(2 * (g - 1) + 1)
+            if g + 1 < NG:
+                shift_odd(g + 1)
+            fv_quantise(g)
+            for i in made:
+                wa_quantise(i, wags[i])
+        wb_quantise(0)
+        wb_quantise(1)
 
         acc1 = [psum.tile([P, 512], F32, name="c1_%d" % j, tag="tr%d" % j) for j in range(4)]
         for g in range(NG - 1):

@@ -18,22 +18,19 @@ NG = C3 // 512
 COLS = PIX * B
 FLOPS = 2 * (CH * C3 * COLS + C * CH * COLS + B * C * C)
 
-MANUAL = True
-
 
 def tile_joint_module_pb_kernel(tc, fv, ft, Wa, ba, Wb, bb, Wfc2, bfc2, out):
     nc = tc.nc
     with ExitStack() as ctx:
         const = ctx.enter_context(tc.tile_pool(name="const", bufs=1))
         keep = ctx.enter_context(tc.tile_pool(name="keep", bufs=1))
-        fvraw_pool = ctx.enter_context(tc.tile_pool(name="fvraw", bufs=4))
-        wraw_pool = ctx.enter_context(tc.tile_pool(name="wraw", bufs=6))
-        odd_pool = ctx.enter_context(tc.tile_pool(name="odd", bufs=3))
-        grp_pool = ctx.enter_context(tc.tile_pool(name="grp", bufs=2))
+        fvraw_pool = ctx.enter_context(tc.tile_pool(name="fvraw", bufs=6))
+        wraw_pool = ctx.enter_context(tc.tile_pool(name="wraw", bufs=5))
+        odd_pool = ctx.enter_context(tc.tile_pool(name="odd", bufs=6))
+        grp_pool = ctx.enter_context(tc.tile_pool(name="grp", bufs=3))
         wag_pool = ctx.enter_context(tc.tile_pool(name="wag", bufs=2))
         psum = ctx.enter_context(tc.psum_pool(name="ps", bufs=1))
-        if MANUAL:
-            ctx.enter_context(tc.manual_schedule())
+        ctx.enter_context(tc.manual_schedule())
 
         ident = const.tile([P, P], F32, name="ident")
         make_identity(nc, ident[:])
@@ -47,20 +44,16 @@ def tile_joint_module_pb_kernel(tc, fv, ft, Wa, ba, Wb, bb, Wfc2, bfc2, out):
         warm_out = const.tile([P, 1], F32, name="warm_out")
         nc.vector.memset(warm_in[:], 0.0)
         nc.scalar.activation(out=warm_out[:], in_=warm_in[:], func=ACT.Sigmoid)
-        nc.vector.tensor_copy(out=ba_f[:], in_=ba_raw[:])
 
         fvc = keep.tile([P, NG, COLS], U32, name="fvc", align_bytes=64)
         fvs = keep.tile([P, NG, COLS], U8, name="fvs", align_bytes=64)
         wac = keep.tile([P, 2, NG, 256], U32, name="wac", align_bytes=64)
         was = keep.tile([P, 2, NG, 256], U8, name="was", align_bytes=64)
-        wbg = keep.tile([P, C, 2], F32, name="wbg", align_bytes=64)
         wbc = keep.tile([P, C], U32, name="wbc", align_bytes=64)
         wbs = keep.tile([P, C], U8, name="wbs", align_bytes=64)
         wfT = keep.tile([P, 4, C], F32, name="wfT")
         ftT = keep.tile([P, 4, P], F32, name="ftT")
         ft2 = keep.tile([P, C], F32, name="ft2")
-        hp = keep.tile([P, 4, COLS], BF16, name="hp")
-        hg = keep.tile([P, COLS, 4], BF16, name="hg", align_bytes=64)
         hc = keep.tile([P, COLS], U32, name="hc", align_bytes=64)
         hs = keep.tile([P, COLS], U8, name="hs", align_bytes=64)
         z = keep.tile([P, C], F32, name="z")
@@ -102,11 +95,13 @@ def tile_joint_module_pb_kernel(tc, fv, ft, Wa, ba, Wb, bb, Wfc2, bfc2, out):
         load_wa(0)
         load_wa(1)
         load_fv(1)
+        load_wa(2)
         nc.sync.dma_start(out=ft_raw[:], in_=ft)
         for g in range(2, NG):
             load_wf(g - 2)
-            load_wa(g)
             load_fv(g)
+            if g + 1 < NG:
+                load_wa(g + 1)
         load_wb(0)
         load_wb(1)
         nc.sync.dma_start(out=bfc_bc[:], in_=bfc2.partition_broadcast(P))
@@ -114,12 +109,18 @@ def tile_joint_module_pb_kernel(tc, fv, ft, Wa, ba, Wb, bb, Wfc2, bfc2, out):
 
         used = []
 
-        def tbank(nrot):
-            tag = "tr%d" % (len(used) % nrot)
+        def tbank():
+            tag = "tr%d" % (len(used) % 4)
             used.append(tag)
             return psum.tile([P, 512], F32, name=tag, tag=tag)
 
-        def conv1_pass(acc, g, j, c0, n, start, stop):
+        def copy(eng, dst, src):
+            if eng == "s":
+                nc.scalar.copy(out=dst, in_=src)
+            else:
+                nc.vector.tensor_copy(out=dst, in_=src)
+
+        def conv1_pass(acc, g, j, c0, n):
             sm, em = divmod(j, 2)
             nc.tensor.matmul_mx(
                 out=acc,
@@ -127,11 +128,10 @@ def tile_joint_module_pb_kernel(tc, fv, ft, Wa, ba, Wb, bb, Wfc2, bfc2, out):
                 lhsT_scale=was[:, sm, g, em * P:(em + 1) * P],
                 rhs=fvc[:, g, c0:c0 + n].bitcast(FP8X4),
                 rhs_scale=fvs[:, g, c0:c0 + n],
-                start=start,
-                stop=stop,
+                start=g == 0,
+                stop=g == NG - 1,
             )
 
-        grps = {}
         oddc = {}
         last = {}
 
@@ -145,8 +145,8 @@ def tile_joint_module_pb_kernel(tc, fv, ft, Wa, ba, Wb, bb, Wfc2, bfc2, out):
                 nc.vector.tensor_copy(out=oddc[g][:, v], in_=rv[:, v, 9:17])
                 nc.vector.tensor_copy(out=last[g][:, v], in_=rv[:, v, 8:18:9])
 
-        def tf_bank(g, a):
-            pb = tbank(4)
+        def tf_bank(g, a, dst, eng):
+            pb = tbank()
             fw = fv_raw[g][:].bitcast(F32)
             ow = oddc[g][:].rearrange("p v r -> p (v r)").bitcast(F32)
             for s in range(2):
@@ -154,42 +154,36 @@ def tile_joint_module_pb_kernel(tc, fv, ft, Wa, ba, Wb, bb, Wfc2, bfc2, out):
                 nc.tensor.transpose(pb[:, 2 * s * P:(2 * s + 1) * P], fw[:, st:st + 1144:9], ident[:])
                 st = s * 512 + a
                 nc.tensor.transpose(pb[:, (2 * s + 1) * P:(2 * s + 2) * P], ow[:, st:st + 509:4], ident[:])
-            src = pb[:].bitcast(BF16).rearrange("p (t b h) -> p h b t", t=4, h=2)
-            if a != 1:
-                nc.scalar.copy(out=grps[g][:, 2 * a:2 * a + 2], in_=src)
-            else:
-                nc.vector.tensor_copy(out=grps[g][:, 2 * a:2 * a + 2], in_=src)
+            copy(eng, dst, pb[:].bitcast(BF16).rearrange("p (t b h) -> p h b t", t=4, h=2))
 
-        def tf_last(g):
-            pb = tbank(4)
+        def tf_last(g, dst, eng):
+            pb = tbank()
             lw = last[g][:].rearrange("p v r -> p (v r)").bitcast(F32)
             for s in range(2):
                 nc.tensor.transpose(pb[:, s * P:(s + 1) * P], lw[:, s * P:(s + 1) * P], ident[:])
-            nc.scalar.copy(
-                out=grps[g][:, 8].bitcast(F32), in_=pb[:, 0:2 * P].rearrange("p (s b) -> p b s", s=2)
-            )
+            copy(eng, dst.bitcast(F32), pb[:, 0:2 * P].rearrange("p (s b) -> p b s", s=2))
 
-        def fv_quantise(g):
-            gf = grps[g][:].rearrange("p x b t -> p (x b t)")
-            for c0, n in ((0, 512), (512, 512), (1024, 128)):
+        def fv_quantise(g, grp, parts):
+            gf = grp[:].rearrange("p x b t -> p (x b t)")
+            first = parts[0][0]
+            for c0, n in parts:
                 nc.vector.quantize_mx(
                     out=fvc[:, g, c0:c0 + n].bitcast(FP8X4),
                     scales=fvs[:, g, c0:c0 + n],
-                    in_=gf[:, 4 * c0:4 * (c0 + n)],
+                    in_=gf[:, 4 * (c0 - first):4 * (c0 - first + n)],
                 )
 
-        def wa_unit(i):
-            sm, gp = i % 2, i // 2
+        def wa_unit(i, engs):
             ww = wa_raw[i][:].bitcast(F32)
-            wag = wag_pool.tile([P, 2, 2, P, 2], F32, name="wag", align_bytes=64)
+            wag = wag_pool.tile([P, 2, 2, P, 2], F32, name="wag", tag="wag", align_bytes=64)
             for g2 in range(2):
-                pb = tbank(4)
+                pb = tbank()
                 for em in range(2):
                     for s in range(2):
                         slot = em * 2 + s
                         c0 = 256 * g2 + P * s
                         nc.tensor.transpose(pb[:, slot * P:(slot + 1) * P], ww[:, em, c0:c0 + P], ident[:])
-                nc.scalar.copy(out=wag[:, g2], in_=pb[:].rearrange("p (e s q) -> p e q s", e=2, s=2))
+                copy(engs[g2], wag[:, g2], pb[:].rearrange("p (e s q) -> p e q s", e=2, s=2))
             return wag
 
         def wa_quantise(i, wag):
@@ -200,170 +194,172 @@ def tile_joint_module_pb_kernel(tc, fv, ft, Wa, ba, Wb, bb, Wfc2, bfc2, out):
                 in_=wag[:].rearrange("p g e q s -> p (g e q s)").bitcast(BF16),
             )
 
-        acc0 = []
-        m0 = [(g, j) for g in range(NG) for j in range(4)]
-
-        def m0_pair(k):
-            for g, j in m0[2 * k:2 * k + 2]:
-                if g == 0:
-                    acc0.append(psum.tile([P, 512], F32, name="acc%d" % j, tag="acc%d" % j))
-                conv1_pass(acc0[j][:], g, j, 0, 512, g == 0, g == NG - 1)
-
         ft_e = ftT[:].bitcast(BF16).rearrange("p k (b e) -> p k b e", e=2)
         wf_e = wfT[:].bitcast(BF16).rearrange("p k (o e) -> p k o e", e=2)
 
-        def ft_unit():
-            pb = tbank(4)
+        def ft_unit(eng):
+            pb = tbank()
             fw = ft_raw[:].bitcast(F32)
             for k in range(4):
                 nc.tensor.transpose(pb[:, k * P:(k + 1) * P], fw[:, k * P:(k + 1) * P], ident[:])
-            nc.scalar.copy(out=ftT[:].rearrange("p k b -> p (k b)"), in_=pb[:])
+            copy(eng, ftT[:].rearrange("p k b -> p (k b)"), pb[:])
 
-        def wf_unit(i):
+        def wf_unit(i, engs):
             ww = wf_raw[i][:].bitcast(F32)
             for h in range(2):
-                pb = tbank(4)
+                pb = tbank()
                 for kl in range(2):
                     for tl in range(2):
                         slot = kl * 2 + tl
                         k = 2 * h + kl
                         nc.tensor.transpose(pb[:, slot * P:(slot + 1) * P], ww[:, tl, k * P:(k + 1) * P], ident[:])
-                dst = wfT[:, 2 * h:2 * h + 2, i * 256:(i + 1) * 256]
-                src = pb[:].rearrange("p (k o) -> p k o", k=2)
-                if h == 0:
-                    nc.scalar.copy(out=dst, in_=src)
-                else:
-                    nc.vector.tensor_copy(out=dst, in_=src)
+                copy(
+                    engs[h], wfT[:, 2 * h:2 * h + 2, i * 256:(i + 1) * 256], pb[:].rearrange("p (k o) -> p k o", k=2)
+                )
 
-        def fc(i):
-            acc = tbank(4)
+        def fc(i, eng):
+            acc = tbank()
             cols = slice(i * 256, (i + 1) * 256)
             for idx in range(8):
                 k, e = divmod(idx, 2)
                 nc.tensor.matmul(
                     out=acc[:, 0:256], lhsT=ft_e[:, k, :, e], rhs=wf_e[:, k, cols, e], start=idx == 0, stop=idx == 7
                 )
-            nc.vector.tensor_copy(out=ft2[:, cols], in_=acc[:, 0:256])
+            copy(eng, ft2[:, cols], acc[:, 0:256])
 
-        def wb_unit(i):
+        def wb_unit(i, engs):
             ww = wb_raw[i][:].bitcast(F32)
+            wbg = wag_pool.tile([P, 512, 2], F32, name="wbg", tag="wag", align_bytes=64)
             for h in range(2):
-                pb = tbank(4)
+                pb = tbank()
                 for tl in range(2):
                     for sm in range(2):
                         slot = tl * 2 + sm
                         nc.tensor.transpose(
                             pb[:, slot * P:(slot + 1) * P], ww[:, 2 * h + tl, sm * P:(sm + 1) * P], ident[:]
                         )
-                o0 = (4 * i + 2 * h) * P
-                dst = wbg[:, o0:o0 + 256, :].rearrange("p (t o) s -> p t o s", t=2)
-                src = pb[:].rearrange("p (t s o) -> p t o s", t=2, s=2)
-                if h == 0:
-                    nc.scalar.copy(out=dst, in_=src)
-                else:
-                    nc.vector.tensor_copy(out=dst, in_=src)
+                copy(
+                    engs[h],
+                    wbg[:, 256 * h:256 * (h + 1), :].rearrange("p (t o) s -> p t o s", t=2),
+                    pb[:].rearrange("p (t s o) -> p t o s", t=2, s=2),
+                )
+            return wbg
 
-        def wb_quantise(i):
+        def wb_quantise(i, wbg):
             nc.vector.quantize_mx(
                 out=wbc[:, i * 512:(i + 1) * 512].bitcast(FP8X4),
                 scales=wbs[:, i * 512:(i + 1) * 512],
-                in_=wbg[:, i * 512:(i + 1) * 512, :].rearrange("p o s -> p (o s)").bitcast(BF16),
+                in_=wbg[:].rearrange("p o s -> p (o s)").bitcast(BF16),
             )
 
-        wags = {}
-
-        shift_odd(0, parts=2)
-        for g in range(NG):
-            grps[g] = grp_pool.tile([P, PIX, P, 4], BF16, name="grp", align_bytes=64)
-            tf_bank(g, 0)
-            tf_bank(g, 1)
-            if g >= 2:
-                fc(g - 2)
-            tf_bank(g, 2)
-            tf_bank(g, 3)
-            tf_last(g)
-            if g >= 1:
-                m0_pair(2 * (g - 1))
-            made = [0, 1] if g == 0 else [g + 1] if g + 1 < NG else []
-            for i in made:
-                wags[i] = wa_unit(i)
-            if g == 1:
-                ft_unit()
-            if 1 <= g < 5:
-                wf_unit(g - 1)
-            if g == 5:
-                wb_unit(0)
-                wb_unit(1)
-            if g >= 1:
-                m0_pair(2 * (g - 1) + 1)
-            if g + 1 < NG:
-                shift_odd(g + 1)
-            fv_quantise(g)
-            for i in made:
-                wa_quantise(i, wags[i])
-        wb_quantise(0)
-        wb_quantise(1)
-
-        acc1 = [psum.tile([P, 512], F32, name="c1_%d" % j, tag="tr%d" % j) for j in range(4)]
-        for g in range(NG - 1):
-            for j in range(4):
-                conv1_pass(acc1[j][:], g, j, 512, 512, g == 0, False)
-        m0_pair(10)
-        m0_pair(11)
-
-        def h_out(eng, bank, j, c0, n):
+        def h_out(eng, hp, bank, j, n):
             if eng == "s":
-                nc.scalar.activation(
-                    out=hp[:, j, c0:c0 + n], in_=bank, func=ACT.Relu, bias=ba_f[:, j:j + 1], scale=1.0
-                )
+                nc.scalar.activation(out=hp[:, j, 0:n], in_=bank, func=ACT.Relu, bias=ba_f[:, j:j + 1], scale=1.0)
             else:
                 nc.vector.tensor_scalar(
-                    out=hp[:, j, c0:c0 + n], in0=bank, scalar1=ba_f[:, j:j + 1], scalar2=0.0,
-                    op0=ALU.add, op1=ALU.max,
+                    out=hp[:, j, 0:n], in0=bank, scalar1=ba_f[:, j:j + 1], scalar2=0.0, op0=ALU.add, op1=ALU.max
                 )
 
-        def h_regroup(c0, n):
+        def h_regroup(hp, hg, c0, n):
             nc.vector.tensor_copy(
                 out=hg[:, c0:c0 + n, :].rearrange("p (c i) t -> p c t i", i=4),
                 in_=hp[:, :, c0:c0 + n].rearrange("p t (c i) -> p c t i", i=4),
             )
 
-        def h_quantise(c0, n):
+        def h_quantise(hg, h0, c0, n):
             nc.vector.quantize_mx(
-                out=hc[:, c0:c0 + n].bitcast(FP8X4),
-                scales=hs[:, c0:c0 + n],
+                out=hc[:, h0 + c0:h0 + c0 + n].bitcast(FP8X4),
+                scales=hs[:, h0 + c0:h0 + c0 + n],
                 in_=hg[:, c0:c0 + n, :].rearrange("p c t -> p (c t)"),
             )
 
-        h_out("s", acc0[0][:], 0, 0, 512)
-        h_out("v", acc0[2][:], 2, 0, 512)
-        h_out("s", acc0[1][:], 1, 0, 512)
-        h_out("v", acc0[3][:], 3, 0, 512)
-        for j in range(4):
-            conv1_pass(acc1[j][:], NG - 1, j, 512, 512, False, True)
-        h_regroup(0, 256)
-        h_regroup(256, 256)
-        h_quantise(0, 256)
-        h_quantise(256, 256)
-        h_out("s", acc1[0][:], 0, 512, 512)
-        h_out("s", acc1[1][:], 1, 512, 512)
-        h_out("v", acc1[3][:], 3, 512, 512)
-        h_out("s", acc1[2][:], 2, 512, 512)
+        def acc_banks():
+            return [psum.tile([P, 512], F32, name="acc%d" % j, tag="acc%d" % j) for j in range(4)]
 
-        acc2 = psum.tile([P, 512], F32, name="c2", tag="acc0")
+        def late_pixels(g, engs):
+            grp = grp_pool.tile([P, 3, P, 4], BF16, name="grp2", tag="grp", align_bytes=64)
+            tf_bank(g, 3, grp[:, 0:2], engs[0])
+            tf_last(g, grp[:, 2], engs[1])
+            return grp
+
+        acc0 = acc_banks()
+        shift_odd(0, parts=2)
+        for g in range(NG):
+            grp = grp_pool.tile([P, 6, P, 4], BF16, name="grp", tag="grp", align_bytes=64)
+            tf_bank(g, 0, grp[:, 0:2], "s")
+            if g >= 2:
+                fc(g - 2, "s")
+            tf_bank(g, 1, grp[:, 2:4], "v")
+            if 1 <= g < NG - 1:
+                shift_odd(g + 1)
+            if g >= 1:
+                for j in range(2):
+                    conv1_pass(acc0[j][:], g - 1, j, 0, 512)
+            tf_bank(g, 2, grp[:, 4:6], "s")
+            made = [0, 1] if g == 0 else [g + 1] if g + 1 < NG else []
+            wags = [wa_unit(i, "sv") for i in made]
+            if g >= 1:
+                for j in range(2, 4):
+                    conv1_pass(acc0[j][:], g - 1, j, 0, 512)
+            if g == 1:
+                ft_unit("s")
+            if 1 <= g < 5:
+                wf_unit(g - 1, "sv")
+            if g == 0:
+                grp0 = late_pixels(0, "ss")
+                nc.vector.tensor_copy(out=ba_f[:], in_=ba_raw[:])
+                shift_odd(1)
+            fv_quantise(g, grp, ((0, 512), (512, 256)))
+            for i, wag in zip(made, wags):
+                wa_quantise(i, wag)
+            if g == 0:
+                fv_quantise(0, grp0, ((768, 256), (1024, 128)))
+
+        for g in range(1, NG):
+            grp = late_pixels(g, "vs" if g % 2 else "ss")
+            if g == 1:
+                for j in range(4):
+                    conv1_pass(acc0[j][:], NG - 1, j, 0, 512)
+                hp0 = grp_pool.tile([P, 4, 512], BF16, name="hp0", tag="grp", align_bytes=64)
+                for j in range(4):
+                    h_out("sv"[j % 2], hp0, acc0[j][:], j, 512)
+                acc1 = acc_banks()
+            if g >= 2:
+                for j in range(4):
+                    conv1_pass(acc1[j][:], g - 2, j, 512, 512)
+            fv_quantise(g, grp, ((768, 256), (1024, 128)))
+            if g == 1:
+                hg0 = grp_pool.tile([P, 512, 4], BF16, name="hg0", tag="grp", align_bytes=64)
+                h_regroup(hp0, hg0, 0, 256)
+                h_regroup(hp0, hg0, 256, 256)
+                h_quantise(hg0, 0, 0, 512)
+        wbgs = [wb_unit(i, "sv") for i in range(2)]
+        for g in (NG - 2, NG - 1):
+            for j in range(4):
+                conv1_pass(acc1[j][:], g, j, 512, 512)
+        for i in range(2):
+            wb_quantise(i, wbgs[i])
+
+        hp1 = grp_pool.tile([P, 4, 512], BF16, name="hp1", tag="grp", align_bytes=64)
+        hg1 = grp_pool.tile([P, 512, 4], BF16, name="hg1", tag="grp", align_bytes=64)
+        for j in range(4):
+            h_out("sv"[j % 2], hp1, acc1[j][:], j, 512)
+        acc2 = psum.tile([P, 512], F32, name="acc2", tag="tr0")
         for j in range(4):
             for g in range(NG):
-                conv1_pass(acc2[:, j * P:(j + 1) * P], g, j, 1024, P, g == 0, g == NG - 1)
-        h_regroup(512, 256)
-        h_regroup(768, 256)
-        h_quantise(512, 256)
-        h_quantise(768, 256)
+                conv1_pass(acc2[:, j * P:(j + 1) * P], g, j, 1024, P)
+        h_regroup(hp1, hg1, 0, 256)
+        h_regroup(hp1, hg1, 256, 256)
+        h_quantise(hg1, 512, 0, 256)
+        h_quantise(hg1, 512, 256, 256)
+        hp2 = grp_pool.tile([P, 4, P], BF16, name="hp2", tag="grp", align_bytes=64)
+        hg2 = grp_pool.tile([P, P, 4], BF16, name="hg2", tag="grp", align_bytes=64)
         for j in range(4):
-            h_out("s", acc2[:, j * P:(j + 1) * P], j, 1024, P)
-        h_regroup(1024, P)
-        h_quantise(1024, P)
+            h_out("s", hp2, acc2[:, j * P:(j + 1) * P], j, P)
+        h_regroup(hp2, hg2, 0, P)
+        h_quantise(hg2, 1024, 0, P)
 
-        gacc = [psum.tile([P, 512], F32, name="g%d" % i, tag="acc%d" % (i + 1)) for i in range(2)]
+        gacc = [psum.tile([P, 512], F32, name="g%d" % i, tag="tr%d" % (i + 1)) for i in range(2)]
         order = [(half, x) for half in range(2) for x in range(4)]
         order += [(half, x) for half in range(2) for x in range(4, PIX)]
         for half, x in order:

@@ -137,23 +137,24 @@ def tile_joint_module_pb_kernel(tc, fv, ft, Wa, ba, Wb, bb, Wfc2, bfc2, out):
 
         def shift_odd(g, parts=1):
             rv = fv_raw[g][:].rearrange("p (v r) -> p v r", r=18)
-            oddc[g] = odd_pool.tile([P, 256, 8], BF16, name="oddc")
+            oddc[g] = odd_pool.tile([P, 4, 256, 2], BF16, name="oddc")
             last[g] = odd_pool.tile([P, 256, 2], BF16, name="last")
             n = 256 // parts
             for i in range(parts):
                 v = slice(i * n, (i + 1) * n)
-                nc.vector.tensor_copy(out=oddc[g][:, v], in_=rv[:, v, 9:17])
+                nc.vector.tensor_copy(
+                    out=oddc[g][:, :, v], in_=rv[:, v, 9:17].rearrange("p v (a h) -> p a v h", h=2)
+                )
                 nc.vector.tensor_copy(out=last[g][:, v], in_=rv[:, v, 8:18:9])
 
         def tf_bank(g, a, dst, eng):
             pb = tbank()
             fw = fv_raw[g][:].bitcast(F32)
-            ow = oddc[g][:].rearrange("p v r -> p (v r)").bitcast(F32)
+            ow = oddc[g][:, a].rearrange("p v h -> p (v h)").bitcast(F32)
             for s in range(2):
                 st = s * 1152 + a
                 nc.tensor.transpose(pb[:, 2 * s * P:(2 * s + 1) * P], fw[:, st:st + 1144:9], ident[:])
-                st = s * 512 + a
-                nc.tensor.transpose(pb[:, (2 * s + 1) * P:(2 * s + 2) * P], ow[:, st:st + 509:4], ident[:])
+                nc.tensor.transpose(pb[:, (2 * s + 1) * P:(2 * s + 2) * P], ow[:, s * P:(s + 1) * P], ident[:])
             copy(eng, dst, pb[:].bitcast(BF16).rearrange("p (t b h) -> p h b t", t=4, h=2))
 
         def tf_last(g, dst, eng):

@@ -27,8 +27,8 @@ def tile_joint_module_pb_kernel(tc, fv, ft, Wa, ba, Wb, bb, Wfc2, bfc2, out):
         fvraw_pool = ctx.enter_context(tc.tile_pool(name="fvraw", bufs=6))
         wraw_pool = ctx.enter_context(tc.tile_pool(name="wraw", bufs=5))
         odd_pool = ctx.enter_context(tc.tile_pool(name="odd", bufs=6))
-        grp_pool = ctx.enter_context(tc.tile_pool(name="grp", bufs=3))
-        wag_pool = ctx.enter_context(tc.tile_pool(name="wag", bufs=2))
+        grp_pool = ctx.enter_context(tc.tile_pool(name="grp", bufs=4))
+        wag_pool = ctx.enter_context(tc.tile_pool(name="wag", bufs=3))
         psum = ctx.enter_context(tc.psum_pool(name="ps", bufs=1))
         ctx.enter_context(tc.manual_schedule())
 
@@ -174,18 +174,19 @@ def tile_joint_module_pb_kernel(tc, fv, ft, Wa, ba, Wb, bb, Wfc2, bfc2, out):
                     in_=gf[:, 4 * (c0 - first):4 * (c0 - first + n)],
                 )
 
-        def wa_unit(i, engs):
+        wags = {}
+
+        def wa_part(i, g2, eng):
             ww = wa_raw[i][:].bitcast(F32)
-            wag = wag_pool.tile([P, 2, 2, P, 2], F32, name="wag", tag="wag", align_bytes=64)
-            for g2 in range(2):
-                pb = tbank()
-                for em in range(2):
-                    for s in range(2):
-                        slot = em * 2 + s
-                        c0 = 256 * g2 + P * s
-                        nc.tensor.transpose(pb[:, slot * P:(slot + 1) * P], ww[:, em, c0:c0 + P], ident[:])
-                copy(engs[g2], wag[:, g2], pb[:].rearrange("p (e s q) -> p e q s", e=2, s=2))
-            return wag
+            if g2 == 0:
+                wags[i] = wag_pool.tile([P, 2, 2, P, 2], F32, name="wag", tag="wag", align_bytes=64)
+            pb = tbank()
+            for em in range(2):
+                for s in range(2):
+                    slot = em * 2 + s
+                    c0 = 256 * g2 + P * s
+                    nc.tensor.transpose(pb[:, slot * P:(slot + 1) * P], ww[:, em, c0:c0 + P], ident[:])
+            copy(eng, wags[i][:, g2], pb[:].rearrange("p (e s q) -> p e q s", e=2, s=2))
 
         def wa_quantise(i, wag):
             sm, gp = i % 2, i // 2
@@ -205,28 +206,25 @@ def tile_joint_module_pb_kernel(tc, fv, ft, Wa, ba, Wb, bb, Wfc2, bfc2, out):
                 nc.tensor.transpose(pb[:, k * P:(k + 1) * P], fw[:, k * P:(k + 1) * P], ident[:])
             copy(eng, ftT[:].rearrange("p k b -> p (k b)"), pb[:])
 
-        def wf_unit(i, engs):
+        def wf_part(i, h, eng):
             ww = wf_raw[i][:].bitcast(F32)
-            for h in range(2):
-                pb = tbank()
-                for kl in range(2):
-                    for tl in range(2):
-                        slot = kl * 2 + tl
-                        k = 2 * h + kl
-                        nc.tensor.transpose(pb[:, slot * P:(slot + 1) * P], ww[:, tl, k * P:(k + 1) * P], ident[:])
-                copy(
-                    engs[h], wfT[:, 2 * h:2 * h + 2, i * 256:(i + 1) * 256], pb[:].rearrange("p (k o) -> p k o", k=2)
-                )
+            pb = tbank()
+            for kl in range(2):
+                for tl in range(2):
+                    slot = kl * 2 + tl
+                    k = 2 * h + kl
+                    nc.tensor.transpose(pb[:, slot * P:(slot + 1) * P], ww[:, tl, k * P:(k + 1) * P], ident[:])
+            copy(eng, wfT[:, 2 * h:2 * h + 2, i * 256:(i + 1) * 256], pb[:].rearrange("p (k o) -> p k o", k=2))
 
-        def fc(i, eng):
+        def fc_half(i, h, eng):
             acc = tbank()
-            cols = slice(i * 256, (i + 1) * 256)
+            cols = slice(i * 256 + h * P, i * 256 + (h + 1) * P)
             for idx in range(8):
                 k, e = divmod(idx, 2)
                 nc.tensor.matmul(
-                    out=acc[:, 0:256], lhsT=ft_e[:, k, :, e], rhs=wf_e[:, k, cols, e], start=idx == 0, stop=idx == 7
+                    out=acc[:, 0:P], lhsT=ft_e[:, k, :, e], rhs=wf_e[:, k, cols, e], start=idx == 0, stop=idx == 7
                 )
-            copy(eng, ft2[:, cols], acc[:, 0:256])
+            copy(eng, ft2[:, cols], acc[:, 0:P])
 
         def wb_unit(i, engs):
             ww = wb_raw[i][:].bitcast(F32)
@@ -284,56 +282,71 @@ def tile_joint_module_pb_kernel(tc, fv, ft, Wa, ba, Wb, bb, Wfc2, bfc2, out):
             return grp
 
         acc0 = acc_banks()
-        shift_odd(0, parts=2)
+        rv = fv_raw[0][:].rearrange("p (v r) -> p v r", r=18)
+        oddc[0] = odd_pool.tile([P, 4, 256, 2], BF16, name="oddc")
+        last[0] = odd_pool.tile([P, 256, 2], BF16, name="last")
+        for v, a0, n in ((0, 0, 4), (1, 0, 1), (1, 1, 1), (1, 2, 2)):
+            vs = slice(v * 128, (v + 1) * 128)
+            nc.vector.tensor_copy(
+                out=oddc[0][:, a0:a0 + n, vs],
+                in_=rv[:, vs, 9 + 2 * a0:9 + 2 * (a0 + n)].rearrange("p v (a h) -> p a v h", h=2),
+            )
+        nc.vector.tensor_copy(out=last[0][:], in_=rv[:, :, 8:18:9])
         for g in range(NG):
             grp = grp_pool.tile([P, 6, P, 4], BF16, name="grp", tag="grp", align_bytes=64)
-            tf_bank(g, 0, grp[:, 0:2], "s")
+            tf_bank(g, 0, grp[:, 0:2], "vs"[g % 2])
+            tf_bank(g, 1, grp[:, 2:4], "sv"[g % 2])
             if g >= 2:
-                fc(g - 2, "s")
-            tf_bank(g, 1, grp[:, 2:4], "v")
-            if 1 <= g < NG - 1:
-                shift_odd(g + 1)
-            if g >= 1:
-                for j in range(2):
-                    conv1_pass(acc0[j][:], g - 1, j, 0, 512)
+                fc_half(g - 2, 0, "s")
             tf_bank(g, 2, grp[:, 4:6], "s")
-            made = [0, 1] if g == 0 else [g + 1] if g + 1 < NG else []
-            wags = [wa_unit(i, "sv") for i in made]
-            if g >= 1:
-                for j in range(2, 4):
-                    conv1_pass(acc0[j][:], g - 1, j, 0, 512)
-            if g == 1:
-                ft_unit("s")
-            if 1 <= g < 5:
-                wf_unit(g - 1, "sv")
             if g == 0:
-                grp0 = late_pixels(0, "ss")
+                late = late_pixels(g, "vs")
                 nc.vector.tensor_copy(out=ba_f[:], in_=ba_raw[:])
                 shift_odd(1)
-            fv_quantise(g, grp, ((0, 512), (512, 256)))
-            for i, wag in zip(made, wags):
-                wa_quantise(i, wag)
-            if g == 0:
-                fv_quantise(0, grp0, ((768, 256), (1024, 128)))
-
-        for g in range(1, NG):
-            grp = late_pixels(g, "vs" if g % 2 else "ss")
+                for i in range(2):
+                    for g2 in range(2):
+                        wa_part(i, g2, "s")
+                fv_quantise(g, grp, ((0, 512), (512, 256)))
+                fv_quantise(g, late, ((768, 256), (1024, 128)))
+                for i in range(2):
+                    wa_quantise(i, wags[i])
+                continue
             if g == 1:
-                for j in range(4):
-                    conv1_pass(acc0[j][:], NG - 1, j, 0, 512)
-                hp0 = grp_pool.tile([P, 4, 512], BF16, name="hp0", tag="grp", align_bytes=64)
-                for j in range(4):
-                    h_out("sv"[j % 2], hp0, acc0[j][:], j, 512)
-                acc1 = acc_banks()
+                ft_unit("v")
+            more = g + 1 < NG
+            if more:
+                wa_part(g + 1, 0, "s")
+            for j in range(4):
+                conv1_pass(acc0[j][:], g - 1, j, 0, 512)
+            if more:
+                shift_odd(g + 1)
+                wa_part(g + 1, 1, "s")
+                wf_part(g - 1, 0, "s")
+            fv_quantise(g, grp, ((0, 512), (512, 256)))
+            if more:
+                wa_quantise(g + 1, wags[g + 1])
+            if more:
+                wf_part(g - 1, 1, "s")
             if g >= 2:
-                for j in range(4):
-                    conv1_pass(acc1[j][:], g - 2, j, 512, 512)
-            fv_quantise(g, grp, ((768, 256), (1024, 128)))
+                fc_half(g - 2, 1, "s")
+
+        for j in range(4):
+            conv1_pass(acc0[j][:], NG - 1, j, 0, 512)
+        hp0 = grp_pool.tile([P, 4, 512], BF16, name="hp0", tag="grp", align_bytes=64)
+        for j in range(4):
+            h_out("sv"[j % 2], hp0, acc0[j][:], j, 512)
+        acc1 = acc_banks()
+        for g in range(1, NG):
+            late = late_pixels(g, "vs" if g % 2 else "ss")
+            fv_quantise(g, late, ((768, 256), (1024, 128)))
             if g == 1:
                 hg0 = grp_pool.tile([P, 512, 4], BF16, name="hg0", tag="grp", align_bytes=64)
                 h_regroup(hp0, hg0, 0, 256)
                 h_regroup(hp0, hg0, 256, 256)
                 h_quantise(hg0, 0, 0, 512)
+            else:
+                for j in range(4):
+                    conv1_pass(acc1[j][:], g - 2, j, 512, 512)
         wbgs = [wb_unit(i, "sv") for i in range(2)]
         for g in (NG - 2, NG - 1):
             for j in range(4):

@@ -93,15 +93,15 @@ def tile_joint_module_pb_kernel(tc, fv, ft, Wa, ba, Wb, bb, Wfc2, bfc2, out):
 
         load_fv(0, parts=2)
         load_wa(0)
+        nc.sync.dma_start(out=ft_raw[:], in_=ft)
+        load_wf(0)
         load_wa(1)
         load_fv(1)
-        load_wa(2)
-        nc.sync.dma_start(out=ft_raw[:], in_=ft)
         for g in range(2, NG):
-            load_wf(g - 2)
+            if g <= 4:
+                load_wf(g - 1)
+            load_wa(g)
             load_fv(g)
-            if g + 1 < NG:
-                load_wa(g + 1)
         load_wb(0)
         load_wb(1)
         nc.sync.dma_start(out=bfc_bc[:], in_=bfc2.partition_broadcast(P))
@@ -135,17 +135,19 @@ def tile_joint_module_pb_kernel(tc, fv, ft, Wa, ba, Wb, bb, Wfc2, bfc2, out):
         oddc = {}
         last = {}
 
-        def shift_odd(g, parts=1):
+        def shift_odd(g, pieces=((0, 256, 0, 4),)):
             rv = fv_raw[g][:].rearrange("p (v r) -> p v r", r=18)
             oddc[g] = odd_pool.tile([P, 4, 256, 2], BF16, name="oddc")
             last[g] = odd_pool.tile([P, 256, 2], BF16, name="last")
-            n = 256 // parts
-            for i in range(parts):
-                v = slice(i * n, (i + 1) * n)
+            for v0, nv, a0, na in pieces:
+                v = slice(v0, v0 + nv)
                 nc.vector.tensor_copy(
-                    out=oddc[g][:, :, v], in_=rv[:, v, 9:17].rearrange("p v (a h) -> p a v h", h=2)
+                    out=oddc[g][:, a0:a0 + na, v],
+                    in_=rv[:, v, 9 + 2 * a0:9 + 2 * (a0 + na)].rearrange("p v (a h) -> p a v h", h=2),
                 )
-                nc.vector.tensor_copy(out=last[g][:, v], in_=rv[:, v, 8:18:9])
+            nc.gpsimd.tensor_scalar(
+                out=last[g][:], in0=rv[:, :, 8:18:9], scalar1=1.0, scalar2=0.0, op0=ALU.mult, op1=ALU.add
+            )
 
         def tf_bank(g, a, dst, eng):
             pb = tbank()
@@ -282,71 +284,74 @@ def tile_joint_module_pb_kernel(tc, fv, ft, Wa, ba, Wb, bb, Wfc2, bfc2, out):
             return grp
 
         acc0 = acc_banks()
-        rv = fv_raw[0][:].rearrange("p (v r) -> p v r", r=18)
-        oddc[0] = odd_pool.tile([P, 4, 256, 2], BF16, name="oddc")
-        last[0] = odd_pool.tile([P, 256, 2], BF16, name="last")
-        for v, a0, n in ((0, 0, 4), (1, 0, 1), (1, 1, 1), (1, 2, 2)):
-            vs = slice(v * 128, (v + 1) * 128)
-            nc.vector.tensor_copy(
-                out=oddc[0][:, a0:a0 + n, vs],
-                in_=rv[:, vs, 9 + 2 * a0:9 + 2 * (a0 + n)].rearrange("p v (a h) -> p a v h", h=2),
-            )
-        nc.vector.tensor_copy(out=last[0][:], in_=rv[:, :, 8:18:9])
+        shift_odd(0, ((0, 128, 0, 4), (128, 128, 0, 1), (128, 128, 1, 1), (128, 128, 2, 2)))
         for g in range(NG):
             grp = grp_pool.tile([P, 6, P, 4], BF16, name="grp", tag="grp", align_bytes=64)
-            tf_bank(g, 0, grp[:, 0:2], "vs"[g % 2])
-            tf_bank(g, 1, grp[:, 2:4], "sv"[g % 2])
-            if g >= 2:
-                fc_half(g - 2, 0, "s")
-            tf_bank(g, 2, grp[:, 4:6], "s")
+            tf_bank(g, 0, grp[:, 0:2], "s")
+            tf_bank(g, 1, grp[:, 2:4], "v")
             if g == 0:
-                late = late_pixels(g, "vs")
+                late = grp_pool.tile([P, 3, P, 4], BF16, name="late", tag="grp", align_bytes=64)
+                tf_bank(g, 2, grp[:, 4:6], "s")
+                tf_bank(g, 3, late[:, 0:2], "v")
+                tf_last(g, late[:, 2], "s")
                 nc.vector.tensor_copy(out=ba_f[:], in_=ba_raw[:])
                 shift_odd(1)
-                for i in range(2):
-                    for g2 in range(2):
-                        wa_part(i, g2, "s")
+                wa_part(0, 0, "s")
+                wa_part(0, 1, "s")
+                ft_unit("s")
+                wf_part(0, 0, "s")
+                wf_part(0, 1, "s")
+                wa_part(1, 0, "s")
+                wa_part(1, 1, "s")
                 fv_quantise(g, grp, ((0, 512), (512, 256)))
                 fv_quantise(g, late, ((768, 256), (1024, 128)))
-                for i in range(2):
-                    wa_quantise(i, wags[i])
+                wa_quantise(0, wags[0])
+                wa_quantise(1, wags[1])
                 continue
-            if g == 1:
-                ft_unit("v")
             more = g + 1 < NG
             if more:
-                wa_part(g + 1, 0, "s")
-            for j in range(4):
+                fc_half(g - 1, 0, "s")
+            for j in range(2):
                 conv1_pass(acc0[j][:], g - 1, j, 0, 512)
+            tf_bank(g, 2, grp[:, 4:6], "s")
             if more:
                 shift_odd(g + 1)
+                wa_part(g + 1, 0, "v")
+            for j in range(2, 4):
+                conv1_pass(acc0[j][:], g - 1, j, 0, 512)
+            if g < 4:
+                wf_part(g, 0, "v")
+            if more:
                 wa_part(g + 1, 1, "s")
-                wf_part(g - 1, 0, "s")
             fv_quantise(g, grp, ((0, 512), (512, 256)))
             if more:
                 wa_quantise(g + 1, wags[g + 1])
-            if more:
-                wf_part(g - 1, 1, "s")
-            if g >= 2:
-                fc_half(g - 2, 1, "s")
+                fc_half(g - 1, 1, "s")
+            if g < 4:
+                wf_part(g, 1, "s")
 
-        for j in range(4):
-            conv1_pass(acc0[j][:], NG - 1, j, 0, 512)
-        hp0 = grp_pool.tile([P, 4, 512], BF16, name="hp0", tag="grp", align_bytes=64)
-        for j in range(4):
-            h_out("sv"[j % 2], hp0, acc0[j][:], j, 512)
-        acc1 = acc_banks()
         for g in range(1, NG):
-            late = late_pixels(g, "vs" if g % 2 else "ss")
+            late = grp_pool.tile([P, 3, P, 4], BF16, name="late", tag="grp", align_bytes=64)
+            tf_bank(g, 3, late[:, 0:2], "s")
+            if g == 1:
+                for j in range(4):
+                    conv1_pass(acc0[j][:], NG - 1, j, 0, 512)
+                hp0 = grp_pool.tile([P, 4, 512], BF16, name="hp0", tag="grp", align_bytes=64)
+                for j in range(4):
+                    h_out("sv"[j % 2], hp0, acc0[j][:], j, 512)
+                acc1 = acc_banks()
+            tf_last(g, late[:, 2], "s")
+            if g >= 2:
+                for j in range(4):
+                    conv1_pass(acc1[j][:], g - 2, j, 512, 512)
             fv_quantise(g, late, ((768, 256), (1024, 128)))
             if g == 1:
                 hg0 = grp_pool.tile([P, 512, 4], BF16, name="hg0", tag="grp", align_bytes=64)
                 h_regroup(hp0, hg0, 0, 256)
                 h_regroup(hp0, hg0, 256, 256)
                 h_quantise(hg0, 0, 0, 512)
-            else:
-                for j in range(4):
-                    conv1_pass(acc1[j][:], g - 2, j, 512, 512)
+            if g == 2:
+                nc.vector.tensor_tensor(out=ft2[:], in0=ft2[:], in1=bfc_bc[:], op=ALU.add)
         wbgs = [wb_unit(i, "sv") for i in range(2)]
         for g in (NG - 2, NG - 1):
             for j in range(4):
@@ -373,37 +378,45 @@ def tile_joint_module_pb_kernel(tc, fv, ft, Wa, ba, Wb, bb, Wfc2, bfc2, out):
         h_regroup(hp2, hg2, 0, P)
         h_quantise(hg2, 1024, 0, P)
 
-        gacc = [psum.tile([P, 512], F32, name="g%d" % i, tag="tr%d" % (i + 1)) for i in range(2)]
-        order = [(half, x) for half in range(2) for x in range(4)]
-        order += [(half, x) for half in range(2) for x in range(4, PIX)]
-        for half, x in order:
+        parts = ((0, 512), (512, 256), (768, 256))
+        gacc = [psum.tile([P, 512], F32, name="g%d" % i, tag="tr%d" % (i + 1)) for i in range(len(parts))]
+
+        def conv2_pass(i, x):
+            c0, n = parts[i]
             nc.tensor.matmul_mx(
-                out=gacc[half][:],
+                out=gacc[i][:, 0:n],
                 lhsT=hc[:, x * P:(x + 1) * P].bitcast(FP8X4),
                 lhsT_scale=hs[:, x * P:(x + 1) * P],
-                rhs=wbc[:, half * 512:(half + 1) * 512].bitcast(FP8X4),
-                rhs_scale=wbs[:, half * 512:(half + 1) * 512],
+                rhs=wbc[:, c0:c0 + n].bitcast(FP8X4),
+                rhs_scale=wbs[:, c0:c0 + n],
                 start=x == 0,
                 stop=x == PIX - 1,
             )
-        nc.vector.tensor_tensor(out=ft2[:], in0=ft2[:], in1=bfc_bc[:], op=ALU.add)
 
-        def gate_in(half, c0, n):
+        for i in range(len(parts)):
+            for x in range(4):
+                conv2_pass(i, x)
+        for i in range(len(parts)):
+            for x in range(4, PIX):
+                conv2_pass(i, x)
+
+        def gate_in(i):
+            c0, n = parts[i]
             nc.vector.scalar_tensor_tensor(
-                out=z[:, c0:c0 + n], in0=gacc[half][:, c0 - half * 512:c0 - half * 512 + n], scalar=1.0 / PIX,
+                out=z[:, c0:c0 + n], in0=gacc[i][:, 0:n], scalar=1.0 / PIX,
                 in1=bb_bc[:, c0:c0 + n], op0=ALU.mult, op1=ALU.add,
             )
             nc.scalar.activation(out=z[:, c0:c0 + n], in_=z[:, c0:c0 + n], func=ACT.Sigmoid)
 
-        def gate_out(c0, n):
+        def gate_out(i):
+            c0, n = parts[i]
             nc.vector.scalar_tensor_tensor(
                 out=z[:, c0:c0 + n], in0=z[:, c0:c0 + n], scalar=1.0, in1=ft2[:, c0:c0 + n], op0=ALU.add, op1=ALU.mult
             )
             nc.sync.dma_start(out=out[:, c0:c0 + n], in_=z[:, c0:c0 + n])
 
-        gate_in(0, 0, 512)
-        gate_out(0, 512)
-        gate_in(1, 512, 256)
-        gate_in(1, 768, 256)
-        gate_out(512, 256)
-        gate_out(768, 256)
+        gate_in(0)
+        for i in range(1, len(parts)):
+            gate_in(i)
+            gate_out(i - 1)
+        gate_out(len(parts) - 1)

@@ -52,7 +52,7 @@ def tile_joint_module_pb_kernel(tc, fv, ft, Wa, ba, Wb, bb, Wfc2, bfc2, out):
         wbc = keep.tile([P, C], U32, name="wbc", align_bytes=64)
         wbs = keep.tile([P, C], U8, name="wbs", align_bytes=64)
         wfT = keep.tile([P, 4, C], F32, name="wfT")
-        ftT = keep.tile([P, 4, P], F32, name="ftT")
+        ftT = keep.tile([P, 4, 2, P], BF16, name="ftT")
         ft2 = keep.tile([P, C], F32, name="ft2")
         hc = keep.tile([P, COLS], U32, name="hc", align_bytes=64)
         hs = keep.tile([P, COLS], U8, name="hs", align_bytes=64)
@@ -145,9 +145,7 @@ def tile_joint_module_pb_kernel(tc, fv, ft, Wa, ba, Wb, bb, Wfc2, bfc2, out):
                     out=oddc[g][:, a0:a0 + na, v],
                     in_=rv[:, v, 9 + 2 * a0:9 + 2 * (a0 + na)].rearrange("p v (a h) -> p a v h", h=2),
                 )
-            nc.gpsimd.tensor_scalar(
-                out=last[g][:], in0=rv[:, :, 8:18:9], scalar1=1.0, scalar2=0.0, op0=ALU.mult, op1=ALU.add
-            )
+            nc.vector.tensor_copy(out=last[g][:], in_=rv[:, :, 8:18:9])
 
         def tf_bank(g, a, dst, eng):
             pb = tbank()
@@ -198,7 +196,6 @@ def tile_joint_module_pb_kernel(tc, fv, ft, Wa, ba, Wb, bb, Wfc2, bfc2, out):
                 in_=wag[:].rearrange("p g e q s -> p (g e q s)").bitcast(BF16),
             )
 
-        ft_e = ftT[:].bitcast(BF16).rearrange("p k (b e) -> p k b e", e=2)
         wf_e = wfT[:].bitcast(BF16).rearrange("p k (o e) -> p k o e", e=2)
 
         def ft_unit(eng):
@@ -206,7 +203,7 @@ def tile_joint_module_pb_kernel(tc, fv, ft, Wa, ba, Wb, bb, Wfc2, bfc2, out):
             fw = ft_raw[:].bitcast(F32)
             for k in range(4):
                 nc.tensor.transpose(pb[:, k * P:(k + 1) * P], fw[:, k * P:(k + 1) * P], ident[:])
-            copy(eng, ftT[:].rearrange("p k b -> p (k b)"), pb[:])
+            copy(eng, ftT[:], pb[:].bitcast(BF16).rearrange("p (k b e) -> p k e b", k=4, e=2))
 
         def wf_part(i, h, eng):
             ww = wf_raw[i][:].bitcast(F32)
@@ -224,7 +221,7 @@ def tile_joint_module_pb_kernel(tc, fv, ft, Wa, ba, Wb, bb, Wfc2, bfc2, out):
             for idx in range(8):
                 k, e = divmod(idx, 2)
                 nc.tensor.matmul(
-                    out=acc[:, 0:P], lhsT=ft_e[:, k, :, e], rhs=wf_e[:, k, cols, e], start=idx == 0, stop=idx == 7
+                    out=acc[:, 0:P], lhsT=ftT[:, k, e], rhs=wf_e[:, k, cols, e], start=idx == 0, stop=idx == 7
                 )
             copy(eng, ft2[:, cols], acc[:, 0:P])
 
@@ -295,7 +292,6 @@ def tile_joint_module_pb_kernel(tc, fv, ft, Wa, ba, Wb, bb, Wfc2, bfc2, out):
                 tf_bank(g, 3, late[:, 0:2], "v")
                 tf_last(g, late[:, 2], "s")
                 nc.vector.tensor_copy(out=ba_f[:], in_=ba_raw[:])
-                shift_odd(1)
                 wa_part(0, 0, "s")
                 wa_part(0, 1, "s")
                 ft_unit("s")
@@ -304,6 +300,7 @@ def tile_joint_module_pb_kernel(tc, fv, ft, Wa, ba, Wb, bb, Wfc2, bfc2, out):
                 wa_part(1, 0, "s")
                 wa_part(1, 1, "s")
                 fv_quantise(g, grp, ((0, 512), (512, 256)))
+                shift_odd(1)
                 fv_quantise(g, late, ((768, 256), (1024, 128)))
                 wa_quantise(0, wags[0])
                 wa_quantise(1, wags[1])
@@ -311,28 +308,28 @@ def tile_joint_module_pb_kernel(tc, fv, ft, Wa, ba, Wb, bb, Wfc2, bfc2, out):
             more = g + 1 < NG
             if more:
                 fc_half(g - 1, 0, "s")
-            for j in range(2):
-                conv1_pass(acc0[j][:], g - 1, j, 0, 512)
             tf_bank(g, 2, grp[:, 4:6], "s")
             if more:
-                shift_odd(g + 1)
-                wa_part(g + 1, 0, "v")
-            for j in range(2, 4):
+                wa_part(g + 1, 0, "s")
+            for j in range(4):
                 conv1_pass(acc0[j][:], g - 1, j, 0, 512)
+            if more:
+                shift_odd(g + 1)
+            fv_quantise(g, grp, ((0, 512), (512, 256)))
             if g < 4:
-                wf_part(g, 0, "v")
+                wf_part(g, 0, "s")
             if more:
                 wa_part(g + 1, 1, "s")
-            fv_quantise(g, grp, ((0, 512), (512, 256)))
-            if more:
-                wa_quantise(g + 1, wags[g + 1])
-                fc_half(g - 1, 1, "s")
+                fc_half(g - 1, 1, "v")
             if g < 4:
                 wf_part(g, 1, "s")
+            if more:
+                wa_quantise(g + 1, wags[g + 1])
 
         for g in range(1, NG):
             late = grp_pool.tile([P, 3, P, 4], BF16, name="late", tag="grp", align_bytes=64)
-            tf_bank(g, 3, late[:, 0:2], "s")
+            tf_bank(g, 3, late[:, 0:2], "v" if g % 2 else "s")
+            tf_last(g, late[:, 2], "s")
             if g == 1:
                 for j in range(4):
                     conv1_pass(acc0[j][:], NG - 1, j, 0, 512)
@@ -340,18 +337,15 @@ def tile_joint_module_pb_kernel(tc, fv, ft, Wa, ba, Wb, bb, Wfc2, bfc2, out):
                 for j in range(4):
                     h_out("sv"[j % 2], hp0, acc0[j][:], j, 512)
                 acc1 = acc_banks()
-            tf_last(g, late[:, 2], "s")
-            if g >= 2:
-                for j in range(4):
-                    conv1_pass(acc1[j][:], g - 2, j, 512, 512)
             fv_quantise(g, late, ((768, 256), (1024, 128)))
             if g == 1:
                 hg0 = grp_pool.tile([P, 512, 4], BF16, name="hg0", tag="grp", align_bytes=64)
                 h_regroup(hp0, hg0, 0, 256)
                 h_regroup(hp0, hg0, 256, 256)
                 h_quantise(hg0, 0, 0, 512)
-            if g == 2:
-                nc.vector.tensor_tensor(out=ft2[:], in0=ft2[:], in1=bfc_bc[:], op=ALU.add)
+            if g >= 2:
+                for j in range(4):
+                    conv1_pass(acc1[j][:], g - 2, j, 512, 512)
         wbgs = [wb_unit(i, "sv") for i in range(2)]
         for g in (NG - 2, NG - 1):
             for j in range(4):
@@ -377,6 +371,7 @@ def tile_joint_module_pb_kernel(tc, fv, ft, Wa, ba, Wb, bb, Wfc2, bfc2, out):
             h_out("s", hp2, acc2[:, j * P:(j + 1) * P], j, P)
         h_regroup(hp2, hg2, 0, P)
         h_quantise(hg2, 1024, 0, P)
+        nc.vector.tensor_tensor(out=ft2[:], in0=ft2[:], in1=bfc_bc[:], op=ALU.add)
 
         parts = ((0, 512), (512, 256), (768, 256))
         gacc = [psum.tile([P, 512], F32, name="g%d" % i, tag="tr%d" % (i + 1)) for i in range(len(parts))]

@@ -27,7 +27,7 @@ def tile_joint_module_pb_kernel(tc, fv, ft, Wa, ba, Wb, bb, Wfc2, bfc2, out):
         fvraw_pool = ctx.enter_context(tc.tile_pool(name="fvraw", bufs=6))
         wraw_pool = ctx.enter_context(tc.tile_pool(name="wraw", bufs=5))
         odd_pool = ctx.enter_context(tc.tile_pool(name="odd", bufs=6))
-        grp_pool = ctx.enter_context(tc.tile_pool(name="grp", bufs=4))
+        grp_pool = ctx.enter_context(tc.tile_pool(name="grp", bufs=5))
         wag_pool = ctx.enter_context(tc.tile_pool(name="wag", bufs=3))
         psum = ctx.enter_context(tc.psum_pool(name="ps", bufs=1))
         ctx.enter_context(tc.manual_schedule())
@@ -135,7 +135,7 @@ def tile_joint_module_pb_kernel(tc, fv, ft, Wa, ba, Wb, bb, Wfc2, bfc2, out):
         oddc = {}
         last = {}
 
-        def shift_odd(g, pieces=((0, 256, 0, 4),)):
+        def shift_odd(g, pieces=((0, 256, 0, 4),), eng="s"):
             rv = fv_raw[g][:].rearrange("p (v r) -> p v r", r=18)
             oddc[g] = odd_pool.tile([P, 4, 256, 2], BF16, name="oddc")
             last[g] = odd_pool.tile([P, 256, 2], BF16, name="last")
@@ -145,7 +145,7 @@ def tile_joint_module_pb_kernel(tc, fv, ft, Wa, ba, Wb, bb, Wfc2, bfc2, out):
                     out=oddc[g][:, a0:a0 + na, v],
                     in_=rv[:, v, 9 + 2 * a0:9 + 2 * (a0 + na)].rearrange("p v (a h) -> p a v h", h=2),
                 )
-            nc.vector.tensor_copy(out=last[g][:], in_=rv[:, :, 8:18:9])
+            copy(eng, last[g][:], rv[:, :, 8:18:9])
 
         def tf_bank(g, a, dst, eng):
             pb = tbank()
@@ -280,17 +280,21 @@ def tile_joint_module_pb_kernel(tc, fv, ft, Wa, ba, Wb, bb, Wfc2, bfc2, out):
             tf_last(g, grp[:, 2], engs[1])
             return grp
 
+        def late_pixels(g, eng):
+            late = grp_pool.tile([P, 5, P, 4], BF16, name="late", tag="grp", align_bytes=64)
+            tf_bank(g, 2, late[:, 0:2], "s")
+            tf_bank(g, 3, late[:, 2:4], eng)
+            tf_last(g, late[:, 4], "s")
+            return late
+
         acc0 = acc_banks()
-        shift_odd(0, ((0, 128, 0, 4), (128, 128, 0, 1), (128, 128, 1, 1), (128, 128, 2, 2)))
+        shift_odd(0, ((0, 128, 0, 4), (128, 128, 0, 1), (128, 128, 1, 1), (128, 128, 2, 2)), "v")
         for g in range(NG):
-            grp = grp_pool.tile([P, 6, P, 4], BF16, name="grp", tag="grp", align_bytes=64)
+            grp = grp_pool.tile([P, 4, P, 4], BF16, name="grp", tag="grp", align_bytes=64)
             tf_bank(g, 0, grp[:, 0:2], "s")
             tf_bank(g, 1, grp[:, 2:4], "v")
             if g == 0:
-                late = grp_pool.tile([P, 3, P, 4], BF16, name="late", tag="grp", align_bytes=64)
-                tf_bank(g, 2, grp[:, 4:6], "s")
-                tf_bank(g, 3, late[:, 0:2], "v")
-                tf_last(g, late[:, 2], "s")
+                late = late_pixels(0, "v")
                 nc.vector.tensor_copy(out=ba_f[:], in_=ba_raw[:])
                 wa_part(0, 0, "s")
                 wa_part(0, 1, "s")
@@ -299,37 +303,30 @@ def tile_joint_module_pb_kernel(tc, fv, ft, Wa, ba, Wb, bb, Wfc2, bfc2, out):
                 wf_part(0, 1, "s")
                 wa_part(1, 0, "s")
                 wa_part(1, 1, "s")
-                fv_quantise(g, grp, ((0, 512), (512, 256)))
+                fv_quantise(g, grp, ((0, 512),))
                 shift_odd(1)
-                fv_quantise(g, late, ((768, 256), (1024, 128)))
+                fv_quantise(g, late, ((512, 512), (1024, 128)))
                 wa_quantise(0, wags[0])
                 wa_quantise(1, wags[1])
                 continue
-            more = g + 1 < NG
-            if more:
-                fc_half(g - 1, 0, "s")
-            tf_bank(g, 2, grp[:, 4:6], "s")
-            if more:
-                wa_part(g + 1, 0, "s")
             for j in range(4):
                 conv1_pass(acc0[j][:], g - 1, j, 0, 512)
-            if more:
-                shift_odd(g + 1)
-            fv_quantise(g, grp, ((0, 512), (512, 256)))
-            if g < 4:
-                wf_part(g, 0, "s")
-            if more:
+            if g + 1 < NG:
+                wa_part(g + 1, 0, "s")
+                fc_half(g - 1, 0, "s")
+                if g < 4:
+                    wf_part(g, 0, "s")
                 wa_part(g + 1, 1, "s")
+                shift_odd(g + 1)
+            fv_quantise(g, grp, ((0, 512),))
+            if g + 1 < NG:
+                if g < 4:
+                    wf_part(g, 1, "v")
                 fc_half(g - 1, 1, "v")
-            if g < 4:
-                wf_part(g, 1, "s")
-            if more:
                 wa_quantise(g + 1, wags[g + 1])
 
         for g in range(1, NG):
-            late = grp_pool.tile([P, 3, P, 4], BF16, name="late", tag="grp", align_bytes=64)
-            tf_bank(g, 3, late[:, 0:2], "v" if g % 2 else "s")
-            tf_last(g, late[:, 2], "s")
+            late = late_pixels(g, "s" if g in (2, 3) else "v")
             if g == 1:
                 for j in range(4):
                     conv1_pass(acc0[j][:], NG - 1, j, 0, 512)
@@ -337,13 +334,13 @@ def tile_joint_module_pb_kernel(tc, fv, ft, Wa, ba, Wb, bb, Wfc2, bfc2, out):
                 for j in range(4):
                     h_out("sv"[j % 2], hp0, acc0[j][:], j, 512)
                 acc1 = acc_banks()
-            fv_quantise(g, late, ((768, 256), (1024, 128)))
+            fv_quantise(g, late, ((512, 512), (1024, 128)))
             if g == 1:
                 hg0 = grp_pool.tile([P, 512, 4], BF16, name="hg0", tag="grp", align_bytes=64)
                 h_regroup(hp0, hg0, 0, 256)
                 h_regroup(hp0, hg0, 256, 256)
                 h_quantise(hg0, 0, 0, 512)
-            if g >= 2:
+            else:
                 for j in range(4):
                     conv1_pass(acc1[j][:], g - 2, j, 512, 512)
         wbgs = [wb_unit(i, "sv") for i in range(2)]

@@ -24,10 +24,10 @@ def tile_joint_module_pb_kernel(tc, fv, ft, Wa, ba, Wb, bb, Wfc2, bfc2, out):
     with ExitStack() as ctx:
         const = ctx.enter_context(tc.tile_pool(name="const", bufs=1))
         keep = ctx.enter_context(tc.tile_pool(name="keep", bufs=1))
-        fvraw_pool = ctx.enter_context(tc.tile_pool(name="fvraw", bufs=6))
-        wraw_pool = ctx.enter_context(tc.tile_pool(name="wraw", bufs=5))
-        odd_pool = ctx.enter_context(tc.tile_pool(name="odd", bufs=6))
-        grp_pool = ctx.enter_context(tc.tile_pool(name="grp", bufs=5))
+        fvraw_pool = ctx.enter_context(tc.tile_pool(name="fvraw", bufs=4))
+        fvw_pool = ctx.enter_context(tc.tile_pool(name="fvw", bufs=6))
+        wraw_pool = ctx.enter_context(tc.tile_pool(name="wraw", bufs=4))
+        grp_pool = ctx.enter_context(tc.tile_pool(name="grp", bufs=6))
         wag_pool = ctx.enter_context(tc.tile_pool(name="wag", bufs=3))
         psum = ctx.enter_context(tc.psum_pool(name="ps", bufs=1))
         ctx.enter_context(tc.manual_schedule())
@@ -45,8 +45,10 @@ def tile_joint_module_pb_kernel(tc, fv, ft, Wa, ba, Wb, bb, Wfc2, bfc2, out):
         nc.vector.memset(warm_in[:], 0.0)
         nc.scalar.activation(out=warm_out[:], in_=warm_in[:], func=ACT.Sigmoid)
 
-        fvc = keep.tile([P, NG, COLS], U32, name="fvc", align_bytes=64)
-        fvs = keep.tile([P, NG, COLS], U8, name="fvs", align_bytes=64)
+        fvc = keep.tile([P, NG, 1024], U32, name="fvc", align_bytes=64)
+        fvs = keep.tile([P, NG, 1024], U8, name="fvs", align_bytes=64)
+        fv8c = keep.tile([P, NG, P], U32, name="fv8c", align_bytes=64)
+        fv8s = keep.tile([P, NG, P], U8, name="fv8s", align_bytes=64)
         wac = keep.tile([P, 2, NG, 256], U32, name="wac", align_bytes=64)
         was = keep.tile([P, 2, NG, 256], U8, name="was", align_bytes=64)
         wbc = keep.tile([P, C], U32, name="wbc", align_bytes=64)
@@ -120,59 +122,58 @@ def tile_joint_module_pb_kernel(tc, fv, ft, Wa, ba, Wb, bb, Wfc2, bfc2, out):
             else:
                 nc.vector.tensor_copy(out=dst, in_=src)
 
-        def conv1_pass(acc, g, j, c0, n):
+        fvw = {}
+
+        def pair_up(g, x0, q0=0, q1=128, eng="v"):
+            if g not in fvw:
+                fvw[g] = fvw_pool.tile([P, PIX, 128, 4], BF16, name="fvw")
+            rv = fv_raw[g][:].rearrange("p (q j x) -> p q x j", j=4, x=PIX)
+            wv = fvw[g][:].rearrange("p x q j -> p q x j")
+            copy(eng, wv[:, q0:q1, x0:x0 + 3], rv[:, q0:q1, x0:x0 + 3])
+
+        def tf_bank(places, dst, eng):
+            pb = tbank()
+            for i, (g, x) in enumerate(places):
+                ww = fvw[g][:, x].rearrange("p q j -> p (q j)").bitcast(F32)
+                for u in range(2):
+                    nc.tensor.transpose(
+                        pb[:, (2 * i + u) * P:(2 * i + u + 1) * P], ww[:, u * P:(u + 1) * P], ident[:]
+                    )
+            n = len(places)
+            copy(
+                eng,
+                dst.rearrange("p x b t -> p (x b t)").bitcast(F32).rearrange("p (x b u) -> p x b u", x=n, u=2),
+                pb[:, 0:2 * n * P].rearrange("p (x u b) -> p x b u", x=n, u=2),
+            )
+
+        def new_grp(n):
+            return grp_pool.tile([P, n, P, 4], BF16, name="grp%d" % n, tag="grp", align_bytes=64)
+
+        def fv_quantise(codes, scales, grp):
+            nc.vector.quantize_mx(
+                out=codes.bitcast(FP8X4), scales=scales, in_=grp.rearrange("p x b t -> p (x b t)")
+            )
+
+        def q_cols(g, x0, x1, grp):
+            c = slice(x0 * P, x1 * P)
+            fv_quantise(fvc[:, g, c], fvs[:, g, c], grp)
+
+        def conv1_pass(acc, j, g, codes, scales):
             sm, em = divmod(j, 2)
             nc.tensor.matmul_mx(
                 out=acc,
                 lhsT=wac[:, sm, g, em * P:(em + 1) * P].bitcast(FP8X4),
                 lhsT_scale=was[:, sm, g, em * P:(em + 1) * P],
-                rhs=fvc[:, g, c0:c0 + n].bitcast(FP8X4),
-                rhs_scale=fvs[:, g, c0:c0 + n],
+                rhs=codes.bitcast(FP8X4),
+                rhs_scale=scales,
                 start=g == 0,
                 stop=g == NG - 1,
             )
 
-        oddc = {}
-        last = {}
-
-        def shift_odd(g, pieces=((0, 256, 0, 4),), eng="s"):
-            rv = fv_raw[g][:].rearrange("p (v r) -> p v r", r=18)
-            oddc[g] = odd_pool.tile([P, 4, 256, 2], BF16, name="oddc")
-            last[g] = odd_pool.tile([P, 256, 2], BF16, name="last")
-            for v0, nv, a0, na in pieces:
-                v = slice(v0, v0 + nv)
-                nc.vector.tensor_copy(
-                    out=oddc[g][:, a0:a0 + na, v],
-                    in_=rv[:, v, 9 + 2 * a0:9 + 2 * (a0 + na)].rearrange("p v (a h) -> p a v h", h=2),
-                )
-            copy(eng, last[g][:], rv[:, :, 8:18:9])
-
-        def tf_bank(g, a, dst, eng):
-            pb = tbank()
-            fw = fv_raw[g][:].bitcast(F32)
-            ow = oddc[g][:, a].rearrange("p v h -> p (v h)").bitcast(F32)
-            for s in range(2):
-                st = s * 1152 + a
-                nc.tensor.transpose(pb[:, 2 * s * P:(2 * s + 1) * P], fw[:, st:st + 1144:9], ident[:])
-                nc.tensor.transpose(pb[:, (2 * s + 1) * P:(2 * s + 2) * P], ow[:, s * P:(s + 1) * P], ident[:])
-            copy(eng, dst, pb[:].bitcast(BF16).rearrange("p (t b h) -> p h b t", t=4, h=2))
-
-        def tf_last(g, dst, eng):
-            pb = tbank()
-            lw = last[g][:].rearrange("p v r -> p (v r)").bitcast(F32)
-            for s in range(2):
-                nc.tensor.transpose(pb[:, s * P:(s + 1) * P], lw[:, s * P:(s + 1) * P], ident[:])
-            copy(eng, dst.bitcast(F32), pb[:, 0:2 * P].rearrange("p (s b) -> p b s", s=2))
-
-        def fv_quantise(g, grp, parts):
-            gf = grp[:].rearrange("p x b t -> p (x b t)")
-            first = parts[0][0]
-            for c0, n in parts:
-                nc.vector.quantize_mx(
-                    out=fvc[:, g, c0:c0 + n].bitcast(FP8X4),
-                    scales=fvs[:, g, c0:c0 + n],
-                    in_=gf[:, 4 * (c0 - first):4 * (c0 - first + n)],
-                )
+        def conv1_run(accs, g, x0):
+            c = slice(x0 * P, (x0 + 4) * P)
+            for j in range(4):
+                conv1_pass(accs[j][:], j, g, fvc[:, g, c], fvs[:, g, c])
 
         wags = {}
 
@@ -188,12 +189,12 @@ def tile_joint_module_pb_kernel(tc, fv, ft, Wa, ba, Wb, bb, Wfc2, bfc2, out):
                     nc.tensor.transpose(pb[:, slot * P:(slot + 1) * P], ww[:, em, c0:c0 + P], ident[:])
             copy(eng, wags[i][:, g2], pb[:].rearrange("p (e s q) -> p e q s", e=2, s=2))
 
-        def wa_quantise(i, wag):
+        def wa_quantise(i):
             sm, gp = i % 2, i // 2
             nc.vector.quantize_mx(
                 out=wac[:, sm, 2 * gp:2 * gp + 2, :].rearrange("p g w -> p (g w)").bitcast(FP8X4),
                 scales=was[:, sm, 2 * gp:2 * gp + 2, :].rearrange("p g w -> p (g w)"),
-                in_=wag[:].rearrange("p g e q s -> p (g e q s)").bitcast(BF16),
+                in_=wags[i][:].rearrange("p g e q s -> p (g e q s)").bitcast(BF16),
             )
 
         wf_e = wfT[:].bitcast(BF16).rearrange("p k (o e) -> p k o e", e=2)
@@ -215,15 +216,15 @@ def tile_joint_module_pb_kernel(tc, fv, ft, Wa, ba, Wb, bb, Wfc2, bfc2, out):
                     nc.tensor.transpose(pb[:, slot * P:(slot + 1) * P], ww[:, tl, k * P:(k + 1) * P], ident[:])
             copy(eng, wfT[:, 2 * h:2 * h + 2, i * 256:(i + 1) * 256], pb[:].rearrange("p (k o) -> p k o", k=2))
 
-        def fc_half(i, h, eng):
+        def fc_quarter(i, eng):
             acc = tbank()
-            cols = slice(i * 256 + h * P, i * 256 + (h + 1) * P)
+            cols = slice(i * 256, (i + 1) * 256)
             for idx in range(8):
                 k, e = divmod(idx, 2)
                 nc.tensor.matmul(
-                    out=acc[:, 0:P], lhsT=ftT[:, k, e], rhs=wf_e[:, k, cols, e], start=idx == 0, stop=idx == 7
+                    out=acc[:, 0:256], lhsT=ftT[:, k, e], rhs=wf_e[:, k, cols, e], start=idx == 0, stop=idx == 7
                 )
-            copy(eng, ft2[:, cols], acc[:, 0:P])
+            copy(eng, ft2[:, cols], acc[:, 0:256])
 
         def wb_unit(i, engs):
             ww = wb_raw[i][:].bitcast(F32)
@@ -274,27 +275,25 @@ def tile_joint_module_pb_kernel(tc, fv, ft, Wa, ba, Wb, bb, Wfc2, bfc2, out):
         def acc_banks():
             return [psum.tile([P, 512], F32, name="acc%d" % j, tag="acc%d" % j) for j in range(4)]
 
-        def late_pixels(g, engs):
-            grp = grp_pool.tile([P, 3, P, 4], BF16, name="grp2", tag="grp", align_bytes=64)
-            tf_bank(g, 3, grp[:, 0:2], engs[0])
-            tf_last(g, grp[:, 2], engs[1])
-            return grp
-
-        def late_pixels(g, eng):
-            late = grp_pool.tile([P, 5, P, 4], BF16, name="late", tag="grp", align_bytes=64)
-            tf_bank(g, 2, late[:, 0:2], "s")
-            tf_bank(g, 3, late[:, 2:4], eng)
-            tf_last(g, late[:, 4], "s")
-            return late
-
         acc0 = acc_banks()
-        shift_odd(0, ((0, 128, 0, 4), (128, 128, 0, 1), (128, 128, 1, 1), (128, 128, 2, 2)), "v")
+        mids = {}
+        lates = {}
+
+        def late67(g, eng):
+            lates[g] = new_grp(2)
+            tf_bank([(g, 6), (g, 7)], lates[g][:], eng)
+
+        for q0 in (0, 64):
+            for x0 in (0, 3, 6):
+                pair_up(0, x0, q0, q0 + 64)
         for g in range(NG):
-            grp = grp_pool.tile([P, 4, P, 4], BF16, name="grp", tag="grp", align_bytes=64)
-            tf_bank(g, 0, grp[:, 0:2], "s")
-            tf_bank(g, 1, grp[:, 2:4], "v")
+            early = new_grp(4)
+            tf_bank([(g, 0), (g, 1)], early[:, 0:2], "s")
+            tf_bank([(g, 2), (g, 3)], early[:, 2:4], "s")
+            mids[g] = new_grp(2)
             if g == 0:
-                late = late_pixels(0, "v")
+                tf_bank([(g, 4), (g, 5)], mids[g][:], "s")
+                late67(0, "s")
                 nc.vector.tensor_copy(out=ba_f[:], in_=ba_raw[:])
                 wa_part(0, 0, "s")
                 wa_part(0, 1, "s")
@@ -303,50 +302,74 @@ def tile_joint_module_pb_kernel(tc, fv, ft, Wa, ba, Wb, bb, Wfc2, bfc2, out):
                 wf_part(0, 1, "s")
                 wa_part(1, 0, "s")
                 wa_part(1, 1, "s")
-                fv_quantise(g, grp, ((0, 512),))
-                shift_odd(1)
-                fv_quantise(g, late, ((512, 512), (1024, 128)))
-                wa_quantise(0, wags[0])
-                wa_quantise(1, wags[1])
+                q_cols(g, 0, 4, early[:])
+                pair_up(1, 0)
+                pair_up(1, 3)
+                q_cols(g, 4, 6, mids[g][:])
+                q_cols(g, 6, 8, lates[g][:])
+                pair_up(1, 6)
+                wa_quantise(0)
+                wa_quantise(1)
                 continue
-            for j in range(4):
-                conv1_pass(acc0[j][:], g - 1, j, 0, 512)
             if g + 1 < NG:
+                pair_up(g + 1, 0)
+                pair_up(g + 1, 3)
                 wa_part(g + 1, 0, "s")
-                fc_half(g - 1, 0, "s")
-                if g < 4:
-                    wf_part(g, 0, "s")
                 wa_part(g + 1, 1, "s")
-                shift_odd(g + 1)
-            fv_quantise(g, grp, ((0, 512),))
+            conv1_run(acc0, g - 1, 0)
+            q_cols(g, 0, 4, early[:])
+            if g < 4:
+                wf_part(g, 0, "s")
+                wf_part(g, 1, "v")
+            if g - 1 < 4:
+                fc_quarter(g - 1, "s")
+            tf_bank([(g, 4), (g, 5)], mids[g][:], "s")
             if g + 1 < NG:
-                if g < 4:
-                    wf_part(g, 1, "v")
-                fc_half(g - 1, 1, "v")
-                wa_quantise(g + 1, wags[g + 1])
+                pair_up(g + 1, 6)
+                wa_quantise(g + 1)
+            q_cols(g, 4, 6, mids[g][:])
 
-        for g in range(1, NG):
-            late = late_pixels(g, "s" if g in (2, 3) else "v")
-            if g == 1:
-                for j in range(4):
-                    conv1_pass(acc0[j][:], NG - 1, j, 0, 512)
-                hp0 = grp_pool.tile([P, 4, 512], BF16, name="hp0", tag="grp", align_bytes=64)
-                for j in range(4):
-                    h_out("sv"[j % 2], hp0, acc0[j][:], j, 512)
-                acc1 = acc_banks()
-            fv_quantise(g, late, ((512, 512), (1024, 128)))
-            if g == 1:
-                hg0 = grp_pool.tile([P, 512, 4], BF16, name="hg0", tag="grp", align_bytes=64)
-                h_regroup(hp0, hg0, 0, 256)
-                h_regroup(hp0, hg0, 256, 256)
-                h_quantise(hg0, 0, 0, 512)
-            else:
-                for j in range(4):
-                    conv1_pass(acc1[j][:], g - 2, j, 512, 512)
-        wbgs = [wb_unit(i, "sv") for i in range(2)]
+        def late8(g, eng):
+            lates[8, g] = new_grp(2)
+            tf_bank([(g, 8), (g + 1, 8)], lates[8, g][:], eng)
+
+        def q_late8(g):
+            fv_quantise(
+                fv8c[:, g:g + 2].rearrange("p g w -> p (g w)"),
+                fv8s[:, g:g + 2].rearrange("p g w -> p (g w)"),
+                lates[8, g][:],
+            )
+
+        late67(1, "s")
+        late67(2, "v")
+        late67(3, "s")
+        late8(0, "v")
+        q_cols(1, 6, 8, lates[1][:])
+        conv1_run(acc0, NG - 1, 0)
+        hp0 = grp_pool.tile([P, 4, 512], BF16, name="hp0", tag="grp", align_bytes=64)
+        for j in range(4):
+            h_out("sv"[j % 2], hp0, acc0[j][:], j, 512)
+        q_cols(2, 6, 8, lates[2][:])
+        q_cols(3, 6, 8, lates[3][:])
+        late67(4, "s")
+        late67(5, "s")
+        late8(2, "s")
+        late8(4, "s")
+        acc1 = acc_banks()
+        q_late8(0)
+        q_cols(4, 6, 8, lates[4][:])
+        for g in range(NG - 2):
+            conv1_run(acc1, g, 4)
+        q_cols(5, 6, 8, lates[5][:])
+        hg0 = grp_pool.tile([P, 512, 4], BF16, name="hg0", tag="grp", align_bytes=64)
+        h_regroup(hp0, hg0, 0, 256)
+        h_regroup(hp0, hg0, 256, 256)
+        h_quantise(hg0, 0, 0, 512)
+        q_late8(2)
+        q_late8(4)
+        wbgs = [wb_unit(i, "ss") for i in range(2)]
         for g in (NG - 2, NG - 1):
-            for j in range(4):
-                conv1_pass(acc1[j][:], g, j, 512, 512)
+            conv1_run(acc1, g, 4)
         for i in range(2):
             wb_quantise(i, wbgs[i])
 
@@ -357,7 +380,7 @@ def tile_joint_module_pb_kernel(tc, fv, ft, Wa, ba, Wb, bb, Wfc2, bfc2, out):
         acc2 = psum.tile([P, 512], F32, name="acc2", tag="tr0")
         for j in range(4):
             for g in range(NG):
-                conv1_pass(acc2[:, j * P:(j + 1) * P], g, j, 1024, P)
+                conv1_pass(acc2[:, j * P:(j + 1) * P], j, g, fv8c[:, g], fv8s[:, g])
         h_regroup(hp1, hg1, 0, 256)
         h_regroup(hp1, hg1, 256, 256)
         h_quantise(hg1, 512, 0, 256)

@@ -25,9 +25,11 @@ def tile_joint_module_pb_kernel(tc, fv, ft, Wa, ba, Wb, bb, Wfc2, bfc2, out):
         const = ctx.enter_context(tc.tile_pool(name="const", bufs=1))
         keep = ctx.enter_context(tc.tile_pool(name="keep", bufs=1))
         fvraw_pool = ctx.enter_context(tc.tile_pool(name="fvraw", bufs=4))
-        fvw_pool = ctx.enter_context(tc.tile_pool(name="fvw", bufs=6))
-        wraw_pool = ctx.enter_context(tc.tile_pool(name="wraw", bufs=4))
-        grp_pool = ctx.enter_context(tc.tile_pool(name="grp", bufs=6))
+        fvw_pool = ctx.enter_context(tc.tile_pool(name="fvw", bufs=3))
+        wraw_pool = ctx.enter_context(tc.tile_pool(name="wraw", bufs=5))
+        grp_pool = ctx.enter_context(tc.tile_pool(name="grp", bufs=4))
+        mid_pool = ctx.enter_context(tc.tile_pool(name="mid", bufs=NG))
+        last_pool = ctx.enter_context(tc.tile_pool(name="last", bufs=NG // 2))
         wag_pool = ctx.enter_context(tc.tile_pool(name="wag", bufs=3))
         psum = ctx.enter_context(tc.psum_pool(name="ps", bufs=1))
         ctx.enter_context(tc.manual_schedule())
@@ -93,17 +95,17 @@ def tile_joint_module_pb_kernel(tc, fv, ft, Wa, ba, Wb, bb, Wfc2, bfc2, out):
             wb_raw[i] = wraw_pool.tile([P, 4, 512], BF16, name="wbr", tag="wr")
             nc.sync.dma_start(out=wb_raw[i][:], in_=wb_view[:, 4 * i:4 * i + 4, :])
 
-        load_fv(0, parts=2)
+        load_fv(0, parts=4)
         load_wa(0)
+        load_fv(1)
+        load_wa(1)
         nc.sync.dma_start(out=ft_raw[:], in_=ft)
         load_wf(0)
-        load_wa(1)
-        load_fv(1)
         for g in range(2, NG):
-            if g <= 4:
-                load_wf(g - 1)
             load_wa(g)
             load_fv(g)
+            if g <= 4:
+                load_wf(g - 1)
         load_wb(0)
         load_wb(1)
         nc.sync.dma_start(out=bfc_bc[:], in_=bfc2.partition_broadcast(P))
@@ -131,14 +133,18 @@ def tile_joint_module_pb_kernel(tc, fv, ft, Wa, ba, Wb, bb, Wfc2, bfc2, out):
             wv = fvw[g][:].rearrange("p x q j -> p q x j")
             copy(eng, wv[:, q0:q1, x0:x0 + 3], rv[:, q0:q1, x0:x0 + 3])
 
-        def tf_bank(places, dst, eng):
-            pb = tbank()
+        def tf_half(pb, places, u):
             for i, (g, x) in enumerate(places):
                 ww = fvw[g][:, x].rearrange("p q j -> p (q j)").bitcast(F32)
-                for u in range(2):
-                    nc.tensor.transpose(
-                        pb[:, (2 * i + u) * P:(2 * i + u + 1) * P], ww[:, u * P:(u + 1) * P], ident[:]
-                    )
+                nc.tensor.transpose(pb[:, (2 * i + u) * P:(2 * i + u + 1) * P], ww[:, u * P:(u + 1) * P], ident[:])
+
+        def tf_bank(places, dst, eng):
+            pb = tbank()
+            for u in range(2):
+                tf_half(pb, places, u)
+            tf_out(pb, places, dst, eng)
+
+        def tf_out(pb, places, dst, eng):
             n = len(places)
             copy(
                 eng,
@@ -146,8 +152,8 @@ def tile_joint_module_pb_kernel(tc, fv, ft, Wa, ba, Wb, bb, Wfc2, bfc2, out):
                 pb[:, 0:2 * n * P].rearrange("p (x u b) -> p x b u", x=n, u=2),
             )
 
-        def new_grp(n):
-            return grp_pool.tile([P, n, P, 4], BF16, name="grp%d" % n, tag="grp", align_bytes=64)
+        def new_grp(pool, n):
+            return pool.tile([P, n, P, 4], BF16, name="grp%d" % n, tag="grp", align_bytes=64)
 
         def fv_quantise(codes, scales, grp):
             nc.vector.quantize_mx(
@@ -277,99 +283,78 @@ def tile_joint_module_pb_kernel(tc, fv, ft, Wa, ba, Wb, bb, Wfc2, bfc2, out):
 
         acc0 = acc_banks()
         mids = {}
-        lates = {}
+        lasts = {}
 
-        def late67(g, eng):
-            lates[g] = new_grp(2)
-            tf_bank([(g, 6), (g, 7)], lates[g][:], eng)
-
-        for q0 in (0, 64):
-            for x0 in (0, 3, 6):
-                pair_up(0, x0, q0, q0 + 64)
-        for g in range(NG):
-            early = new_grp(4)
-            tf_bank([(g, 0), (g, 1)], early[:, 0:2], "s")
-            tf_bank([(g, 2), (g, 3)], early[:, 2:4], "s")
-            mids[g] = new_grp(2)
-            if g == 0:
-                tf_bank([(g, 4), (g, 5)], mids[g][:], "s")
-                late67(0, "s")
-                nc.vector.tensor_copy(out=ba_f[:], in_=ba_raw[:])
-                wa_part(0, 0, "s")
-                wa_part(0, 1, "s")
-                ft_unit("s")
-                wf_part(0, 0, "s")
-                wf_part(0, 1, "s")
-                wa_part(1, 0, "s")
-                wa_part(1, 1, "s")
-                q_cols(g, 0, 4, early[:])
-                pair_up(1, 0)
-                pair_up(1, 3)
-                q_cols(g, 4, 6, mids[g][:])
-                q_cols(g, 6, 8, lates[g][:])
-                pair_up(1, 6)
-                wa_quantise(0)
-                wa_quantise(1)
-                continue
-            if g + 1 < NG:
-                pair_up(g + 1, 0)
-                pair_up(g + 1, 3)
-                wa_part(g + 1, 0, "s")
-                wa_part(g + 1, 1, "s")
-            conv1_run(acc0, g - 1, 0)
-            q_cols(g, 0, 4, early[:])
-            if g < 4:
-                wf_part(g, 0, "s")
-                wf_part(g, 1, "v")
-            if g - 1 < 4:
-                fc_quarter(g - 1, "s")
-            tf_bank([(g, 4), (g, 5)], mids[g][:], "s")
-            if g + 1 < NG:
-                pair_up(g + 1, 6)
-                wa_quantise(g + 1)
-            q_cols(g, 4, 6, mids[g][:])
-
-        def late8(g, eng):
-            lates[8, g] = new_grp(2)
-            tf_bank([(g, 8), (g + 1, 8)], lates[8, g][:], eng)
-
-        def q_late8(g):
+        def q_last(g):
             fv_quantise(
                 fv8c[:, g:g + 2].rearrange("p g w -> p (g w)"),
                 fv8s[:, g:g + 2].rearrange("p g w -> p (g w)"),
-                lates[8, g][:],
+                lasts[g][:],
             )
 
-        late67(1, "s")
-        late67(2, "v")
-        late67(3, "s")
-        late8(0, "v")
-        q_cols(1, 6, 8, lates[1][:])
+        for q0, q1 in ((0, 32), (32, 64), (64, 128)):
+            for x0 in (0, 3, 6):
+                pair_up(0, x0, q0, q1)
+        for g in range(NG):
+            more = g + 1 < NG
+            early = new_grp(grp_pool, 4)
+            mids[g] = new_grp(mid_pool, 4)
+            pairs = [[(g, x), (g, x + 1)] for x in range(0, 8, 2)]
+            dsts = [early[:, 0:2], early[:, 2:4], mids[g][:, 0:2], mids[g][:, 2:4]]
+            if g == 0:
+                banks = [tbank() for i in range(4)]
+                for u in range(2):
+                    for i in range(4):
+                        tf_half(banks[i], pairs[i], u)
+                for i in range(4):
+                    tf_out(banks[i], pairs[i], dsts[i], "s")
+            else:
+                for i in range(4):
+                    tf_bank(pairs[i], dsts[i], "s")
+            if more:
+                pair_up(g + 1, 0)
+                pair_up(g + 1, 3)
+            q_cols(g, 0, 4, early[:])
+            if g == 0:
+                wa_part(0, 0, "s")
+                wa_part(0, 1, "s")
+                wa_quantise(0)
+            else:
+                conv1_run(acc0, g - 1, 0)
+            if more:
+                wa_part(g + 1, 0, "s")
+                wa_part(g + 1, 1, "s")
+                pair_up(g + 1, 6)
+                wa_quantise(g + 1)
+            if g == 0:
+                ft_unit("s")
+            if g < 4:
+                wf_part(g, 0, "s")
+                wf_part(g, 1, "s")
+            if 0 < g < 5:
+                fc_quarter(g - 1, "s")
+            if g % 2:
+                lasts[g - 1] = new_grp(last_pool, 2)
+                tf_bank([(g - 1, 8), (g, 8)], lasts[g - 1][:], "s")
         conv1_run(acc0, NG - 1, 0)
+        nc.vector.tensor_copy(out=ba_f[:], in_=ba_raw[:])
         hp0 = grp_pool.tile([P, 4, 512], BF16, name="hp0", tag="grp", align_bytes=64)
+        q_cols(0, 4, 8, mids[0][:])
+        q_cols(1, 4, 8, mids[1][:])
         for j in range(4):
             h_out("sv"[j % 2], hp0, acc0[j][:], j, 512)
-        q_cols(2, 6, 8, lates[2][:])
-        q_cols(3, 6, 8, lates[3][:])
-        late67(4, "s")
-        late67(5, "s")
-        late8(2, "s")
-        late8(4, "s")
+        wbgs = [wb_unit(i, "ss") for i in range(2)]
         acc1 = acc_banks()
-        q_late8(0)
-        q_cols(4, 6, 8, lates[4][:])
-        for g in range(NG - 2):
+        for g in range(2, NG):
+            q_cols(g, 4, 8, mids[g][:])
+        for g in range(NG):
             conv1_run(acc1, g, 4)
-        q_cols(5, 6, 8, lates[5][:])
+        for g in range(0, NG, 2):
+            q_last(g)
         hg0 = grp_pool.tile([P, 512, 4], BF16, name="hg0", tag="grp", align_bytes=64)
         h_regroup(hp0, hg0, 0, 256)
         h_regroup(hp0, hg0, 256, 256)
         h_quantise(hg0, 0, 0, 512)
-        q_late8(2)
-        q_late8(4)
-        wbgs = [wb_unit(i, "ss") for i in range(2)]
-        for g in (NG - 2, NG - 1):
-            conv1_run(acc1, g, 4)
         for i in range(2):
             wb_quantise(i, wbgs[i])
 
@@ -430,8 +415,7 @@ def tile_joint_module_pb_kernel(tc, fv, ft, Wa, ba, Wb, bb, Wfc2, bfc2, out):
             )
             nc.sync.dma_start(out=out[:, c0:c0 + n], in_=z[:, c0:c0 + n])
 
-        gate_in(0)
-        for i in range(1, len(parts)):
+        for i in range(len(parts)):
             gate_in(i)
-            gate_out(i - 1)
-        gate_out(len(parts) - 1)
+        for i in range(len(parts)):
+            gate_out(i)

@@ -25,7 +25,8 @@ def tile_joint_module_pb_kernel(tc, fv, ft, Wa, ba, Wb, bb, Wfc2, bfc2, out):
         const = ctx.enter_context(tc.tile_pool(name="const", bufs=1))
         keep = ctx.enter_context(tc.tile_pool(name="keep", bufs=1))
         fvraw_pool = ctx.enter_context(tc.tile_pool(name="fvraw", bufs=4))
-        fvw_pool = ctx.enter_context(tc.tile_pool(name="fvw", bufs=3))
+        fvw_pool = ctx.enter_context(tc.tile_pool(name="fvw", bufs=2))
+        fvl_pool = ctx.enter_context(tc.tile_pool(name="fvl", bufs=NG))
         wraw_pool = ctx.enter_context(tc.tile_pool(name="wraw", bufs=5))
         grp_pool = ctx.enter_context(tc.tile_pool(name="grp", bufs=4))
         mid_pool = ctx.enter_context(tc.tile_pool(name="mid", bufs=NG))
@@ -127,15 +128,15 @@ def tile_joint_module_pb_kernel(tc, fv, ft, Wa, ba, Wb, bb, Wfc2, bfc2, out):
         fvw = {}
 
         def pair_up(g, x0, q0=0, q1=128, eng="v"):
-            if g not in fvw:
-                fvw[g] = fvw_pool.tile([P, PIX, 128, 4], BF16, name="fvw")
+            if (g, x0) not in fvw:
+                fvw[g, x0] = (fvl_pool if x0 == 6 else fvw_pool).tile([P, 3, 128, 4], BF16, name="fvw", tag="fvw%d" % x0)
             rv = fv_raw[g][:].rearrange("p (q j x) -> p q x j", j=4, x=PIX)
-            wv = fvw[g][:].rearrange("p x q j -> p q x j")
-            copy(eng, wv[:, q0:q1, x0:x0 + 3], rv[:, q0:q1, x0:x0 + 3])
+            wv = fvw[g, x0][:].rearrange("p x q j -> p q x j")
+            copy(eng, wv[:, q0:q1], rv[:, q0:q1, x0:x0 + 3])
 
         def tf_half(pb, places, u):
             for i, (g, x) in enumerate(places):
-                ww = fvw[g][:, x].rearrange("p q j -> p (q j)").bitcast(F32)
+                ww = fvw[g, x - x % 3][:, x % 3].rearrange("p q j -> p (q j)").bitcast(F32)
                 nc.tensor.transpose(pb[:, (2 * i + u) * P:(2 * i + u + 1) * P], ww[:, u * P:(u + 1) * P], ident[:])
 
         def tf_bank(places, dst, eng):
@@ -333,9 +334,6 @@ def tile_joint_module_pb_kernel(tc, fv, ft, Wa, ba, Wb, bb, Wfc2, bfc2, out):
                 wf_part(g, 1, "s")
             if 0 < g < 5:
                 fc_quarter(g - 1, "s")
-            if g % 2:
-                lasts[g - 1] = new_grp(last_pool, 2)
-                tf_bank([(g - 1, 8), (g, 8)], lasts[g - 1][:], "s")
         conv1_run(acc0, NG - 1, 0)
         nc.vector.tensor_copy(out=ba_f[:], in_=ba_raw[:])
         hp0 = grp_pool.tile([P, 4, 512], BF16, name="hp0", tag="grp", align_bytes=64)
@@ -343,11 +341,16 @@ def tile_joint_module_pb_kernel(tc, fv, ft, Wa, ba, Wb, bb, Wfc2, bfc2, out):
         q_cols(1, 4, 8, mids[1][:])
         for j in range(4):
             h_out("sv"[j % 2], hp0, acc0[j][:], j, 512)
-        wbgs = [wb_unit(i, "ss") for i in range(2)]
+        for g in range(0, NG, 2):
+            lasts[g] = new_grp(last_pool, 2)
+            tf_bank([(g, 8), (g + 1, 8)], lasts[g][:], "s")
         acc1 = acc_banks()
         for g in range(2, NG):
             q_cols(g, 4, 8, mids[g][:])
-        for g in range(NG):
+        for g in range(3):
+            conv1_run(acc1, g, 4)
+        wbgs = [wb_unit(i, "ss") for i in range(2)]
+        for g in range(3, NG):
             conv1_run(acc1, g, 4)
         for g in range(0, NG, 2):
             q_last(g)
@@ -378,8 +381,8 @@ def tile_joint_module_pb_kernel(tc, fv, ft, Wa, ba, Wb, bb, Wfc2, bfc2, out):
         h_quantise(hg2, 1024, 0, P)
         nc.vector.tensor_tensor(out=ft2[:], in0=ft2[:], in1=bfc_bc[:], op=ALU.add)
 
-        parts = ((0, 512), (512, 256), (768, 256))
-        gacc = [psum.tile([P, 512], F32, name="g%d" % i, tag="tr%d" % (i + 1)) for i in range(len(parts))]
+        parts = ((0, 256), (256, 256), (512, 256), (768, 256))
+        gacc = [psum.tile([P, 512], F32, name="g%d" % i, tag="tr%d" % (i + 1) if i < 3 else "acc%d" % (i - 3)) for i in range(len(parts))]
 
         def conv2_pass(i, x):
             c0, n = parts[i]
@@ -415,7 +418,8 @@ def tile_joint_module_pb_kernel(tc, fv, ft, Wa, ba, Wb, bb, Wfc2, bfc2, out):
             )
             nc.sync.dma_start(out=out[:, c0:c0 + n], in_=z[:, c0:c0 + n])
 
-        for i in range(len(parts)):
-            gate_in(i)
-        for i in range(len(parts)):
-            gate_out(i)
+        for i in range(len(parts) + 1):
+            if i < len(parts):
+                gate_in(i)
+            if i >= 1:
+                gate_out(i - 1)

@@ -102,11 +102,17 @@ def tile_joint_module_pb_kernel(tc, fv, ft, Wa, ba, Wb, bb, Wfc2, bfc2, out):
         load_wa(1)
         nc.sync.dma_start(out=ft_raw[:], in_=ft)
         load_wf(0)
-        for g in range(2, NG):
-            load_wa(g)
-            load_fv(g)
-            if g <= 4:
-                load_wf(g - 1)
+        load_fv(2)
+        load_wa(2)
+        load_wf(1)
+        load_fv(3)
+        load_wa(3)
+        load_wf(2)
+        load_fv(4)
+        load_wa(4)
+        load_wf(3)
+        load_fv(5)
+        load_wa(5)
         load_wb(0)
         load_wb(1)
         nc.sync.dma_start(out=bfc_bc[:], in_=bfc2.partition_broadcast(P))
@@ -133,6 +139,12 @@ def tile_joint_module_pb_kernel(tc, fv, ft, Wa, ba, Wb, bb, Wfc2, bfc2, out):
             rv = fv_raw[g][:].rearrange("p (q j x) -> p q x j", j=4, x=PIX)
             wv = fvw[g, x0][:].rearrange("p x q j -> p q x j")
             copy(eng, wv[:, q0:q1], rv[:, q0:q1, x0:x0 + 3])
+
+        def keep_warm(n):
+            pb = psum.tile([P, 512], F32, name="warm", tag="acc3")
+            iv = ident[:].bitcast(BF16)
+            for i in range(n):
+                nc.tensor.matmul(out=pb[:, 0:256], lhsT=iv[:, 0:P], rhs=iv, start=True, stop=True)
 
         def tf_half(pb, places, u):
             for i, (g, x) in enumerate(places):
@@ -282,7 +294,6 @@ def tile_joint_module_pb_kernel(tc, fv, ft, Wa, ba, Wb, bb, Wfc2, bfc2, out):
         def acc_banks():
             return [psum.tile([P, 512], F32, name="acc%d" % j, tag="acc%d" % j) for j in range(4)]
 
-        acc0 = acc_banks()
         mids = {}
         lasts = {}
 
@@ -307,33 +318,45 @@ def tile_joint_module_pb_kernel(tc, fv, ft, Wa, ba, Wb, bb, Wfc2, bfc2, out):
                 for u in range(2):
                     for i in range(4):
                         tf_half(banks[i], pairs[i], u)
+                        pass
                 for i in range(4):
                     tf_out(banks[i], pairs[i], dsts[i], "s")
-            else:
-                for i in range(4):
-                    tf_bank(pairs[i], dsts[i], "s")
-            if more:
-                pair_up(g + 1, 0)
-                pair_up(g + 1, 3)
-            q_cols(g, 0, 4, early[:])
-            if g == 0:
+                pair_up(1, 0)
+                pair_up(1, 3)
+                q_cols(0, 0, 4, early[:])
                 wa_part(0, 0, "s")
                 wa_part(0, 1, "s")
+                keep_warm(8)
                 wa_quantise(0)
-            else:
-                conv1_run(acc0, g - 1, 0)
-            if more:
-                wa_part(g + 1, 0, "s")
-                wa_part(g + 1, 1, "s")
-                pair_up(g + 1, 6)
-                wa_quantise(g + 1)
-            if g == 0:
+                wa_part(1, 0, "s")
+                wa_part(1, 1, "s")
+                pair_up(1, 6)
+                wa_quantise(1)
                 ft_unit("s")
-            if g < 4:
-                wf_part(g, 0, "s")
-                wf_part(g, 1, "s")
-            if 0 < g < 5:
-                fc_quarter(g - 1, "s")
+                keep_warm(4)
+                wf_part(0, 0, "s")
+                wf_part(0, 1, "s")
+                keep_warm(4)
+            else:
+                if g == 1:
+                    acc0 = acc_banks()
+                for i in range(4):
+                    tf_bank(pairs[i], dsts[i], "s")
+                if more:
+                    pair_up(g + 1, 0)
+                    pair_up(g + 1, 3)
+                q_cols(g, 0, 4, early[:])
+                conv1_run(acc0, g - 1, 0)
+                if more:
+                    wa_part(g + 1, 0, "s")
+                    wa_part(g + 1, 1, "s")
+                    pair_up(g + 1, 6)
+                    wa_quantise(g + 1)
+                if g < 4:
+                    wf_part(g, 0, "s")
+                    wf_part(g, 1, "s")
+                if g < 5:
+                    fc_quarter(g - 1, "s")
         conv1_run(acc0, NG - 1, 0)
         nc.vector.tensor_copy(out=ba_f[:], in_=ba_raw[:])
         hp0 = grp_pool.tile([P, 4, 512], BF16, name="hp0", tag="grp", align_bytes=64)

@@ -48,19 +48,19 @@ def tile_joint_module_pb_kernel(tc, fv, ft, Wa, ba, Wb, bb, Wfc2, bfc2, out):
         nc.vector.memset(warm_in[:], 0.0)
         nc.scalar.activation(out=warm_out[:], in_=warm_in[:], func=ACT.Sigmoid)
 
-        fvc = keep.tile([P, NG, 1024], U32, name="fvc", align_bytes=64)
-        fvs = keep.tile([P, NG, 1024], U8, name="fvs", align_bytes=64)
-        fv8c = keep.tile([P, NG, P], U32, name="fv8c", align_bytes=64)
-        fv8s = keep.tile([P, NG, P], U8, name="fv8s", align_bytes=64)
-        wac = keep.tile([P, 2, NG, 256], U32, name="wac", align_bytes=64)
-        was = keep.tile([P, 2, NG, 256], U8, name="was", align_bytes=64)
-        wbc = keep.tile([P, C], U32, name="wbc", align_bytes=64)
-        wbs = keep.tile([P, C], U8, name="wbs", align_bytes=64)
+        fvc = keep.tile([P, NG, 1024], U32, name="fvc", align_bytes=256)
+        fvs = keep.tile([P, NG, 1024], U8, name="fvs", align_bytes=256)
+        fv8c = keep.tile([P, NG, P], U32, name="fv8c", align_bytes=256)
+        fv8s = keep.tile([P, NG, P], U8, name="fv8s", align_bytes=256)
+        wac = keep.tile([P, 2, NG, 256], U32, name="wac", align_bytes=256)
+        was = keep.tile([P, 2, NG, 256], U8, name="was", align_bytes=256)
+        wbc = keep.tile([P, C], U32, name="wbc", align_bytes=256)
+        wbs = keep.tile([P, C], U8, name="wbs", align_bytes=256)
         wfT = keep.tile([P, 4, C], F32, name="wfT")
         ftT = keep.tile([P, 4, 2, P], BF16, name="ftT")
         ft2 = keep.tile([P, C], F32, name="ft2")
-        hc = keep.tile([P, COLS], U32, name="hc", align_bytes=64)
-        hs = keep.tile([P, COLS], U8, name="hs", align_bytes=64)
+        hc = keep.tile([P, COLS], U32, name="hc", align_bytes=256)
+        hs = keep.tile([P, COLS], U8, name="hs", align_bytes=256)
         z = keep.tile([P, C], F32, name="z")
         ft_raw = const.tile([P, C], BF16, name="ft_raw")
         bfc_bc = const.tile([P, C], BF16, name="bfc_bc")
@@ -136,9 +136,9 @@ def tile_joint_module_pb_kernel(tc, fv, ft, Wa, ba, Wb, bb, Wfc2, bfc2, out):
         def pair_up(g, x0, q0=0, q1=128, eng="v"):
             if (g, x0) not in fvw:
                 fvw[g, x0] = (fvl_pool if x0 == 6 else fvw_pool).tile([P, 3, 128, 4], BF16, name="fvw", tag="fvw%d" % x0)
-            rv = fv_raw[g][:].rearrange("p (q j x) -> p q x j", j=4, x=PIX)
-            wv = fvw[g, x0][:].rearrange("p x q j -> p q x j")
-            copy(eng, wv[:, q0:q1], rv[:, q0:q1, x0:x0 + 3])
+            rv = fv_raw[g][:].rearrange("p (q j x) -> p q j x", j=4, x=PIX)
+            wv = fvw[g, x0][:].rearrange("p x q j -> p q j x")
+            copy(eng, wv[:, q0:q1], rv[:, q0:q1, :, x0:x0 + 3])
 
         def keep_warm(n):
             pb = psum.tile([P, 512], F32, name="warm", tag="acc3")

@@ -39,10 +39,6 @@ def tile_joint_module_pb_kernel(tc, fv, ft, Wa, ba, Wb, bb, Wfc2, bfc2, out):
         make_identity(nc, ident[:])
         ba_raw = const.tile([P, 4], BF16, name="ba_raw")
         ba_f = const.tile([P, 4], F32, name="ba_f")
-        nc.scalar.dma_start(
-            out=ba_raw[:].rearrange("p (s e) -> p s e", s=2),
-            in_=ba.rearrange("(s p e) -> p s e", s=2, e=2),
-        )
         warm_in = const.tile([P, 1], F32, name="warm_in")
         warm_out = const.tile([P, 1], F32, name="warm_out")
         nc.vector.memset(warm_in[:], 0.0)
@@ -113,6 +109,10 @@ def tile_joint_module_pb_kernel(tc, fv, ft, Wa, ba, Wb, bb, Wfc2, bfc2, out):
         load_wf(3)
         load_fv(5)
         load_wa(5)
+        nc.sync.dma_start(
+            out=ba_raw[:].rearrange("p (s e) -> p s e", s=2),
+            in_=ba.rearrange("(s p e) -> p s e", s=2, e=2),
+        )
         load_wb(0)
         load_wb(1)
         nc.sync.dma_start(out=bfc_bc[:], in_=bfc2.partition_broadcast(P))
@@ -426,23 +426,26 @@ def tile_joint_module_pb_kernel(tc, fv, ft, Wa, ba, Wb, bb, Wfc2, bfc2, out):
             for x in range(4, PIX):
                 conv2_pass(i, x)
 
-        def gate_in(i):
-            c0, n = parts[i]
+        pieces = [(i, 0, 256) for i in range(3)] + [(3, 0, P), (3, P, P)]
+
+        def gate_in(i, o, n):
+            c0 = parts[i][0] + o
             nc.vector.scalar_tensor_tensor(
-                out=z[:, c0:c0 + n], in0=gacc[i][:, 0:n], scalar=1.0 / PIX,
+                out=z[:, c0:c0 + n], in0=gacc[i][:, o:o + n], scalar=1.0 / PIX,
                 in1=bb_bc[:, c0:c0 + n], op0=ALU.mult, op1=ALU.add,
             )
             nc.scalar.activation(out=z[:, c0:c0 + n], in_=z[:, c0:c0 + n], func=ACT.Sigmoid)
 
-        def gate_out(i):
-            c0, n = parts[i]
+        def gate_out(i, o, n):
+            c0 = parts[i][0] + o
             nc.vector.scalar_tensor_tensor(
                 out=z[:, c0:c0 + n], in0=z[:, c0:c0 + n], scalar=1.0, in1=ft2[:, c0:c0 + n], op0=ALU.add, op1=ALU.mult
             )
             nc.sync.dma_start(out=out[:, c0:c0 + n], in_=z[:, c0:c0 + n])
 
-        for i in range(len(parts) + 1):
-            if i < len(parts):
-                gate_in(i)
-            if i >= 1:
-                gate_out(i - 1)
+        for i in range(len(pieces)):
+            gate_in(*pieces[i])
+            if 0 < i < 3:
+                gate_out(*pieces[i - 1])
+        for i in range(2, len(pieces)):
+            gate_out(*pieces[i])

@@ -97,17 +97,17 @@ def tile_joint_module_pb_kernel(tc, fv, ft, Wa, ba, Wb, bb, Wfc2, bfc2, out):
         load_fv(1)
         load_wa(1)
         nc.sync.dma_start(out=ft_raw[:], in_=ft)
-        load_wf(0)
         load_fv(2)
+        load_wf(0)
         load_wa(2)
-        load_wf(1)
         load_fv(3)
+        load_wf(1)
         load_wa(3)
-        load_wf(2)
         load_fv(4)
+        load_wf(2)
         load_wa(4)
-        load_wf(3)
         load_fv(5)
+        load_wf(3)
         load_wa(5)
         nc.sync.dma_start(
             out=ba_raw[:].rearrange("p (s e) -> p s e", s=2),
@@ -318,7 +318,6 @@ def tile_joint_module_pb_kernel(tc, fv, ft, Wa, ba, Wb, bb, Wfc2, bfc2, out):
                 for u in range(2):
                     for i in range(4):
                         tf_half(banks[i], pairs[i], u)
-                        pass
                 for i in range(4):
                     tf_out(banks[i], pairs[i], dsts[i], "s")
                 pair_up(1, 0)
@@ -333,10 +332,7 @@ def tile_joint_module_pb_kernel(tc, fv, ft, Wa, ba, Wb, bb, Wfc2, bfc2, out):
                 pair_up(1, 6)
                 wa_quantise(1)
                 ft_unit("s")
-                keep_warm(4)
-                wf_part(0, 0, "s")
-                wf_part(0, 1, "s")
-                keep_warm(4)
+                keep_warm(8)
             else:
                 if g == 1:
                     acc0 = acc_banks()
@@ -347,14 +343,18 @@ def tile_joint_module_pb_kernel(tc, fv, ft, Wa, ba, Wb, bb, Wfc2, bfc2, out):
                     pair_up(g + 1, 3)
                 q_cols(g, 0, 4, early[:])
                 conv1_run(acc0, g - 1, 0)
+                if not more:
+                    for x in range(0, NG, 2):
+                        lasts[x] = new_grp(last_pool, 2)
+                        tf_bank([(x, 8), (x + 1, 8)], lasts[x][:], "s")
+                if g < 5:
+                    wf_part(g - 1, 0, "s")
+                    wf_part(g - 1, 1, "s")
                 if more:
                     wa_part(g + 1, 0, "s")
                     wa_part(g + 1, 1, "s")
                     pair_up(g + 1, 6)
                     wa_quantise(g + 1)
-                if g < 4:
-                    wf_part(g, 0, "s")
-                    wf_part(g, 1, "s")
                 if g < 5:
                     fc_quarter(g - 1, "s")
         conv1_run(acc0, NG - 1, 0)
@@ -364,15 +364,12 @@ def tile_joint_module_pb_kernel(tc, fv, ft, Wa, ba, Wb, bb, Wfc2, bfc2, out):
         q_cols(1, 4, 8, mids[1][:])
         for j in range(4):
             h_out("sv"[j % 2], hp0, acc0[j][:], j, 512)
-        for g in range(0, NG, 2):
-            lasts[g] = new_grp(last_pool, 2)
-            tf_bank([(g, 8), (g + 1, 8)], lasts[g][:], "s")
+        wbgs = [wb_unit(i, "ss") for i in range(2)]
         acc1 = acc_banks()
         for g in range(2, NG):
             q_cols(g, 4, 8, mids[g][:])
         for g in range(3):
             conv1_run(acc1, g, 4)
-        wbgs = [wb_unit(i, "ss") for i in range(2)]
         for g in range(3, NG):
             conv1_run(acc1, g, 4)
         for g in range(0, NG, 2):

from contextlib import ExitStack

import concourse.mybir as mybir
from concourse.masks import make_identity

F32 = mybir.dt.float32
BF16 = mybir.dt.bfloat16
U32 = mybir.dt.uint32
U8 = mybir.dt.uint8
FP8X4 = mybir.dt.float8_e4m3fn_x4
ACT = mybir.ActivationFunctionType
ALU = mybir.AluOpType

P = 128
B, C, PIX = 128, 1024, 9
C3, CH = 3 * C, C // 2
NG = C3 // 512
COLS = PIX * B
FLOPS = 2 * (CH * C3 * COLS + C * CH * COLS + B * C * C)


def tile_joint_module_pb_kernel(tc, fv, ft, Wa, ba, Wb, bb, Wfc2, bfc2, out):
    nc = tc.nc
    with ExitStack() as ctx:
        const = ctx.enter_context(tc.tile_pool(name="const", bufs=1))
        keep = ctx.enter_context(tc.tile_pool(name="keep", bufs=1))
        fvraw_pool = ctx.enter_context(tc.tile_pool(name="fvraw", bufs=4))
        fvw_pool = ctx.enter_context(tc.tile_pool(name="fvw", bufs=2))
        fvl_pool = ctx.enter_context(tc.tile_pool(name="fvl", bufs=NG))
        wraw_pool = ctx.enter_context(tc.tile_pool(name="wraw", bufs=5))
        grp_pool = ctx.enter_context(tc.tile_pool(name="grp", bufs=4))
        mid_pool = ctx.enter_context(tc.tile_pool(name="mid", bufs=NG))
        last_pool = ctx.enter_context(tc.tile_pool(name="last", bufs=NG // 2))
        wag_pool = ctx.enter_context(tc.tile_pool(name="wag", bufs=3))
        psum = ctx.enter_context(tc.psum_pool(name="ps", bufs=1))
        ctx.enter_context(tc.manual_schedule())

        ident = const.tile([P, P], F32, name="ident")
        make_identity(nc, ident[:])
        ba_raw = const.tile([P, 4], BF16, name="ba_raw")
        ba_f = const.tile([P, 4], F32, name="ba_f")
        warm_in = const.tile([P, 1], F32, name="warm_in")
        warm_out = const.tile([P, 1], F32, name="warm_out")
        nc.vector.memset(warm_in[:], 0.0)
        nc.scalar.activation(out=warm_out[:], in_=warm_in[:], func=ACT.Sigmoid)

        fvc = keep.tile([P, NG, 1024], U32, name="fvc", align_bytes=256)
        fvs = keep.tile([P, NG, 1024], U8, name="fvs", align_bytes=256)
        fv8c = keep.tile([P, NG, P], U32, name="fv8c", align_bytes=256)
        fv8s = keep.tile([P, NG, P], U8, name="fv8s", align_bytes=256)
        wac = keep.tile([P, 2, NG, 256], U32, name="wac", align_bytes=256)
        was = keep.tile([P, 2, NG, 256], U8, name="was", align_bytes=256)
        wbc = keep.tile([P, C], U32, name="wbc", align_bytes=256)
        wbs = keep.tile([P, C], U8, name="wbs", align_bytes=256)
        wfT = keep.tile([P, 4, C], F32, name="wfT")
        ftT = keep.tile([P, 4, 2, P], BF16, name="ftT")
        ft2 = keep.tile([P, C], F32, name="ft2")
        hc = keep.tile([P, COLS], U32, name="hc", align_bytes=256)
        hs = keep.tile([P, COLS], U8, name="hs", align_bytes=256)
        z = keep.tile([P, C], F32, name="z")
        ft_raw = const.tile([P, C], BF16, name="ft_raw")
        bfc_bc = const.tile([P, C], BF16, name="bfc_bc")
        bb_bc = const.tile([P, C], BF16, name="bb_bc")

        fv_flat = fv.rearrange("b c h w -> b (c h w)")
        wa_view = Wa.rearrange("(s p e) c -> s p e c", s=2, e=2)
        wf_view = Wfc2.rearrange("(t p) c -> p t c", p=P)
        wb_view = Wb.rearrange("(t p) m -> p t m", p=P)
        fv_raw = {}
        wa_raw = {}
        wf_raw = {}
        wb_raw = {}

        def load_fv(g, parts=1):
            fv_raw[g] = fvraw_pool.tile([P, 4608], BF16, name="fvr", tag="fvr")
            n = 4608 // parts
            for i in range(parts):
                nc.sync.dma_start(
                    out=fv_raw[g][:, i * n:(i + 1) * n], in_=fv_flat[:, g * 4608 + i * n:g * 4608 + (i + 1) * n]
                )

        def load_wa(i):
            sm, gp = i % 2, i // 2
            wa_raw[i] = wraw_pool.tile([P, 2, 1024], BF16, name="war", tag="wr")
            nc.sync.dma_start(out=wa_raw[i][:], in_=wa_view[sm][:, :, gp * 1024:(gp + 1) * 1024])

        def load_wf(i):
            wf_raw[i] = wraw_pool.tile([P, 2, 1024], BF16, name="wfr", tag="wr")
            nc.sync.dma_start(out=wf_raw[i][:], in_=wf_view[:, 2 * i:2 * i + 2, :])

        def load_wb(i):
            wb_raw[i] = wraw_pool.tile([P, 4, 512], BF16, name="wbr", tag="wr")
            nc.sync.dma_start(out=wb_raw[i][:], in_=wb_view[:, 4 * i:4 * i + 4, :])

        load_fv(0, parts=4)
        load_wa(0)
        load_fv(1)
        load_wa(1)
        nc.sync.dma_start(out=ft_raw[:], in_=ft)
        load_fv(2)
        load_wf(0)
        load_wa(2)
        load_fv(3)
        load_wf(1)
        load_wa(3)
        load_fv(4)
        load_wf(2)
        load_wa(4)
        load_fv(5)
        load_wf(3)
        load_wa(5)
        nc.sync.dma_start(
            out=ba_raw[:].rearrange("p (s e) -> p s e", s=2),
            in_=ba.rearrange("(s p e) -> p s e", s=2, e=2),
        )
        load_wb(0)
        load_wb(1)
        nc.sync.dma_start(out=bfc_bc[:], in_=bfc2.partition_broadcast(P))
        nc.sync.dma_start(out=bb_bc[:], in_=bb.partition_broadcast(P))

        used = []

        def tbank():
            tag = "tr%d" % (len(used) % 4)
            used.append(tag)
            return psum.tile([P, 512], F32, name=tag, tag=tag)

        def copy(eng, dst, src):
            if eng == "s":
                nc.scalar.copy(out=dst, in_=src)
            else:
                nc.vector.tensor_copy(out=dst, in_=src)

        fvw = {}

        def pair_up(g, x0, q0=0, q1=128, eng="v"):
            if (g, x0) not in fvw:
                fvw[g, x0] = (fvl_pool if x0 == 6 else fvw_pool).tile([P, 3, 128, 4], BF16, name="fvw", tag="fvw%d" % x0)
            rv = fv_raw[g][:].rearrange("p (q j x) -> p q j x", j=4, x=PIX)
            wv = fvw[g, x0][:].rearrange("p x q j -> p q j x")
            copy(eng, wv[:, q0:q1], rv[:, q0:q1, :, x0:x0 + 3])

        def keep_warm(n):
            pb = psum.tile([P, 512], F32, name="warm", tag="acc3")
            iv = ident[:].bitcast(BF16)
            for i in range(n):
                nc.tensor.matmul(out=pb[:, 0:256], lhsT=iv[:, 0:P], rhs=iv, start=True, stop=True)

        def tf_half(pb, places, u):
            for i, (g, x) in enumerate(places):
                ww = fvw[g, x - x % 3][:, x % 3].rearrange("p q j -> p (q j)").bitcast(F32)
                nc.tensor.transpose(pb[:, (2 * i + u) * P:(2 * i + u + 1) * P], ww[:, u * P:(u + 1) * P], ident[:])

        def tf_bank(places, dst, eng):
            pb = tbank()
            for u in range(2):
                tf_half(pb, places, u)
            tf_out(pb, places, dst, eng)

        def tf_out(pb, places, dst, eng):
            n = len(places)
            copy(
                eng,
                dst.rearrange("p x b t -> p (x b t)").bitcast(F32).rearrange("p (x b u) -> p x b u", x=n, u=2),
                pb[:, 0:2 * n * P].rearrange("p (x u b) -> p x b u", x=n, u=2),
            )

        def new_grp(pool, n):
            return pool.tile([P, n, P, 4], BF16, name="grp%d" % n, tag="grp", align_bytes=64)

        def fv_quantise(codes, scales, grp):
            nc.vector.quantize_mx(
                out=codes.bitcast(FP8X4), scales=scales, in_=grp.rearrange("p x b t -> p (x b t)")
            )

        def q_cols(g, x0, x1, grp):
            c = slice(x0 * P, x1 * P)
            fv_quantise(fvc[:, g, c], fvs[:, g, c], grp)

        def conv1_pass(acc, j, g, codes, scales):
            sm, em = divmod(j, 2)
            nc.tensor.matmul_mx(
                out=acc,
                lhsT=wac[:, sm, g, em * P:(em + 1) * P].bitcast(FP8X4),
                lhsT_scale=was[:, sm, g, em * P:(em + 1) * P],
                rhs=codes.bitcast(FP8X4),
                rhs_scale=scales,
                start=g == 0,
                stop=g == NG - 1,
            )

        def conv1_run(accs, g, x0):
            c = slice(x0 * P, (x0 + 4) * P)
            for j in range(4):
                conv1_pass(accs[j][:], j, g, fvc[:, g, c], fvs[:, g, c])

        wags = {}

        def wa_part(i, g2, eng):
            ww = wa_raw[i][:].bitcast(F32)
            if g2 == 0:
                wags[i] = wag_pool.tile([P, 2, 2, P, 2], F32, name="wag", tag="wag", align_bytes=64)
            pb = tbank()
            for em in range(2):
                for s in range(2):
                    slot = em * 2 + s
                    c0 = 256 * g2 + P * s
                    nc.tensor.transpose(pb[:, slot * P:(slot + 1) * P], ww[:, em, c0:c0 + P], ident[:])
            copy(eng, wags[i][:, g2], pb[:].rearrange("p (e s q) -> p e q s", e=2, s=2))

        def wa_quantise(i):
            sm, gp = i % 2, i // 2
            nc.vector.quantize_mx(
                out=wac[:, sm, 2 * gp:2 * gp + 2, :].rearrange("p g w -> p (g w)").bitcast(FP8X4),
                scales=was[:, sm, 2 * gp:2 * gp + 2, :].rearrange("p g w -> p (g w)"),
                in_=wags[i][:].rearrange("p g e q s -> p (g e q s)").bitcast(BF16),
            )

        wf_e = wfT[:].bitcast(BF16).rearrange("p k (o e) -> p k o e", e=2)

        def ft_unit(eng):
            pb = tbank()
            fw = ft_raw[:].bitcast(F32)
            for k in range(4):
                nc.tensor.transpose(pb[:, k * P:(k + 1) * P], fw[:, k * P:(k + 1) * P], ident[:])
            copy(eng, ftT[:], pb[:].bitcast(BF16).rearrange("p (k b e) -> p k e b", k=4, e=2))

        def wf_part(i, h, eng):
            ww = wf_raw[i][:].bitcast(F32)
            pb = tbank()
            for kl in range(2):
                for tl in range(2):
                    slot = kl * 2 + tl
                    k = 2 * h + kl
                    nc.tensor.transpose(pb[:, slot * P:(slot + 1) * P], ww[:, tl, k * P:(k + 1) * P], ident[:])
            copy(eng, wfT[:, 2 * h:2 * h + 2, i * 256:(i + 1) * 256], pb[:].rearrange("p (k o) -> p k o", k=2))

        def fc_quarter(i, eng):
            acc = tbank()
            cols = slice(i * 256, (i + 1) * 256)
            for idx in range(8):
                k, e = divmod(idx, 2)
                nc.tensor.matmul(
                    out=acc[:, 0:256], lhsT=ftT[:, k, e], rhs=wf_e[:, k, cols, e], start=idx == 0, stop=idx == 7
                )
            copy(eng, ft2[:, cols], acc[:, 0:256])

        def wb_unit(i, engs):
            ww = wb_raw[i][:].bitcast(F32)
            wbg = wag_pool.tile([P, 512, 2], F32, name="wbg", tag="wag", align_bytes=64)
            for h in range(2):
                pb = tbank()
                for tl in range(2):
                    for sm in range(2):
                        slot = tl * 2 + sm
                        nc.tensor.transpose(
                            pb[:, slot * P:(slot + 1) * P], ww[:, 2 * h + tl, sm * P:(sm + 1) * P], ident[:]
                        )
                copy(
                    engs[h],
                    wbg[:, 256 * h:256 * (h + 1), :].rearrange("p (t o) s -> p t o s", t=2),
                    pb[:].rearrange("p (t s o) -> p t o s", t=2, s=2),
                )
            return wbg

        def wb_quantise(i, wbg):
            nc.vector.quantize_mx(
                out=wbc[:, i * 512:(i + 1) * 512].bitcast(FP8X4),
                scales=wbs[:, i * 512:(i + 1) * 512],
                in_=wbg[:].rearrange("p o s -> p (o s)").bitcast(BF16),
            )

        def h_out(eng, hp, bank, j, n):
            if eng == "s":
                nc.scalar.activation(out=hp[:, j, 0:n], in_=bank, func=ACT.Relu, bias=ba_f[:, j:j + 1], scale=1.0)
            else:
                nc.vector.tensor_scalar(
                    out=hp[:, j, 0:n], in0=bank, scalar1=ba_f[:, j:j + 1], scalar2=0.0, op0=ALU.add, op1=ALU.max
                )

        def h_regroup(hp, hg, c0, n):
            nc.vector.tensor_copy(
                out=hg[:, c0:c0 + n, :].rearrange("p (c i) t -> p c t i", i=4),
                in_=hp[:, :, c0:c0 + n].rearrange("p t (c i) -> p c t i", i=4),
            )

        def h_quantise(hg, h0, c0, n):
            nc.vector.quantize_mx(
                out=hc[:, h0 + c0:h0 + c0 + n].bitcast(FP8X4),
                scales=hs[:, h0 + c0:h0 + c0 + n],
                in_=hg[:, c0:c0 + n, :].rearrange("p c t -> p (c t)"),
            )

        def acc_banks():
            return [psum.tile([P, 512], F32, name="acc%d" % j, tag="acc%d" % j) for j in range(4)]

        mids = {}
        lasts = {}

        def q_last(g):
            fv_quantise(
                fv8c[:, g:g + 2].rearrange("p g w -> p (g w)"),
                fv8s[:, g:g + 2].rearrange("p g w -> p (g w)"),
                lasts[g][:],
            )

        for q0, q1 in ((0, 32), (32, 64), (64, 128)):
            for x0 in (0, 3, 6):
                pair_up(0, x0, q0, q1)
        for g in range(NG):
            more = g + 1 < NG
            early = new_grp(grp_pool, 4)
            mids[g] = new_grp(mid_pool, 4)
            pairs = [[(g, x), (g, x + 1)] for x in range(0, 8, 2)]
            dsts = [early[:, 0:2], early[:, 2:4], mids[g][:, 0:2], mids[g][:, 2:4]]
            if g == 0:
                banks = [tbank() for i in range(4)]
                for u in range(2):
                    for i in range(4):
                        tf_half(banks[i], pairs[i], u)
                for i in range(4):
                    tf_out(banks[i], pairs[i], dsts[i], "s")
                pair_up(1, 0)
                pair_up(1, 3)
                q_cols(0, 0, 4, early[:])
                wa_part(0, 0, "s")
                wa_part(0, 1, "s")
                keep_warm(8)
                wa_quantise(0)
                wa_part(1, 0, "s")
                wa_part(1, 1, "s")
                pair_up(1, 6)
                wa_quantise(1)
                ft_unit("s")
                keep_warm(8)
            else:
                if g == 1:
                    acc0 = acc_banks()
                for i in range(4):
                    tf_bank(pairs[i], dsts[i], "s")
                if more:
                    pair_up(g + 1, 0)
                    pair_up(g + 1, 3)
                q_cols(g, 0, 4, early[:])
                conv1_run(acc0, g - 1, 0)
                if not more:
                    for x in range(0, NG, 2):
                        lasts[x] = new_grp(last_pool, 2)
                        tf_bank([(x, 8), (x + 1, 8)], lasts[x][:], "s")
                if g < 5:
                    wf_part(g - 1, 0, "s")
                    wf_part(g - 1, 1, "s")
                if more:
                    wa_part(g + 1, 0, "s")
                    wa_part(g + 1, 1, "s")
                    pair_up(g + 1, 6)
                    wa_quantise(g + 1)
                if g < 5:
                    fc_quarter(g - 1, "s")
        conv1_run(acc0, NG - 1, 0)
        nc.vector.tensor_copy(out=ba_f[:], in_=ba_raw[:])
        hp0 = grp_pool.tile([P, 4, 512], BF16, name="hp0", tag="grp", align_bytes=64)
        q_cols(0, 4, 8, mids[0][:])
        q_cols(1, 4, 8, mids[1][:])
        for j in range(4):
            h_out("sv"[j % 2], hp0, acc0[j][:], j, 512)
        wbgs = [wb_unit(i, "ss") for i in range(2)]
        acc1 = acc_banks()
        for g in range(2, NG):
            q_cols(g, 4, 8, mids[g][:])
        for g in range(3):
            conv1_run(acc1, g, 4)
        for g in range(3, NG):
            conv1_run(acc1, g, 4)
        for g in range(0, NG, 2):
            q_last(g)
        hg0 = grp_pool.tile([P, 512, 4], BF16, name="hg0", tag="grp", align_bytes=64)
        h_regroup(hp0, hg0, 0, 256)
        h_regroup(hp0, hg0, 256, 256)
        h_quantise(hg0, 0, 0, 512)
        for i in range(2):
            wb_quantise(i, wbgs[i])

        hp1 = grp_pool.tile([P, 4, 512], BF16, name="hp1", tag="grp", align_bytes=64)
        hg1 = grp_pool.tile([P, 512, 4], BF16, name="hg1", tag="grp", align_bytes=64)
        for j in range(4):
            h_out("sv"[j % 2], hp1, acc1[j][:], j, 512)
        acc2 = psum.tile([P, 512], F32, name="acc2", tag="tr0")
        for j in range(4):
            for g in range(NG):
                conv1_pass(acc2[:, j * P:(j + 1) * P], j, g, fv8c[:, g], fv8s[:, g])
        h_regroup(hp1, hg1, 0, 256)
        h_regroup(hp1, hg1, 256, 256)
        h_quantise(hg1, 512, 0, 256)
        h_quantise(hg1, 512, 256, 256)
        hp2 = grp_pool.tile([P, 4, P], BF16, name="hp2", tag="grp", align_bytes=64)
        hg2 = grp_pool.tile([P, P, 4], BF16, name="hg2", tag="grp", align_bytes=64)
        for j in range(4):
            h_out("s", hp2, acc2[:, j * P:(j + 1) * P], j, P)
        h_regroup(hp2, hg2, 0, P)
        h_quantise(hg2, 1024, 0, P)
        nc.vector.tensor_tensor(out=ft2[:], in0=ft2[:], in1=bfc_bc[:], op=ALU.add)

        parts = ((0, 256), (256, 256), (512, 256), (768, 256))
        gacc = [psum.tile([P, 512], F32, name="g%d" % i, tag="tr%d" % (i + 1) if i < 3 else "acc%d" % (i - 3)) for i in range(len(parts))]

        def conv2_pass(i, x):
            c0, n = parts[i]
            nc.tensor.matmul_mx(
                out=gacc[i][:, 0:n],
                lhsT=hc[:, x * P:(x + 1) * P].bitcast(FP8X4),
                lhsT_scale=hs[:, x * P:(x + 1) * P],
                rhs=wbc[:, c0:c0 + n].bitcast(FP8X4),
                rhs_scale=wbs[:, c0:c0 + n],
                start=x == 0,
                stop=x == PIX - 1,
            )

        for i in range(len(parts)):
            for x in range(4):
                conv2_pass(i, x)
        for i in range(len(parts)):
            for x in range(4, PIX):
                conv2_pass(i, x)

        pieces = [(i, 0, 256) for i in range(3)] + [(3, 0, P), (3, P, P)]

        def gate_in(i, o, n):
            c0 = parts[i][0] + o
            nc.vector.scalar_tensor_tensor(
                out=z[:, c0:c0 + n], in0=gacc[i][:, o:o + n], scalar=1.0 / PIX,
                in1=bb_bc[:, c0:c0 + n], op0=ALU.mult, op1=ALU.add,
            )
            nc.scalar.activation(out=z[:, c0:c0 + n], in_=z[:, c0:c0 + n], func=ACT.Sigmoid)

        def gate_out(i, o, n):
            c0 = parts[i][0] + o
            nc.vector.scalar_tensor_tensor(
                out=z[:, c0:c0 + n], in0=z[:, c0:c0 + n], scalar=1.0, in1=ft2[:, c0:c0 + n], op0=ALU.add, op1=ALU.mult
            )
            nc.sync.dma_start(out=out[:, c0:c0 + n], in_=z[:, c0:c0 + n])

        for i in range(len(pieces)):
            gate_in(*pieces[i])
            if 0 < i < 3:
                gate_out(*pieces[i - 1])
        for i in range(2, len(pieces)):
            gate_out(*pieces[i])
